import numpy as np
import ml_dtypes


def mxq(x, axis, fmt="e4m3"):
    dtype, down = {"e4m3": (ml_dtypes.float8_e4m3fn, 7), "e5m2": (ml_dtypes.float8_e5m2, 14)}[fmt]
    v = np.moveaxis(np.asarray(x, np.float32).astype(ml_dtypes.bfloat16).astype(np.float64), axis, -1)
    blocks = v.reshape(v.shape[:-1] + (-1, 32))
    amax = np.abs(blocks).max(-1, keepdims=True)
    byte = np.maximum(np.where(amax > 0, np.frexp(amax)[1] - 1 + 127, 0) - down, 1)
    scale = np.exp2(byte - 127.0)
    codes = (blocks / scale).astype(np.float32).astype(dtype).astype(np.float64)
    return np.moveaxis((codes * scale).reshape(v.shape), -1, axis)


WIDE = False


def mx_kscale(k):
    if not WIDE:
        return np.ones(k)
    levels = np.array([10, -10, 5, -5, 0])
    if k % 512:
        return np.exp2(np.random.permutation(np.resize(levels, k // 32))).repeat(32)
    a = np.empty((k // 512, 16))
    for p in range(k // 512):
        a[p, :8] = np.random.permutation(np.resize(levels, 8))
        for g in range(8):
            far = levels[np.abs(levels - a[p, g]) >= 10]
            a[p, g + 8] = far[np.random.randint(len(far))]
    return np.exp2(a.ravel()).repeat(32)


BF16 = ml_dtypes.bfloat16


def bf(x):
    return np.asarray(x, np.float32).astype(BF16)


def f64(x):
    return np.asarray(x).astype(np.float64)


B, T, C, H, NOPE, ROPE, VD, LORA = 1, 512, 2048, 16, 128, 128, 128, 512
EPS = 1e-6
HALF = ROPE // 2
KVW = H * (NOPE + VD)


def make_freq_cis():
    inv = 1.0 / (10000.0 ** (np.arange(0, ROPE, 2) / ROPE))
    ang = np.outer(np.arange(T), inv)
    return np.stack([np.cos(ang), np.sin(ang)], -1)


def apply_rope(v, fc):
    vr = v.reshape(B, T, HALF, 2)
    real = vr[..., 0] * fc[..., 0] - vr[..., 1] * fc[..., 1]
    imag = vr[..., 1] * fc[..., 0] + vr[..., 0] * fc[..., 1]
    return np.stack([real, imag], -1).reshape(B, T, ROPE)


def draw0():
    s, t = mx_kscale(C), mx_kscale(LORA)
    return {"x": bf(np.random.standard_normal((B, T, C)) * s),
            "freq_cis": bf(make_freq_cis()),
            "Wckv": bf(np.random.standard_normal((C, LORA + ROPE)) / np.sqrt(C) / s[:, None]),
            "kv_norm_w": bf((1.0 + 0.1 * np.random.standard_normal(LORA)) * t),
            "Wdkv": bf(np.random.standard_normal((LORA, KVW)) / np.sqrt(LORA) / t[:, None])}


def core(x, freq_cis, Wckv, kv_norm_w, Wdkv):
    ckv = mxq(f64(x), 2, "e4m3") @ mxq(f64(Wckv), 0, "e4m3")
    kv_lat, k_rope = ckv[..., :LORA], ckv[..., LORA:]
    k_rope = apply_rope(k_rope, f64(freq_cis))
    lat_n = kv_lat / np.sqrt(np.mean(kv_lat * kv_lat, -1, keepdims=True) + EPS) * f64(kv_norm_w)
    kv = mxq(lat_n, 2, "e4m3") @ mxq(f64(Wdkv), 0, "e4m3")
    return kv, k_rope


def e4m3fn_bytes(y):
    return np.clip(np.asarray(y, np.float64), -448.0, 448.0).astype(np.float32).astype(ml_dtypes.float8_e4m3fn).view(np.uint8)


def e4m3fn_values(b):
    return np.asarray(b, np.uint8).view(ml_dtypes.float8_e4m3fn).astype(np.float64)


def setup_inputs():
    d = draw0()
    x0 = np.asarray(d['Wdkv']).astype(np.float64)
    s = (np.max(np.abs(x0), axis=(1,), keepdims=True) / 448.0).astype(np.float32)
    out = {}
    for k, v in d.items():
        if k == 'Wdkv':
            out['Wdkv_bytes'] = e4m3fn_bytes(x0 / s.astype(np.float64))
            out['Wdkv_scale'] = s
        else:
            out[k] = v
    return out


def reference(x, freq_cis, Wckv, kv_norm_w, Wdkv_bytes, Wdkv_scale):
    return core(x, freq_cis, Wckv, kv_norm_w, e4m3fn_values(Wdkv_bytes) * Wdkv_scale.astype(np.float64))

@@ -1,0 +1,353 @@
+from contextlib import ExitStack
+
+import concourse.mybir as mybir
+from concourse.masks import make_identity
+
+T, C, LORA, ROPE, KVW = 512, 2048, 512, 128, 4096
+WIDTH = LORA + ROPE
+FLOPS = 2 * T * C * WIDTH + 2 * T * LORA * KVW
+
+F32 = mybir.dt.float32
+BF16 = mybir.dt.bfloat16
+U32 = mybir.dt.uint32
+U8 = mybir.dt.uint8
+FP8 = mybir.dt.float8_e4m3fn
+FP8X4 = mybir.dt.float8_e4m3fn_x4
+ALU = mybir.AluOpType
+ACT = mybir.ActivationFunctionType
+
+P = 128
+NB = T // P
+NP = C // 512
+CHUNKS = [(512 * c, 512) for c in range(8)]
+NCH = len(CHUNKS)
+BLOADS = [(0, 512), (512, 1536), (2048, 2048)]
+WSPLIT = [352, 416, 64, 448]
+DSPLIT = [320, 448, 416, 480, 512, 416, 512, 512]
+
+
+def tile_multiheadlatentattention_pa_kernel(tc, x, freq_cis, Wckv, kv_norm_w, Wdkv_bytes, Wdkv_scale, out_0, out_1):
+    nc = tc.nc
+    xv = x.flatten_outer_dims().rearrange("(p b) c -> p b c", b=NB)
+    kvv = out_0.flatten_outer_dims().rearrange("(p b) n -> p b n", b=NB)
+    krv = out_1.flatten_outer_dims().rearrange("(p b) f -> p (b f)", b=NB)
+
+    with ExitStack() as ctx:
+        keep = ctx.enter_context(tc.tile_pool(name="keep", bufs=1))
+        work = ctx.enter_context(tc.tile_pool(name="work", bufs=4))
+        outs = ctx.enter_context(tc.tile_pool(name="outs", bufs=8))
+        psum = ctx.enter_context(tc.psum_pool(name="psum", bufs=1))
+        ctx.enter_context(tc.manual_schedule())
+
+        ident = keep.tile([P, P], F32, name="ident")
+        ones = keep.tile([P, P], BF16, name="ones")
+        grow = keep.tile([P, LORA], BF16, name="grow")
+        gain = keep.tile([P, LORA], F32, name="gain")
+        eps = keep.tile([P, 1], F32, name="eps")
+        dummy = keep.tile([P, 1], F32, name="dummy")
+        scale = keep.tile([P, 4], F32, name="scale")
+        fr = keep.tile([P, NB * 64, 2], BF16, name="fr")
+        nsin = keep.tile([P, NB * 64, 1], F32, name="nsin")
+        xraw = [keep.tile([P, C], BF16, name="xraw%d" % b) for b in range(NB)]
+        wraw = [keep.tile([P, 4, WIDTH], BF16, name="wraw%d" % g) for g in range(NP)]
+        wb = [keep.tile([P, 4, n], U8, name="wb%d" % i) for i, (o, n) in enumerate(BLOADS)]
+        xc = [keep.tile([P, NP, P], U32, name="xc%d" % b, align_bytes=64) for b in range(NB)]
+        xs = [keep.tile([P, NP, P], U8, name="xs%d" % b, align_bytes=64) for b in range(NB)]
+        wc = [keep.tile([P, LORA], U32, name="wc%d" % g, align_bytes=64) for g in range(NP)]
+        ws = [keep.tile([P, LORA], U8, name="ws%d" % g, align_bytes=64) for g in range(NP)]
+        wrg = keep.tile([P, NP, ROPE, 4], BF16, name="wrg", align_bytes=64)
+        wrc = keep.tile([P, NP, ROPE], U32, name="wrc", align_bytes=64)
+        wrs = keep.tile([P, NP, ROPE], U8, name="wrs", align_bytes=64)
+        ncod = [keep.tile([P, P], U32, name="ncod%d" % b, align_bytes=64) for b in range(NB)]
+        nsc = [keep.tile([P, P], U8, name="nsc%d" % b, align_bytes=64) for b in range(NB)]
+        dc = [keep.tile([P, CHUNKS[c][1]], U32, name="dc%d" % c, align_bytes=64) for c in range(NCH)]
+        ds = [keep.tile([P, CHUNKS[c][1]], U8, name="ds%d" % c, align_bytes=64) for c in range(NCH)]
+        sumsq = [keep.tile([P, 1], F32, name="sumsq%d" % b) for b in range(NB)]
+        rstd = [keep.tile([P, 1], F32, name="rstd%d" % b) for b in range(NB)]
+
+        wv = Wckv.rearrange("(g p j) n -> g p j n", p=P, j=4)
+        bv = Wdkv_bytes.rearrange("(p j) n -> p j n", j=4)
+
+        def load_x(b):
+            nc.sync.dma_start(out=xraw[b][:], in_=xv[:, b, :])
+
+        def load_w(g):
+            nc.sync.dma_start(out=wraw[g][:], in_=wv[g])
+
+        nc.vector.memset(grow[:].bitcast(U32), 0)
+        def load_b(c):
+            o, n = BLOADS[c]
+            nc.sync.dma_start(out=wb[c][:], in_=bv[:, :, o : o + n])
+
+        nc.sync.dma_start(out=scale[:], in_=Wdkv_scale.rearrange("(p j) o -> p (j o)", j=4))
+        load_b(0)
+        load_b(1)
+        load_x(0)
+        load_w(0)
+        load_w(1)
+        nc.scalar.dma_start(out=grow[0:1, :], in_=kv_norm_w.rearrange("(o n) -> o n", o=1))
+        load_w(2)
+        load_w(3)
+        load_x(1)
+        load_x(2)
+        load_x(3)
+        nc.sync.dma_start(out=fr[:].rearrange("p i e -> p (i e)"), in_=freq_cis.rearrange("(p b) i e -> p (b i e)", b=NB))
+        load_b(2)
+
+        make_identity(nc, ident[:])
+        nc.vector.memset(ones[:], 1.0)
+        nc.vector.memset(eps[:], 1e-6)
+        nc.scalar.activation(dummy[:], eps[:], ACT.Abs_reciprocal_sqrt)
+        nc.gpsimd.tensor_scalar(nsin[:], fr[:, :, 1:2], -1.0, 0.0, ALU.mult, ALU.add)
+
+        def four(t):
+            return t.rearrange("p (c i) t -> p c t i", i=4)
+
+        def by_four(t):
+            return t.rearrange("p t (c i) -> p c t i", i=4)
+
+        wg = {}
+        xg = {}
+        wide = {}
+        dg = {}
+        tp = {}
+        lat = {}
+        ng = {}
+        nb = {}
+        idle = list(range(8))
+
+        def take():
+            i = idle[0]
+            idle.remove(i)
+            return i, psum.tile([P, 512], F32, name="bank%d" % i)
+
+
+        def wg_tile(g):
+            if g not in wg:
+                wg[g] = work.tile([P, LORA, 4], BF16, name="wg", align_bytes=64)
+            return wg[g]
+
+        def w_inter_v(g):
+            nc.vector.tensor_copy(four(wg_tile(g)[:, 0 : WSPLIT[g], :]), by_four(wraw[g][:, :, 0 : WSPLIT[g]]))
+
+        def w_inter_s(g):
+            nc.scalar.copy(four(wg_tile(g)[:, WSPLIT[g] : LORA, :]), by_four(wraw[g][:, :, WSPLIT[g] : LORA]))
+
+        def w_quant(g):
+            nc.vector.quantize_mx(out=wc[g][:].bitcast(FP8X4), scales=ws[g][:], in_=wg[g][:].rearrange("p w j -> p (w j)"))
+
+        def wr_inter(g, eng):
+            copy(eng, four(wrg[:, g, :, :]), by_four(wraw[g][:, :, LORA:WIDTH]))
+
+        def wr_quant():
+            nc.vector.quantize_mx(
+                out=wrc[:].rearrange("p g w -> p (g w)").bitcast(FP8X4),
+                scales=wrs[:].rearrange("p g w -> p (g w)"),
+                in_=wrg[:].rearrange("p g w j -> p (g w j)"),
+            )
+
+        def x_trans(b, h):
+            words = xraw[b][:].bitcast(F32)
+            tp[(b, h)] = take()
+            t = tp[(b, h)][1][:].rearrange("p (a r) -> p a r", a=4)
+            for gg in range(2):
+                for u in range(2):
+                    nc.tensor.transpose(t[:, 2 * gg + u, :], words[:, 256 * (2 * h + gg) + u : 256 * (2 * h + gg + 1) : 2], ident[:])
+
+        def copy(eng, out, in_):
+            if eng == "v":
+                nc.vector.tensor_copy(out, in_)
+            else:
+                nc.scalar.copy(out, in_)
+
+        def x_out(b, h, eng):
+            if b not in xg:
+                xg[b] = work.tile([P, NP, P, 4], BF16, name="xg", align_bytes=64)
+            flat = xg[b][:].rearrange("p g r t -> p (g r t)").bitcast(F32)
+            i, t = tp[(b, h)]
+            copy(
+                eng,
+                flat[:, 512 * h : 512 * (h + 1)].rearrange("p (g r u) -> p g r u", g=2, u=2),
+                t[:].rearrange("p (g u r) -> p g r u", g=2, u=2),
+            )
+            idle.append(i)
+
+        def x_quant(b):
+            nc.vector.quantize_mx(
+                out=xc[b][:].rearrange("p g r -> p (g r)").bitcast(FP8X4),
+                scales=xs[b][:].rearrange("p g r -> p (g r)"),
+                in_=xg[b][:].rearrange("p g r t -> p (g r t)"),
+            )
+
+        def lat_pass(b, g):
+            if g == 0:
+                lat[b] = take()
+            nc.tensor.matmul_mx(
+                out=lat[b][1][:],
+                lhsT=xc[b][:, g, :].bitcast(FP8X4),
+                lhsT_scale=xs[b][:, g, :],
+                rhs=wc[g][:].bitcast(FP8X4),
+                rhs_scale=ws[g][:],
+                start=(g == 0),
+                stop=(g == NP - 1),
+            )
+
+        def kr_passes(b):
+            if b % 2 == 0:
+                tp[("kr", b // 2)] = take()
+            kr = tp[("kr", b // 2)][1][:, 128 * (b % 2) : 128 * (b % 2 + 1)]
+            for g in range(NP):
+                nc.tensor.matmul_mx(
+                    out=kr,
+                    lhsT=xc[b][:, g, :].bitcast(FP8X4),
+                    lhsT_scale=xs[b][:, g, :],
+                    rhs=wrc[:, g, :].bitcast(FP8X4),
+                    rhs_scale=wrs[:, g, :],
+                    start=(g == 0),
+                    stop=(g == NP - 1),
+                )
+
+        def stats(b):
+            sq = work.tile([P, LORA], BF16, name="sq")
+            nc.scalar.activation(sq[:], lat[b][1][:], ACT.Square, accum_out=sumsq[b][:])
+
+        def root(b):
+            nc.scalar.activation(rstd[b][:], sumsq[b][:], ACT.Abs_reciprocal_sqrt, bias=eps[:], scale=1.0 / LORA)
+
+        def norm(b):
+            nb[b] = work.tile([P, LORA], BF16, name="nb")
+            nc.vector.scalar_tensor_tensor(nb[b][:], lat[b][1][:], rstd[b][:], gain[:], ALU.mult, ALU.mult)
+            idle.append(lat[b][0])
+
+        def n_trans(b):
+            tp[(b, 2)] = take()
+            words = nb[b][:].bitcast(F32)
+            for u in range(2):
+                nc.tensor.transpose(tp[(b, 2)][1][:, P * u : P * (u + 1)], words[:, u::2], ident[:])
+
+        def n_out(b, eng):
+            ng[b] = work.tile([P, P, 4], BF16, name="ng", align_bytes=64)
+            i, t = tp[(b, 2)]
+            copy(
+                eng,
+                ng[b][:].rearrange("p r t -> p (r t)").bitcast(F32).rearrange("p (r u) -> p r u", u=2),
+                t[:, 0 : 2 * P].rearrange("p (u r) -> p r u", u=2),
+            )
+            idle.append(i)
+
+        def n_quant(b):
+            nc.vector.quantize_mx(out=ncod[b][:].bitcast(FP8X4), scales=nsc[b][:], in_=ng[b][:].rearrange("p r t -> p (r t)"))
+
+        def bytes_of(c):
+            o, n = CHUNKS[c]
+            for i, (bo, bn) in enumerate(BLOADS):
+                if bo <= o < bo + bn:
+                    return wb[i], o - bo, n
+
+        def widen(c, j, eng):
+            t, o, n = bytes_of(c)
+            if c not in wide:
+                wide[c] = work.tile([P, 4, n], BF16, name="wide", bufs=5)
+            w = wide[c][:, j, :]
+            b = t[:, j, o : o + n].bitcast(FP8)
+            if eng == "v":
+                nc.vector.tensor_scalar(w, b, scale[:, j : j + 1], None, ALU.mult)
+            else:
+                nc.scalar.activation(w, b, ACT.Copy, scale=scale[:, j : j + 1])
+
+        def dg_tile(c):
+            if c not in dg:
+                dg[c] = work.tile([P, CHUNKS[c][1], 4], BF16, name="dg", align_bytes=64)
+            return dg[c]
+
+        def d_inter_v(c):
+            nc.vector.tensor_copy(four(dg_tile(c)[:, 0 : DSPLIT[c], :]), by_four(wide[c][:, :, 0 : DSPLIT[c]]))
+
+        def d_inter_s(c):
+            n = CHUNKS[c][1]
+            nc.scalar.copy(four(dg_tile(c)[:, DSPLIT[c] : n, :]), by_four(wide[c][:, :, DSPLIT[c] : n]))
+
+        def d_quant(c):
+            nc.vector.quantize_mx(out=dc[c][:].bitcast(FP8X4), scales=ds[c][:], in_=dg[c][:].rearrange("p w j -> p (w j)"))
+
+        def kv_mm(b, c):
+            n = CHUNKS[c][1]
+            tp[("kv", b, c)] = take()
+            nc.tensor.matmul_mx(
+                out=tp[("kv", b, c)][1][:, 0:n],
+                lhsT=ncod[b][:].bitcast(FP8X4),
+                lhsT_scale=nsc[b][:],
+                rhs=dc[c][:].bitcast(FP8X4),
+                rhs_scale=ds[c][:],
+                start=True,
+                stop=True,
+            )
+
+        def kv_out(b, c, eng):
+            i, t = tp[("kv", b, c)]
+            key = ("o", b, c // 2)
+            first = key not in tp
+            if first:
+                tp[key] = outs.tile([P, 1024], F32, name="o")
+            copy(eng, tp[key][:, 512 * (c % 2) : 512 * (c % 2 + 1)], t[:])
+            idle.append(i)
+            if not first:
+                m = c // 2
+                nc.sync.dma_start(out=kvv[:, b, 1024 * m : 1024 * (m + 1)], in_=tp[key][:])
+
+        def rope(h):
+            pairs = slice(128 * h, 128 * (h + 1))
+            cos, sin = fr[:, pairs, 0:1], fr[:, pairs, 1:2]
+            i, t = tp[("kr", h)]
+            k2 = t[:, 0:256].rearrange("p (i e) -> p i e", e=2)
+            t1 = work.tile([P, 128, 2], F32, name="t1", bufs=2)
+            t2 = work.tile([P, 2, 128], F32, name="t2", bufs=2)
+            ro = work.tile([P, 128, 2], F32, name="ro", bufs=2)
+            nc.vector.tensor_tensor(t1[:], k2, cos.to_broadcast([P, 128, 2]), ALU.mult)
+            nc.vector.tensor_tensor(t2[:, 0, :].unsqueeze(2), k2[:, :, 1:2], nsin[:, pairs, :], ALU.mult)
+            nc.vector.tensor_tensor(t2[:, 1, :].unsqueeze(2), k2[:, :, 0:1], sin, ALU.mult)
+            idle.append(i)
+            nc.vector.tensor_tensor(ro[:], t1[:], t2[:].rearrange("p e i -> p i e"), ALU.add)
+            nc.sync.dma_start(out=krv[:, 256 * h : 256 * (h + 1)], in_=ro[:].rearrange("p i e -> p (i e)"))
+
+        def gains():
+            tp["gain"] = take()
+            nc.tensor.matmul(tp["gain"][1][:], lhsT=ones[:], rhs=grow[:], start=True, stop=True)
+
+        def gain_out(eng):
+            i, t = tp["gain"]
+            copy(eng, gain[:], t[:])
+            idle.append(i)
+
+        gains(); widen(0, 2, "s"); widen(0, 3, "v"); widen(0, 1, "v"); widen(0, 0, "v"); d_inter_s(0)
+        d_inter_v(0); widen(1, 2, "v"); widen(1, 0, "v"); widen(2, 0, "v"); widen(1, 1, "v"); d_quant(0)
+        widen(1, 3, "s"); d_inter_v(1); widen(3, 3, "s"); widen(3, 0, "s"); w_inter_v(0); widen(2, 3, "v")
+        w_inter_v(1); d_inter_s(1); widen(2, 2, "s"); x_trans(0, 0); x_out(0, 0, "s"); w_inter_s(0)
+        x_trans(0, 1); x_out(0, 1, "s"); x_quant(0); w_inter_v(2); w_quant(0); lat_pass(0, 0); widen(2, 1, "s")
+        w_inter_s(1); w_quant(1); lat_pass(0, 1); w_inter_v(3); w_inter_s(2); w_quant(2); widen(3, 2, "s")
+        w_inter_s(3); w_quant(3); widen(3, 1, "s"); d_inter_v(2); x_trans(1, 0); x_out(1, 0, "s"); x_trans(1, 1)
+        x_out(1, 1, "s"); x_quant(1); d_inter_v(3); lat_pass(0, 2); lat_pass(0, 3); stats(0); gain_out("s")
+        x_trans(2, 0); x_trans(2, 1); x_out(2, 1, "s"); x_trans(3, 1); root(0); norm(0); x_out(2, 0, "s")
+        x_quant(2); lat_pass(1, 0); lat_pass(1, 1); lat_pass(1, 2); d_inter_s(2); x_out(3, 1, "s"); d_quant(1)
+        d_quant(2); x_trans(3, 0); x_out(3, 0, "s"); n_trans(0); n_out(0, "s"); lat_pass(1, 3); stats(1)
+        d_inter_s(3); root(1); lat_pass(2, 0); lat_pass(2, 1); lat_pass(2, 2); lat_pass(2, 3); stats(2)
+        n_quant(0); kv_mm(0, 1); kv_out(0, 1, "s"); kv_mm(0, 0); kv_out(0, 0, "s"); root(2); x_quant(3)
+        lat_pass(3, 0); lat_pass(3, 1); lat_pass(3, 2); lat_pass(3, 3); stats(3); widen(6, 2, "v"); norm(1)
+        n_trans(1); n_out(1, "s"); kv_mm(0, 2); kv_out(0, 2, "s"); root(3); widen(7, 2, "v"); d_quant(3)
+        kv_mm(0, 3); kv_out(0, 3, "s"); widen(6, 3, "v"); norm(2); n_trans(2); widen(4, 1, "v"); n_quant(1)
+        widen(7, 3, "v"); widen(6, 1, "v"); norm(3); widen(7, 0, "v"); n_out(2, "s"); n_quant(2)
+        widen(7, 1, "v"); widen(6, 0, "v"); kv_mm(1, 3); kv_out(1, 3, "s"); kv_mm(1, 1); kv_mm(1, 2)
+        kv_out(1, 2, "s"); n_trans(3); n_out(3, "v"); widen(4, 3, "v"); kv_out(1, 1, "s"); kv_mm(1, 0)
+        kv_out(1, 0, "s"); kv_mm(2, 0); kv_mm(2, 1); kv_out(2, 0, "s"); kv_mm(2, 2); kv_out(2, 1, "s")
+        n_quant(3); kv_mm(3, 1); kv_mm(2, 3); kv_out(2, 3, "s"); kv_out(2, 2, "s"); d_inter_v(7)
+        widen(5, 2, "v"); kv_mm(3, 0); kv_mm(3, 2); kv_out(3, 0, "s"); kv_out(3, 1, "s"); kv_mm(3, 3)
+        kv_out(3, 3, "s"); d_quant(7); kv_mm(2, 7); kv_mm(0, 7); kv_out(3, 2, "s"); kv_mm(3, 7)
+        kv_out(3, 7, "s"); d_inter_v(6); widen(5, 0, "v"); d_quant(6); widen(4, 2, "v"); kv_mm(3, 6)
+        kv_out(3, 6, "s"); widen(4, 0, "v"); kv_out(2, 7, "s"); kv_mm(1, 6); kv_mm(2, 6); kv_out(2, 6, "s")
+        kv_mm(0, 6); kv_out(0, 6, "s"); kv_out(0, 7, "s"); widen(5, 3, "v"); d_inter_v(4); widen(5, 1, "v")
+        d_inter_s(5); kv_out(1, 6, "s"); kv_mm(1, 7); kv_out(1, 7, "s"); d_quant(4); kv_mm(1, 4); kv_mm(2, 4)
+        kv_out(1, 4, "s"); kv_mm(3, 4); d_inter_v(5); d_quant(5); kv_mm(1, 5); kv_out(1, 5, "s")
+        wr_inter(0, "v"); wr_inter(1, "v"); wr_inter(2, "v"); wr_inter(3, "v"); kv_out(3, 4, "v"); wr_quant()
+        kv_mm(0, 5); kv_out(0, 5, "v"); kv_out(2, 4, "v"); kv_mm(3, 5); kv_mm(2, 5); kv_out(3, 5, "s")
+        kv_mm(0, 4); kv_out(0, 4, "s"); kr_passes(0); kr_passes(1); rope(0); kv_out(2, 5, "s"); kr_passes(2)
+        kr_passes(3); rope(1)

@@ -21,9 +21,8 @@ NB = T // P
 NP = C // 512
 CHUNKS = [(512 * c, 512) for c in range(8)]
 NCH = len(CHUNKS)
-BLOADS = [(0, 512), (512, 1536), (2048, 2048)]
-WSPLIT = [352, 416, 64, 448]
-DSPLIT = [320, 448, 416, 480, 512, 416, 512, 512]
+BLOADS = [(0, 1024), (1024, 1024), (2048, 2048)]
+WSPLIT = 320
 
 
 def tile_multiheadlatentattention_pa_kernel(tc, x, freq_cis, Wckv, kv_norm_w, Wdkv_bytes, Wdkv_scale, out_0, out_1):
@@ -35,19 +34,22 @@ def tile_multiheadlatentattention_pa_kernel(tc, x, freq_cis, Wckv, kv_norm_w, Wd
     with ExitStack() as ctx:
         keep = ctx.enter_context(tc.tile_pool(name="keep", bufs=1))
         work = ctx.enter_context(tc.tile_pool(name="work", bufs=4))
-        outs = ctx.enter_context(tc.tile_pool(name="outs", bufs=8))
+        outs = ctx.enter_context(tc.tile_pool(name="outs", bufs=11))
         psum = ctx.enter_context(tc.psum_pool(name="psum", bufs=1))
         ctx.enter_context(tc.manual_schedule())
 
         ident = keep.tile([P, P], F32, name="ident")
-        ones = keep.tile([P, P], BF16, name="ones")
-        grow = keep.tile([P, LORA], BF16, name="grow")
-        gain = keep.tile([P, LORA], F32, name="gain")
+        identb = keep.tile([P, P], BF16, name="identb")
+        gain4 = keep.tile([P, 4], BF16, name="gain4")
+        gain = keep.tile([P, LORA], BF16, name="gain")
         eps = keep.tile([P, 1], F32, name="eps")
         dummy = keep.tile([P, 1], F32, name="dummy")
         scale = keep.tile([P, 4], F32, name="scale")
         fr = keep.tile([P, NB * 64, 2], BF16, name="fr")
         nsin = keep.tile([P, NB * 64, 1], F32, name="nsin")
+        t1 = keep.tile([P, NB * 64, 2], F32, name="t1")
+        t2 = keep.tile([P, 2, NB * 64], F32, name="t2")
+        ro = keep.tile([P, NB * 64, 2], F32, name="ro")
         xraw = [keep.tile([P, C], BF16, name="xraw%d" % b) for b in range(NB)]
         wraw = [keep.tile([P, 4, WIDTH], BF16, name="wraw%d" % g) for g in range(NP)]
         wb = [keep.tile([P, 4, n], U8, name="wb%d" % i) for i, (o, n) in enumerate(BLOADS)]
@@ -74,31 +76,29 @@ def tile_multiheadlatentattention_pa_kernel(tc, x, freq_cis, Wckv, kv_norm_w, Wd
         def load_w(g):
             nc.sync.dma_start(out=wraw[g][:], in_=wv[g])
 
-        nc.vector.memset(grow[:].bitcast(U32), 0)
         def load_b(c):
             o, n = BLOADS[c]
             nc.sync.dma_start(out=wb[c][:], in_=bv[:, :, o : o + n])
 
         nc.sync.dma_start(out=scale[:], in_=Wdkv_scale.rearrange("(p j) o -> p (j o)", j=4))
+        nc.sync.dma_start(out=gain4[:], in_=kv_norm_w.rearrange("(p j) -> p j", j=4))
         load_b(0)
-        load_b(1)
-        load_x(0)
         load_w(0)
+        load_x(0)
         load_w(1)
-        nc.scalar.dma_start(out=grow[0:1, :], in_=kv_norm_w.rearrange("(o n) -> o n", o=1))
+        load_x(1)
         load_w(2)
         load_w(3)
-        load_x(1)
         load_x(2)
+        load_b(1)
         load_x(3)
-        nc.sync.dma_start(out=fr[:].rearrange("p i e -> p (i e)"), in_=freq_cis.rearrange("(p b) i e -> p (b i e)", b=NB))
         load_b(2)
+        nc.sync.dma_start(out=fr[:].rearrange("p i e -> p (i e)"), in_=freq_cis.rearrange("(p b) i e -> p (b i e)", b=NB))
 
         make_identity(nc, ident[:])
-        nc.vector.memset(ones[:], 1.0)
+        make_identity(nc, identb[:])
         nc.vector.memset(eps[:], 1e-6)
         nc.scalar.activation(dummy[:], eps[:], ACT.Abs_reciprocal_sqrt)
-        nc.gpsimd.tensor_scalar(nsin[:], fr[:, :, 1:2], -1.0, 0.0, ALU.mult, ALU.add)
 
         def four(t):
             return t.rearrange("p (c i) t -> p c t i", i=4)
@@ -127,17 +127,49 @@ def tile_multiheadlatentattention_pa_kernel(tc, x, freq_cis, Wckv, kv_norm_w, Wd
                 wg[g] = work.tile([P, LORA, 4], BF16, name="wg", align_bytes=64)
             return wg[g]
 
-        def w_inter_v(g):
-            nc.vector.tensor_copy(four(wg_tile(g)[:, 0 : WSPLIT[g], :]), by_four(wraw[g][:, :, 0 : WSPLIT[g]]))
+        def inter(eng, dst, src, lo, hi):
+            copy(eng, four(dst[:, lo:hi, :]), by_four(src[:, :, lo:hi]))
 
-        def w_inter_s(g):
-            nc.scalar.copy(four(wg_tile(g)[:, WSPLIT[g] : LORA, :]), by_four(wraw[g][:, :, WSPLIT[g] : LORA]))
+        def pe_inter(key, parts):
+            tp[key] = take()
+            bank = tp[key][1][:].bitcast(BF16)
+            for h, rows in enumerate(parts):
+                nc.tensor.matmul(bank[:, 512 * h : 512 * (h + 1)].rearrange("p (n j) -> p j n", j=4), lhsT=identb[:], rhs=rows, start=True, stop=True)
+
+        def pe_out(key, dst):
+            i, t = tp[key]
+            nc.scalar.copy(dst, t[:].bitcast(BF16))
+            idle.append(i)
+
+        def halves(src, h):
+            return [src[:, :, 256 * h + 128 * q : 256 * h + 128 * (q + 1)] for q in range(2)]
+
+        def w_pe(g, h):
+            pe_inter(("w", g, h), halves(wraw[g], h))
+
+        def w_pe_out(g, h):
+            pe_out(("w", g, h), wg_tile(g)[:, 256 * h : 256 * (h + 1), :].rearrange("p w j -> p (w j)"))
+
+        def w_inter(g, eng, lo, hi):
+            inter(eng, wg_tile(g), wraw[g], lo, hi)
+
+        def wr_pe(h):
+            pe_inter(("wr", h), [wraw[2 * h + q][:, :, LORA:WIDTH] for q in range(2)])
+
+        def wr_pe_out(h):
+            pe_out(("wr", h), wrg[:, 2 * h : 2 * h + 2, :, :].rearrange("p g w j -> p (g w j)"))
+
+        def d_pe(c, h):
+            pe_inter(("d", c, h), halves(wide[c], h))
+
+        def d_pe_out(c, h):
+            pe_out(("d", c, h), dg_tile(c)[:, 256 * h : 256 * (h + 1), :].rearrange("p w j -> p (w j)"))
 
         def w_quant(g):
             nc.vector.quantize_mx(out=wc[g][:].bitcast(FP8X4), scales=ws[g][:], in_=wg[g][:].rearrange("p w j -> p (w j)"))
 
         def wr_inter(g, eng):
-            copy(eng, four(wrg[:, g, :, :]), by_four(wraw[g][:, :, LORA:WIDTH]))
+            inter(eng, wrg[:, g, :, :], wraw[g][:, :, LORA:WIDTH], 0, ROPE)
 
         def wr_quant():
             nc.vector.quantize_mx(
@@ -193,9 +225,9 @@ def tile_multiheadlatentattention_pa_kernel(tc, x, freq_cis, Wckv, kv_norm_w, Wd
             )
 
         def kr_passes(b):
-            if b % 2 == 0:
-                tp[("kr", b // 2)] = take()
-            kr = tp[("kr", b // 2)][1][:, 128 * (b % 2) : 128 * (b % 2 + 1)]
+            if b == 0:
+                tp["kr"] = take()
+            kr = tp["kr"][1][:, ROPE * b : ROPE * (b + 1)]
             for g in range(NP):
                 nc.tensor.matmul_mx(
                     out=kr,
@@ -260,12 +292,8 @@ def tile_multiheadlatentattention_pa_kernel(tc, x, freq_cis, Wckv, kv_norm_w, Wd
                 dg[c] = work.tile([P, CHUNKS[c][1], 4], BF16, name="dg", align_bytes=64)
             return dg[c]
 
-        def d_inter_v(c):
-            nc.vector.tensor_copy(four(dg_tile(c)[:, 0 : DSPLIT[c], :]), by_four(wide[c][:, :, 0 : DSPLIT[c]]))
-
-        def d_inter_s(c):
-            n = CHUNKS[c][1]
-            nc.scalar.copy(four(dg_tile(c)[:, DSPLIT[c] : n, :]), by_four(wide[c][:, :, DSPLIT[c] : n]))
+        def d_inter(c):
+            inter("v", dg_tile(c), wide[c], 0, 512)
 
         def d_quant(c):
             nc.vector.quantize_mx(out=dc[c][:].bitcast(FP8X4), scales=ds[c][:], in_=dg[c][:].rearrange("p w j -> p (w j)"))
@@ -283,71 +311,212 @@ def tile_multiheadlatentattention_pa_kernel(tc, x, freq_cis, Wckv, kv_norm_w, Wd
                 stop=True,
             )
 
+        def single(b, c):
+            return c >= 4 or (b < 2 and c < 4)
+
         def kv_out(b, c, eng):
             i, t = tp[("kv", b, c)]
             key = ("o", b, c // 2)
-            first = key not in tp
-            if first:
+            if key not in tp:
                 tp[key] = outs.tile([P, 1024], F32, name="o")
             copy(eng, tp[key][:, 512 * (c % 2) : 512 * (c % 2 + 1)], t[:])
             idle.append(i)
-            if not first:
+            if single(b, c):
+                nc.sync.dma_start(out=kvv[:, b, 512 * c : 512 * (c + 1)], in_=tp[key][:, 512 * (c % 2) : 512 * (c % 2 + 1)])
+            elif c % 2 == 1:
                 m = c // 2
                 nc.sync.dma_start(out=kvv[:, b, 1024 * m : 1024 * (m + 1)], in_=tp[key][:])
 
-        def rope(h):
-            pairs = slice(128 * h, 128 * (h + 1))
-            cos, sin = fr[:, pairs, 0:1], fr[:, pairs, 1:2]
-            i, t = tp[("kr", h)]
-            k2 = t[:, 0:256].rearrange("p (i e) -> p i e", e=2)
-            t1 = work.tile([P, 128, 2], F32, name="t1", bufs=2)
-            t2 = work.tile([P, 2, 128], F32, name="t2", bufs=2)
-            ro = work.tile([P, 128, 2], F32, name="ro", bufs=2)
-            nc.vector.tensor_tensor(t1[:], k2, cos.to_broadcast([P, 128, 2]), ALU.mult)
-            nc.vector.tensor_tensor(t2[:, 0, :].unsqueeze(2), k2[:, :, 1:2], nsin[:, pairs, :], ALU.mult)
-            nc.vector.tensor_tensor(t2[:, 1, :].unsqueeze(2), k2[:, :, 0:1], sin, ALU.mult)
+        def rope_products():
+            i, t = tp["kr"]
+            k2 = t[:].rearrange("p (i e) -> p i e", e=2)
+            nc.vector.tensor_tensor(t1[:], k2, fr[:, :, 0:1].to_broadcast([P, NB * 64, 2]), ALU.mult)
+            nc.vector.tensor_tensor(t2[:, 0, :].unsqueeze(2), k2[:, :, 1:2], nsin[:], ALU.mult)
+            nc.vector.tensor_tensor(t2[:, 1, :].unsqueeze(2), k2[:, :, 0:1], fr[:, :, 1:2], ALU.mult)
             idle.append(i)
+
+        def rope_sum():
             nc.vector.tensor_tensor(ro[:], t1[:], t2[:].rearrange("p e i -> p i e"), ALU.add)
-            nc.sync.dma_start(out=krv[:, 256 * h : 256 * (h + 1)], in_=ro[:].rearrange("p i e -> p (i e)"))
+            nc.sync.dma_start(out=krv, in_=ro[:].rearrange("p i e -> p (i e)"))
 
         def gains():
             tp["gain"] = take()
-            nc.tensor.matmul(tp["gain"][1][:], lhsT=ones[:], rhs=grow[:], start=True, stop=True)
+            words = gain4[:].bitcast(F32)
+            for u in range(2):
+                nc.tensor.transpose(tp["gain"][1][:, u : 2 * P : 2], words[:, u : u + 1].to_broadcast([P, P]), ident[:])
 
-        def gain_out(eng):
+        def gain_out():
             i, t = tp["gain"]
-            copy(eng, gain[:], t[:])
+            nc.scalar.copy(gain[:].bitcast(F32), t[:, 0 : 2 * P])
             idle.append(i)
 
-        gains(); widen(0, 2, "s"); widen(0, 3, "v"); widen(0, 1, "v"); widen(0, 0, "v"); d_inter_s(0)
-        d_inter_v(0); widen(1, 2, "v"); widen(1, 0, "v"); widen(2, 0, "v"); widen(1, 1, "v"); d_quant(0)
-        widen(1, 3, "s"); d_inter_v(1); widen(3, 3, "s"); widen(3, 0, "s"); w_inter_v(0); widen(2, 3, "v")
-        w_inter_v(1); d_inter_s(1); widen(2, 2, "s"); x_trans(0, 0); x_out(0, 0, "s"); w_inter_s(0)
-        x_trans(0, 1); x_out(0, 1, "s"); x_quant(0); w_inter_v(2); w_quant(0); lat_pass(0, 0); widen(2, 1, "s")
-        w_inter_s(1); w_quant(1); lat_pass(0, 1); w_inter_v(3); w_inter_s(2); w_quant(2); widen(3, 2, "s")
-        w_inter_s(3); w_quant(3); widen(3, 1, "s"); d_inter_v(2); x_trans(1, 0); x_out(1, 0, "s"); x_trans(1, 1)
-        x_out(1, 1, "s"); x_quant(1); d_inter_v(3); lat_pass(0, 2); lat_pass(0, 3); stats(0); gain_out("s")
-        x_trans(2, 0); x_trans(2, 1); x_out(2, 1, "s"); x_trans(3, 1); root(0); norm(0); x_out(2, 0, "s")
-        x_quant(2); lat_pass(1, 0); lat_pass(1, 1); lat_pass(1, 2); d_inter_s(2); x_out(3, 1, "s"); d_quant(1)
-        d_quant(2); x_trans(3, 0); x_out(3, 0, "s"); n_trans(0); n_out(0, "s"); lat_pass(1, 3); stats(1)
-        d_inter_s(3); root(1); lat_pass(2, 0); lat_pass(2, 1); lat_pass(2, 2); lat_pass(2, 3); stats(2)
-        n_quant(0); kv_mm(0, 1); kv_out(0, 1, "s"); kv_mm(0, 0); kv_out(0, 0, "s"); root(2); x_quant(3)
-        lat_pass(3, 0); lat_pass(3, 1); lat_pass(3, 2); lat_pass(3, 3); stats(3); widen(6, 2, "v"); norm(1)
-        n_trans(1); n_out(1, "s"); kv_mm(0, 2); kv_out(0, 2, "s"); root(3); widen(7, 2, "v"); d_quant(3)
-        kv_mm(0, 3); kv_out(0, 3, "s"); widen(6, 3, "v"); norm(2); n_trans(2); widen(4, 1, "v"); n_quant(1)
-        widen(7, 3, "v"); widen(6, 1, "v"); norm(3); widen(7, 0, "v"); n_out(2, "s"); n_quant(2)
-        widen(7, 1, "v"); widen(6, 0, "v"); kv_mm(1, 3); kv_out(1, 3, "s"); kv_mm(1, 1); kv_mm(1, 2)
-        kv_out(1, 2, "s"); n_trans(3); n_out(3, "v"); widen(4, 3, "v"); kv_out(1, 1, "s"); kv_mm(1, 0)
-        kv_out(1, 0, "s"); kv_mm(2, 0); kv_mm(2, 1); kv_out(2, 0, "s"); kv_mm(2, 2); kv_out(2, 1, "s")
-        n_quant(3); kv_mm(3, 1); kv_mm(2, 3); kv_out(2, 3, "s"); kv_out(2, 2, "s"); d_inter_v(7)
-        widen(5, 2, "v"); kv_mm(3, 0); kv_mm(3, 2); kv_out(3, 0, "s"); kv_out(3, 1, "s"); kv_mm(3, 3)
-        kv_out(3, 3, "s"); d_quant(7); kv_mm(2, 7); kv_mm(0, 7); kv_out(3, 2, "s"); kv_mm(3, 7)
-        kv_out(3, 7, "s"); d_inter_v(6); widen(5, 0, "v"); d_quant(6); widen(4, 2, "v"); kv_mm(3, 6)
-        kv_out(3, 6, "s"); widen(4, 0, "v"); kv_out(2, 7, "s"); kv_mm(1, 6); kv_mm(2, 6); kv_out(2, 6, "s")
-        kv_mm(0, 6); kv_out(0, 6, "s"); kv_out(0, 7, "s"); widen(5, 3, "v"); d_inter_v(4); widen(5, 1, "v")
-        d_inter_s(5); kv_out(1, 6, "s"); kv_mm(1, 7); kv_out(1, 7, "s"); d_quant(4); kv_mm(1, 4); kv_mm(2, 4)
-        kv_out(1, 4, "s"); kv_mm(3, 4); d_inter_v(5); d_quant(5); kv_mm(1, 5); kv_out(1, 5, "s")
-        wr_inter(0, "v"); wr_inter(1, "v"); wr_inter(2, "v"); wr_inter(3, "v"); kv_out(3, 4, "v"); wr_quant()
-        kv_mm(0, 5); kv_out(0, 5, "v"); kv_out(2, 4, "v"); kv_mm(3, 5); kv_mm(2, 5); kv_out(3, 5, "s")
-        kv_mm(0, 4); kv_out(0, 4, "s"); kr_passes(0); kr_passes(1); rope(0); kv_out(2, 5, "s"); kr_passes(2)
-        kr_passes(3); rope(1)
+        def neg_sin():
+            nc.vector.tensor_scalar(nsin[:], fr[:, :, 1:2], -1.0, None, ALU.mult)
+
+        def x_turn(b):
+            for h in range(2):
+                x_trans(b, h)
+                x_out(b, h, "s")
+
+        def x_both(b):
+            for h in range(2):
+                x_trans(b, h)
+
+        def d_both(c):
+            for h in range(2):
+                d_pe(c, h)
+
+        def lat_all(b):
+            for g in range(NP):
+                lat_pass(b, g)
+
+        def widen_all(c):
+            for j in range(4):
+                widen(c, j, "v")
+
+        def kv(b, c, eng="s"):
+            kv_mm(b, c)
+            kv_out(b, c, eng)
+
+        gains()
+        for c in range(2):
+            for j in range(3):
+                widen(c, j, "v")
+            widen(c, 3, "s")
+        gain_out()
+        d_pe(0, 0)
+        d_pe(0, 1)
+        x_both(0)
+        w_inter(0, "v", 0, LORA)
+        wr_inter(0, "s")
+        d_pe_out(0, 0)
+        d_pe_out(0, 1)
+        w_quant(0)
+        w_inter(1, "v", 0, LORA)
+        x_out(0, 0, "s")
+        x_out(0, 1, "s")
+        d_pe(1, 0)
+        x_both(1)
+        d_pe(1, 1)
+        d_quant(0)
+        w_quant(1)
+        wr_inter(1, "s")
+        d_pe_out(1, 0)
+        x_quant(0)
+        w_inter(2, "v", 0, WSPLIT)
+        w_inter(2, "s", WSPLIT, LORA)
+        x_out(1, 0, "s")
+        w_inter(3, "v", 0, WSPLIT)
+        w_inter(3, "s", WSPLIT, LORA)
+        x_out(1, 1, "s")
+        w_quant(2)
+        w_quant(3)
+        x_quant(1)
+        lat_pass(0, 0)
+        lat_pass(0, 1)
+        x_trans(2, 0)
+        lat_pass(0, 2)
+        lat_pass(0, 3)
+        x_trans(2, 1)
+        lat_all(1)
+        x_trans(3, 0)
+        d_pe_out(1, 1)
+        x_out(2, 0, "s")
+        stats(0)
+        root(0)
+        x_out(2, 1, "s")
+        stats(1)
+        x_out(3, 0, "s")
+        root(1)
+        d_quant(1)
+        for j in range(3):
+            widen(2, j, "v")
+        norm(0)
+        n_trans(0)
+        x_trans(3, 1)
+        n_out(0, "s")
+        x_out(3, 1, "s")
+        widen(3, 1, "s")
+        x_quant(2)
+        widen(2, 3, "v")
+        widen(3, 0, "v")
+        norm(1)
+        n_quant(0)
+        lat_all(2)
+        n_trans(1)
+        kv_mm(0, 0)
+        kv_mm(0, 1)
+        x_quant(3)
+        lat_all(3)
+        stats(2)
+        n_out(1, "s")
+        root(2)
+        kv_out(0, 0, "s")
+        kv_out(0, 1, "s")
+        d_inter(2)
+        n_quant(1)
+        norm(2)
+        d_quant(2)
+        kv_mm(1, 0)
+        kv_mm(1, 1)
+        n_trans(2)
+        kv_mm(0, 2)
+        kv_mm(1, 2)
+        stats(3)
+        kv_out(1, 0, "s")
+        root(3)
+        n_out(2, "s")
+        kv_out(1, 1, "s")
+        widen(3, 2, "v")
+        widen(3, 3, "v")
+        norm(3)
+        n_quant(2)
+        n_trans(3)
+        kv_mm(2, 0)
+        kv_mm(2, 1)
+        kv_out(0, 2, "s")
+        n_out(3, "s")
+        kv_out(1, 2, "s")
+        d_inter(3)
+        n_quant(3)
+        widen(4, 0, "v")
+        d_quant(3)
+        for j in range(1, 4):
+            widen(4, j, "v")
+        kv_out(2, 0, "s")
+        kv_out(2, 1, "s")
+        kv(3, 0)
+        kv(3, 1)
+        wr_pe(1)
+        kv(0, 3)
+        kv(1, 3)
+        wr_pe_out(1)
+        for b in range(2, 4):
+            kv(b, 2)
+            kv(b, 3)
+        widen(5, 0, "v")
+        for c in range(4, NCH):
+            d_inter(c)
+            if c + 1 < NCH:
+                for j in range(1, 4):
+                    widen(c + 1, j, "v")
+            else:
+                neg_sin()
+            d_quant(c)
+            if c + 2 < NCH:
+                widen(c + 2, 0, "v")
+            if c + 1 < NCH:
+                for b in range(NB):
+                    kv(b, c)
+            if c == 5:
+                wr_quant()
+                for b in range(NB):
+                    kr_passes(b)
+        for b in range(NB):
+            kv_mm(b, NCH - 1)
+        rope_products()
+        kv_out(0, NCH - 1, "s")
+        kv_out(1, NCH - 1, "s")
+        kv_out(3, NCH - 1, "v")
+        kv_out(2, NCH - 1, "s")
+        rope_sum()

@@ -34,7 +34,7 @@ def tile_multiheadlatentattention_pa_kernel(tc, x, freq_cis, Wckv, kv_norm_w, Wd
     with ExitStack() as ctx:
         keep = ctx.enter_context(tc.tile_pool(name="keep", bufs=1))
         work = ctx.enter_context(tc.tile_pool(name="work", bufs=4))
-        outs = ctx.enter_context(tc.tile_pool(name="outs", bufs=11))
+        outs = ctx.enter_context(tc.tile_pool(name="outs", bufs=10))
         psum = ctx.enter_context(tc.psum_pool(name="psum", bufs=1))
         ctx.enter_context(tc.manual_schedule())
 
@@ -144,20 +144,8 @@ def tile_multiheadlatentattention_pa_kernel(tc, x, freq_cis, Wckv, kv_norm_w, Wd
         def halves(src, h):
             return [src[:, :, 256 * h + 128 * q : 256 * h + 128 * (q + 1)] for q in range(2)]
 
-        def w_pe(g, h):
-            pe_inter(("w", g, h), halves(wraw[g], h))
-
-        def w_pe_out(g, h):
-            pe_out(("w", g, h), wg_tile(g)[:, 256 * h : 256 * (h + 1), :].rearrange("p w j -> p (w j)"))
-
         def w_inter(g, eng, lo, hi):
             inter(eng, wg_tile(g), wraw[g], lo, hi)
-
-        def wr_pe(h):
-            pe_inter(("wr", h), [wraw[2 * h + q][:, :, LORA:WIDTH] for q in range(2)])
-
-        def wr_pe_out(h):
-            pe_out(("wr", h), wrg[:, 2 * h : 2 * h + 2, :, :].rearrange("p g w j -> p (g w j)"))
 
         def d_pe(c, h):
             pe_inter(("d", c, h), halves(wide[c], h))
@@ -279,7 +267,7 @@ def tile_multiheadlatentattention_pa_kernel(tc, x, freq_cis, Wckv, kv_norm_w, Wd
         def widen(c, j, eng):
             t, o, n = bytes_of(c)
             if c not in wide:
-                wide[c] = work.tile([P, 4, n], BF16, name="wide", bufs=5)
+                wide[c] = work.tile([P, 4, n], BF16, name="wide", bufs=4)
             w = wide[c][:, j, :]
             b = t[:, j, o : o + n].bitcast(FP8)
             if eng == "v":
@@ -294,6 +282,9 @@ def tile_multiheadlatentattention_pa_kernel(tc, x, freq_cis, Wckv, kv_norm_w, Wd
 
         def d_inter(c):
             inter("v", dg_tile(c), wide[c], 0, 512)
+
+        def d_half(c, h, eng):
+            inter(eng, dg_tile(c), wide[c], 256 * h, 256 * (h + 1))
 
         def d_quant(c):
             nc.vector.quantize_mx(out=dc[c][:].bitcast(FP8X4), scales=ds[c][:], in_=dg[c][:].rearrange("p w j -> p (w j)"))
@@ -311,9 +302,6 @@ def tile_multiheadlatentattention_pa_kernel(tc, x, freq_cis, Wckv, kv_norm_w, Wd
                 stop=True,
             )
 
-        def single(b, c):
-            return c >= 4 or (b < 2 and c < 4)
-
         def kv_out(b, c, eng):
             i, t = tp[("kv", b, c)]
             key = ("o", b, c // 2)
@@ -321,9 +309,7 @@ def tile_multiheadlatentattention_pa_kernel(tc, x, freq_cis, Wckv, kv_norm_w, Wd
                 tp[key] = outs.tile([P, 1024], F32, name="o")
             copy(eng, tp[key][:, 512 * (c % 2) : 512 * (c % 2 + 1)], t[:])
             idle.append(i)
-            if single(b, c):
-                nc.sync.dma_start(out=kvv[:, b, 512 * c : 512 * (c + 1)], in_=tp[key][:, 512 * (c % 2) : 512 * (c % 2 + 1)])
-            elif c % 2 == 1:
+            if c % 2 == 1:
                 m = c // 2
                 nc.sync.dma_start(out=kvv[:, b, 1024 * m : 1024 * (m + 1)], in_=tp[key][:])
 
@@ -361,10 +347,6 @@ def tile_multiheadlatentattention_pa_kernel(tc, x, freq_cis, Wckv, kv_norm_w, Wd
         def x_both(b):
             for h in range(2):
                 x_trans(b, h)
-
-        def d_both(c):
-            for h in range(2):
-                d_pe(c, h)
 
         def lat_all(b):
             for g in range(NP):
@@ -436,10 +418,11 @@ def tile_multiheadlatentattention_pa_kernel(tc, x, freq_cis, Wckv, kv_norm_w, Wd
         x_trans(3, 1)
         n_out(0, "s")
         x_out(3, 1, "s")
-        widen(3, 1, "s")
+        widen(3, 3, "s")
         x_quant(2)
         widen(2, 3, "v")
         widen(3, 0, "v")
+        widen(3, 1, "v")
         norm(1)
         n_quant(0)
         lat_all(2)
@@ -447,76 +430,101 @@ def tile_multiheadlatentattention_pa_kernel(tc, x, freq_cis, Wckv, kv_norm_w, Wd
         kv_mm(0, 0)
         kv_mm(0, 1)
         x_quant(3)
-        lat_all(3)
+        lat_pass(3, 0)
+        lat_pass(3, 1)
         stats(2)
         n_out(1, "s")
         root(2)
-        kv_out(0, 0, "s")
-        kv_out(0, 1, "s")
-        d_inter(2)
+        d_half(2, 0, "v")
         n_quant(1)
         norm(2)
-        d_quant(2)
         kv_mm(1, 0)
         kv_mm(1, 1)
         n_trans(2)
-        kv_mm(0, 2)
-        kv_mm(1, 2)
+        lat_pass(3, 2)
+        lat_pass(3, 3)
+        for b in range(2):
+            kv_out(b, 0, "s")
+            kv_out(b, 1, "s")
         stats(3)
-        kv_out(1, 0, "s")
         root(3)
-        n_out(2, "s")
-        kv_out(1, 1, "s")
+        d_half(2, 1, "v")
         widen(3, 2, "v")
-        widen(3, 3, "v")
-        norm(3)
+        n_out(2, "v")
+        d_quant(2)
         n_quant(2)
-        n_trans(3)
-        kv_mm(2, 0)
-        kv_mm(2, 1)
-        kv_out(0, 2, "s")
-        n_out(3, "s")
-        kv_out(1, 2, "s")
+        kv(2, 0)
+        kv(2, 1)
         d_inter(3)
-        n_quant(3)
-        widen(4, 0, "v")
+        for b in range(3):
+            kv_mm(b, 2)
+        norm(3)
         d_quant(3)
+        n_trans(3)
+        for b in range(3):
+            kv_mm(b, 3)
+        for b in range(2):
+            kv_out(b, 2, "s")
+        widen(4, 0, "v")
+        n_out(3, "v")
+        widen(4, 1, "v")
+        n_quant(3)
+        for b in range(2):
+            kv_out(b, 3, "s")
+        for c in range(4):
+            kv_mm(3, c)
+        kv_out(2, 2, "s")
+        kv_out(2, 3, "s")
+        widen(4, 2, "v")
+        widen(4, 3, "v")
+        widen_all(5)
+        d_pe(5, 0)
+        d_inter(4)
+        d_half(5, 1, "v")
+        d_quant(4)
+        for c in range(3):
+            kv_out(3, c, "s")
+        d_pe_out(5, 0)
+        kv_out(3, 3, "s")
+        for b in range(2):
+            kv_mm(b, 4)
+        widen(6, 0, "v")
+        d_quant(5)
+        for b in range(2):
+            kv_mm(b, 5)
         for j in range(1, 4):
-            widen(4, j, "v")
-        kv_out(2, 0, "s")
-        kv_out(2, 1, "s")
-        kv(3, 0)
-        kv(3, 1)
-        wr_pe(1)
-        kv(0, 3)
-        kv(1, 3)
-        wr_pe_out(1)
+            widen(6, j, "v")
+        d_pe(6, 0)
+        widen_all(7)
+        d_half(6, 1, "v")
+        for b in range(2):
+            kv_out(b, 4, "s")
+        for b in range(2):
+            kv_out(b, 5, "s")
+        d_pe_out(6, 0)
         for b in range(2, 4):
-            kv(b, 2)
-            kv(b, 3)
-        widen(5, 0, "v")
-        for c in range(4, NCH):
-            d_inter(c)
-            if c + 1 < NCH:
-                for j in range(1, 4):
-                    widen(c + 1, j, "v")
-            else:
-                neg_sin()
-            d_quant(c)
-            if c + 2 < NCH:
-                widen(c + 2, 0, "v")
-            if c + 1 < NCH:
-                for b in range(NB):
-                    kv(b, c)
-            if c == 5:
-                wr_quant()
-                for b in range(NB):
-                    kr_passes(b)
+            kv(b, 4)
+            kv(b, 5)
+        d_inter(7)
+        d_quant(6)
+        d_quant(7)
+        wr_inter(2, "v")
+        wr_inter(3, "v")
+        neg_sin()
+        wr_quant()
         for b in range(NB):
-            kv_mm(b, NCH - 1)
+            kv_mm(b, 6)
+            kv_mm(b, 7)
+            if b == 1:
+                kv_out(0, 6, "s")
+                kv_out(0, 7, "s")
+        kv_out(1, 6, "v")
+        kv_out(1, 7, "v")
+        for b in range(NB):
+            kr_passes(b)
+        kv_out(2, 6, "s")
+        kv_out(2, 7, "s")
         rope_products()
-        kv_out(0, NCH - 1, "s")
-        kv_out(1, NCH - 1, "s")
-        kv_out(3, NCH - 1, "v")
-        kv_out(2, NCH - 1, "s")
+        kv_out(3, 6, "s")
+        kv_out(3, 7, "s")
         rope_sum()

@@ -21,7 +21,7 @@ NB = T // P
 NP = C // 512
 CHUNKS = [(512 * c, 512) for c in range(8)]
 NCH = len(CHUNKS)
-BLOADS = [(0, 1024), (1024, 1024), (2048, 2048)]
+BLOADS = [(0, 512), (512, 1536), (2048, 2048)]
 WSPLIT = 320
 
 
@@ -80,17 +80,17 @@ def tile_multiheadlatentattention_pa_kernel(tc, x, freq_cis, Wckv, kv_norm_w, Wd
             o, n = BLOADS[c]
             nc.sync.dma_start(out=wb[c][:], in_=bv[:, :, o : o + n])
 
-        nc.sync.dma_start(out=scale[:], in_=Wdkv_scale.rearrange("(p j) o -> p (j o)", j=4))
-        nc.sync.dma_start(out=gain4[:], in_=kv_norm_w.rearrange("(p j) -> p j", j=4))
+        nc.scalar.dma_start(out=scale[:], in_=Wdkv_scale.rearrange("(p j) o -> p (j o)", j=4))
+        nc.scalar.dma_start(out=gain4[:], in_=kv_norm_w.rearrange("(p j) -> p j", j=4))
         load_b(0)
-        load_w(0)
+        load_b(1)
         load_x(0)
+        load_w(0)
         load_w(1)
         load_x(1)
         load_w(2)
         load_w(3)
         load_x(2)
-        load_b(1)
         load_x(3)
         load_b(2)
         nc.sync.dma_start(out=fr[:].rearrange("p i e -> p (i e)"), in_=freq_cis.rearrange("(p b) i e -> p (b i e)", b=NB))
@@ -138,7 +138,7 @@ def tile_multiheadlatentattention_pa_kernel(tc, x, freq_cis, Wckv, kv_norm_w, Wd
 
         def pe_out(key, dst):
             i, t = tp[key]
-            nc.scalar.copy(dst, t[:].bitcast(BF16))
+            nc.scalar.copy(dst.bitcast(F32), t[:])
             idle.append(i)
 
         def halves(src, h):
@@ -361,36 +361,46 @@ def tile_multiheadlatentattention_pa_kernel(tc, x, freq_cis, Wckv, kv_norm_w, Wd
             kv_out(b, c, eng)
 
         gains()
-        for c in range(2):
-            for j in range(3):
-                widen(c, j, "v")
-            widen(c, 3, "s")
-        gain_out()
-        d_pe(0, 0)
-        d_pe(0, 1)
+        for j in range(3):
+            widen(0, j, "v")
+        widen(0, 3, "s")
+        d_inter(0)
+        for j in range(3):
+            widen(1, j, "v")
+        widen(1, 3, "s")
+        d_pe(1, 0)
         x_both(0)
-        w_inter(0, "v", 0, LORA)
-        wr_inter(0, "s")
-        d_pe_out(0, 0)
-        d_pe_out(0, 1)
-        w_quant(0)
-        w_inter(1, "v", 0, LORA)
+        d_pe(1, 1)
+        for j in range(3):
+            widen(2, j, "v")
+        widen(2, 3, "s")
+        for j in range(2):
+            widen(3, j, "v")
+            widen(3, j + 2, "s")
+        gain_out()
+        d_pe(2, 0)
+        x_both(1)
+        d_pe(2, 1)
+        d_pe_out(1, 0)
         x_out(0, 0, "s")
         x_out(0, 1, "s")
-        d_pe(1, 0)
-        x_both(1)
-        d_pe(1, 1)
+        w_inter(0, "v", 0, LORA)
         d_quant(0)
-        w_quant(1)
-        wr_inter(1, "s")
-        d_pe_out(1, 0)
+        w_inter(1, "v", 0, WSPLIT)
+        w_inter(1, "s", WSPLIT, LORA)
+        d_pe_out(1, 1)
+        d_pe_out(2, 0)
+        w_quant(0)
         x_quant(0)
+        w_quant(1)
         w_inter(2, "v", 0, WSPLIT)
         w_inter(2, "s", WSPLIT, LORA)
         x_out(1, 0, "s")
+        d_quant(1)
         w_inter(3, "v", 0, WSPLIT)
         w_inter(3, "s", WSPLIT, LORA)
         x_out(1, 1, "s")
+        d_pe_out(2, 1)
         w_quant(2)
         w_quant(3)
         x_quant(1)
@@ -402,129 +412,109 @@ def tile_multiheadlatentattention_pa_kernel(tc, x, freq_cis, Wckv, kv_norm_w, Wd
         x_trans(2, 1)
         lat_all(1)
         x_trans(3, 0)
-        d_pe_out(1, 1)
         x_out(2, 0, "s")
         stats(0)
         root(0)
         x_out(2, 1, "s")
+        wr_inter(0, "s")
         stats(1)
         x_out(3, 0, "s")
         root(1)
-        d_quant(1)
-        for j in range(3):
-            widen(2, j, "v")
+        d_inter(3)
         norm(0)
         n_trans(0)
         x_trans(3, 1)
         n_out(0, "s")
         x_out(3, 1, "s")
-        widen(3, 3, "s")
+        wr_inter(1, "s")
         x_quant(2)
-        widen(2, 3, "v")
-        widen(3, 0, "v")
-        widen(3, 1, "v")
-        norm(1)
+        d_quant(2)
+        d_quant(3)
         n_quant(0)
+        norm(1)
         lat_all(2)
-        n_trans(1)
         kv_mm(0, 0)
         kv_mm(0, 1)
+        n_trans(1)
+        kv_mm(0, 2)
+        kv_mm(0, 3)
         x_quant(3)
-        lat_pass(3, 0)
-        lat_pass(3, 1)
+        lat_all(3)
         stats(2)
-        n_out(1, "s")
+        kv_out(0, 0, "s")
         root(2)
-        d_half(2, 0, "v")
+        for c in range(1, 4):
+            kv_out(0, c, "s")
+        widen(4, 0, "v")
+        n_out(1, "v")
+        widen(4, 1, "v")
         n_quant(1)
         norm(2)
-        kv_mm(1, 0)
-        kv_mm(1, 1)
         n_trans(2)
-        lat_pass(3, 2)
-        lat_pass(3, 3)
-        for b in range(2):
-            kv_out(b, 0, "s")
-            kv_out(b, 1, "s")
-        stats(3)
-        root(3)
-        d_half(2, 1, "v")
-        widen(3, 2, "v")
-        n_out(2, "v")
-        d_quant(2)
-        n_quant(2)
-        kv(2, 0)
-        kv(2, 1)
-        d_inter(3)
-        for b in range(3):
-            kv_mm(b, 2)
-        norm(3)
-        d_quant(3)
-        n_trans(3)
-        for b in range(3):
-            kv_mm(b, 3)
-        for b in range(2):
-            kv_out(b, 2, "s")
-        widen(4, 0, "v")
-        n_out(3, "v")
-        widen(4, 1, "v")
-        n_quant(3)
-        for b in range(2):
-            kv_out(b, 3, "s")
         for c in range(4):
-            kv_mm(3, c)
-        kv_out(2, 2, "s")
-        kv_out(2, 3, "s")
+            kv_mm(1, c)
+        stats(3)
+        kv_out(1, 0, "s")
+        root(3)
+        for c in range(1, 4):
+            kv_out(1, c, "s")
         widen(4, 2, "v")
         widen(4, 3, "v")
-        widen_all(5)
-        d_pe(5, 0)
-        d_inter(4)
-        d_half(5, 1, "v")
+        widen(5, 0, "v")
+        n_out(2, "v")
+        d_half(4, 0, "v")
+        n_quant(2)
+        norm(3)
+        kv_mm(2, 0)
+        kv_mm(2, 1)
+        n_trans(3)
+        kv_mm(2, 2)
+        kv_mm(2, 3)
+        for c in range(4):
+            kv_out(2, c, "s")
+        d_half(4, 1, "v")
+        n_out(3, "v")
         d_quant(4)
-        for c in range(3):
-            kv_out(3, c, "s")
-        d_pe_out(5, 0)
-        kv_out(3, 3, "s")
-        for b in range(2):
-            kv_mm(b, 4)
-        widen(6, 0, "v")
-        d_quant(5)
-        for b in range(2):
-            kv_mm(b, 5)
+        n_quant(3)
+        for c in range(4):
+            kv(3, c)
         for j in range(1, 4):
-            widen(6, j, "v")
-        d_pe(6, 0)
-        widen_all(7)
-        d_half(6, 1, "v")
-        for b in range(2):
-            kv_out(b, 4, "s")
-        for b in range(2):
-            kv_out(b, 5, "s")
-        d_pe_out(6, 0)
-        for b in range(2, 4):
-            kv(b, 4)
-            kv(b, 5)
-        d_inter(7)
+            widen(5, j, "v")
+        widen(6, 0, "v")
+        d_inter(5)
+        widen(6, 1, "v")
+        d_quant(5)
+        widen(6, 2, "v")
+        widen(6, 3, "v")
+        widen(7, 0, "v")
+        d_inter(6)
+        for j in range(1, 4):
+            widen(7, j, "v")
         d_quant(6)
-        d_quant(7)
+        d_inter(7)
         wr_inter(2, "v")
+        d_quant(7)
         wr_inter(3, "v")
         neg_sin()
         wr_quant()
         for b in range(NB):
+            kv(b, 4)
+            kv(b, 5)
+        for b in range(NB):
             kv_mm(b, 6)
+        for b in range(2):
             kv_mm(b, 7)
-            if b == 1:
-                kv_out(0, 6, "s")
-                kv_out(0, 7, "s")
-        kv_out(1, 6, "v")
-        kv_out(1, 7, "v")
+        for b in range(2):
+            kv_out(b, 6, "s")
+        kv_out(0, 7, "s")
+        kv_out(3, 6, "v")
+        for b in range(2, NB):
+            kv_mm(b, 7)
         for b in range(NB):
             kr_passes(b)
+        kv_out(1, 7, "s")
         kv_out(2, 6, "s")
         kv_out(2, 7, "s")
         rope_products()
-        kv_out(3, 6, "s")
         kv_out(3, 7, "s")
         rope_sum()

@@ -21,7 +21,7 @@ NB = T // P
 NP = C // 512
 CHUNKS = [(512 * c, 512) for c in range(8)]
 NCH = len(CHUNKS)
-BLOADS = [(0, 512), (512, 1536), (2048, 2048)]
+BLOADS = [(0, 1024), (1024, 1024), (2048, 2048)]
 WSPLIT = 320
 
 
@@ -361,35 +361,31 @@ def tile_multiheadlatentattention_pa_kernel(tc, x, freq_cis, Wckv, kv_norm_w, Wd
             kv_out(b, c, eng)
 
         gains()
-        for j in range(3):
-            widen(0, j, "v")
-        widen(0, 3, "s")
-        d_inter(0)
-        for j in range(3):
-            widen(1, j, "v")
-        widen(1, 3, "s")
-        d_pe(1, 0)
+        for c in (0, 1, 3, 2):
+            for j in range(3):
+                widen(c, j, "v")
+            widen(c, 3, "s")
+            if c == 1:
+                gain_out()
+        d_pe(0, 0)
+        d_pe(0, 1)
         x_both(0)
+        d_pe(1, 0)
         d_pe(1, 1)
-        for j in range(3):
-            widen(2, j, "v")
-        widen(2, 3, "s")
-        for j in range(2):
-            widen(3, j, "v")
-            widen(3, j + 2, "s")
-        gain_out()
-        d_pe(2, 0)
         x_both(1)
-        d_pe(2, 1)
-        d_pe_out(1, 0)
+        d_pe_out(0, 0)
+        d_pe_out(0, 1)
+        d_pe(2, 0)
         x_out(0, 0, "s")
         x_out(0, 1, "s")
+        d_pe(2, 1)
+        d_half(3, 0, "v")
         w_inter(0, "v", 0, LORA)
         d_quant(0)
         w_inter(1, "v", 0, WSPLIT)
         w_inter(1, "s", WSPLIT, LORA)
+        d_pe_out(1, 0)
         d_pe_out(1, 1)
-        d_pe_out(2, 0)
         w_quant(0)
         x_quant(0)
         w_quant(1)
@@ -400,6 +396,7 @@ def tile_multiheadlatentattention_pa_kernel(tc, x, freq_cis, Wckv, kv_norm_w, Wd
         w_inter(3, "v", 0, WSPLIT)
         w_inter(3, "s", WSPLIT, LORA)
         x_out(1, 1, "s")
+        d_pe_out(2, 0)
         d_pe_out(2, 1)
         w_quant(2)
         w_quant(3)
@@ -416,20 +413,23 @@ def tile_multiheadlatentattention_pa_kernel(tc, x, freq_cis, Wckv, kv_norm_w, Wd
         stats(0)
         root(0)
         x_out(2, 1, "s")
-        wr_inter(0, "s")
         stats(1)
         x_out(3, 0, "s")
         root(1)
-        d_inter(3)
+        d_half(3, 1, "v")
+        d_quant(2)
+        d_quant(3)
         norm(0)
         n_trans(0)
         x_trans(3, 1)
         n_out(0, "s")
         x_out(3, 1, "s")
-        wr_inter(1, "s")
+        widen(4, 3, "s")
         x_quant(2)
-        d_quant(2)
-        d_quant(3)
+        widen(4, 0, "v")
+        widen(4, 1, "v")
+        widen(4, 2, "v")
+        widen(5, 0, "v")
         n_quant(0)
         norm(1)
         lat_all(2)
@@ -442,27 +442,28 @@ def tile_multiheadlatentattention_pa_kernel(tc, x, freq_cis, Wckv, kv_norm_w, Wd
         lat_all(3)
         stats(2)
         kv_out(0, 0, "s")
+        kv_out(0, 1, "v")
         root(2)
-        for c in range(1, 4):
-            kv_out(0, c, "s")
-        widen(4, 0, "v")
-        n_out(1, "v")
-        widen(4, 1, "v")
+        n_out(1, "s")
+        kv_out(0, 2, "s")
+        kv_out(0, 3, "s")
+        d_half(4, 0, "v")
         n_quant(1)
         norm(2)
+        kv_mm(1, 0)
+        kv_mm(1, 1)
         n_trans(2)
-        for c in range(4):
-            kv_mm(1, c)
+        kv_mm(1, 2)
+        kv_mm(1, 3)
         stats(3)
         kv_out(1, 0, "s")
         root(3)
-        for c in range(1, 4):
-            kv_out(1, c, "s")
-        widen(4, 2, "v")
-        widen(4, 3, "v")
-        widen(5, 0, "v")
+        d_half(4, 1, "v")
+        kv_out(1, 1, "v")
+        kv_out(1, 2, "s")
+        kv_out(1, 3, "s")
         n_out(2, "v")
-        d_half(4, 0, "v")
+        widen(5, 1, "v")
         n_quant(2)
         norm(3)
         kv_mm(2, 0)
@@ -472,15 +473,14 @@ def tile_multiheadlatentattention_pa_kernel(tc, x, freq_cis, Wckv, kv_norm_w, Wd
         kv_mm(2, 3)
         for c in range(4):
             kv_out(2, c, "s")
-        d_half(4, 1, "v")
-        n_out(3, "v")
         d_quant(4)
+        widen(5, 2, "v")
+        widen(5, 3, "v")
+        n_out(3, "v")
+        widen(6, 0, "v")
         n_quant(3)
         for c in range(4):
             kv(3, c)
-        for j in range(1, 4):
-            widen(5, j, "v")
-        widen(6, 0, "v")
         d_inter(5)
         widen(6, 1, "v")
         d_quant(5)
@@ -492,9 +492,10 @@ def tile_multiheadlatentattention_pa_kernel(tc, x, freq_cis, Wckv, kv_norm_w, Wd
             widen(7, j, "v")
         d_quant(6)
         d_inter(7)
-        wr_inter(2, "v")
+        wr_inter(0, "v")
         d_quant(7)
-        wr_inter(3, "v")
+        for g in range(1, NP):
+            wr_inter(g, "v")
         neg_sin()
         wr_quant()
         for b in range(NB):

@@ -22,6 +22,7 @@ NP = C // 512
 CHUNKS = [(512 * c, 512) for c in range(8)]
 NCH = len(CHUNKS)
 BLOADS = [(0, 1024), (1024, 1024), (2048, 2048)]
+WARM_UPS = 6
 WSPLIT = 320
 
 
@@ -325,6 +326,12 @@ def tile_multiheadlatentattention_pa_kernel(tc, x, freq_cis, Wckv, kv_norm_w, Wd
             nc.vector.tensor_tensor(ro[:], t1[:], t2[:].rearrange("p e i -> p i e"), ALU.add)
             nc.sync.dma_start(out=krv, in_=ro[:].rearrange("p i e -> p (i e)"))
 
+        def warm_up():
+            i, t = take()
+            for n in range(WARM_UPS):
+                nc.tensor.matmul(t[:].rearrange("p (a n) -> p a n", a=4), lhsT=identb[:], rhs=identb[:].unsqueeze(1).to_broadcast([P, 4, P]), start=True, stop=True)
+            idle.append(i)
+
         def gains():
             tp["gain"] = take()
             words = gain4[:].bitcast(F32)
@@ -360,6 +367,7 @@ def tile_multiheadlatentattention_pa_kernel(tc, x, freq_cis, Wckv, kv_norm_w, Wd
             kv_mm(b, c)
             kv_out(b, c, eng)
 
+        warm_up()
         gains()
         for c in (0, 1, 3, 2):
             for j in range(3):

@@ -22,7 +22,7 @@ NP = C // 512
 CHUNKS = [(512 * c, 512) for c in range(8)]
 NCH = len(CHUNKS)
 BLOADS = [(0, 1024), (1024, 1024), (2048, 2048)]
-WARM_UPS = 6
+WARM_UPS = 5
 WSPLIT = 320
 
 
@@ -146,7 +146,9 @@ def tile_multiheadlatentattention_pa_kernel(tc, x, freq_cis, Wckv, kv_norm_w, Wd
             return [src[:, :, 256 * h + 128 * q : 256 * h + 128 * (q + 1)] for q in range(2)]
 
         def w_inter(g, eng, lo, hi):
-            inter(eng, wg_tile(g), wraw[g], lo, hi)
+            dst = wg_tile(g)[:].rearrange("p (u c e) t -> p c t u e", u=2, e=2)
+            src = wraw[g][:, :, 0:LORA].rearrange("p t (c u e) -> p c t u e", u=2, e=2)
+            copy(eng, dst[:, lo // 4 : hi // 4], src[:, lo // 4 : hi // 4])
 
         def d_pe(c, h):
             pe_inter(("d", c, h), halves(wide[c], h))
@@ -244,7 +246,7 @@ def tile_multiheadlatentattention_pa_kernel(tc, x, freq_cis, Wckv, kv_norm_w, Wd
             tp[(b, 2)] = take()
             words = nb[b][:].bitcast(F32)
             for u in range(2):
-                nc.tensor.transpose(tp[(b, 2)][1][:, P * u : P * (u + 1)], words[:, u::2], ident[:])
+                nc.tensor.transpose(tp[(b, 2)][1][:, P * u : P * (u + 1)], words[:, P * u : P * (u + 1)], ident[:])
 
         def n_out(b, eng):
             ng[b] = work.tile([P, P, 4], BF16, name="ng", align_bytes=64)
@@ -336,7 +338,7 @@ def tile_multiheadlatentattention_pa_kernel(tc, x, freq_cis, Wckv, kv_norm_w, Wd
             tp["gain"] = take()
             words = gain4[:].bitcast(F32)
             for u in range(2):
-                nc.tensor.transpose(tp["gain"][1][:, u : 2 * P : 2], words[:, u : u + 1].to_broadcast([P, P]), ident[:])
+                nc.tensor.transpose(tp["gain"][1][:, P * u : P * (u + 1)], words[:, u : u + 1].to_broadcast([P, P]), ident[:])
 
         def gain_out():
             i, t = tp["gain"]
@@ -373,16 +375,15 @@ def tile_multiheadlatentattention_pa_kernel(tc, x, freq_cis, Wckv, kv_norm_w, Wd
             for j in range(3):
                 widen(c, j, "v")
             widen(c, 3, "s")
-            if c == 1:
-                gain_out()
         d_pe(0, 0)
         d_pe(0, 1)
         x_both(0)
         d_pe(1, 0)
         d_pe(1, 1)
-        x_both(1)
         d_pe_out(0, 0)
+        gain_out()
         d_pe_out(0, 1)
+        x_both(1)
         d_pe(2, 0)
         x_out(0, 0, "s")
         x_out(0, 1, "s")

@@ -23,7 +23,7 @@ CHUNKS = [(512 * c, 512) for c in range(8)]
 NCH = len(CHUNKS)
 BLOADS = [(0, 1024), (1024, 1024), (2048, 2048)]
 WARM_UPS = 5
-WSPLIT = 320
+WSPLIT = 288
 
 
 def tile_multiheadlatentattention_pa_kernel(tc, x, freq_cis, Wckv, kv_norm_w, Wdkv_bytes, Wdkv_scale, out_0, out_1):
@@ -63,8 +63,8 @@ def tile_multiheadlatentattention_pa_kernel(tc, x, freq_cis, Wckv, kv_norm_w, Wd
         wrs = keep.tile([P, NP, ROPE], U8, name="wrs", align_bytes=64)
         ncod = [keep.tile([P, P], U32, name="ncod%d" % b, align_bytes=64) for b in range(NB)]
         nsc = [keep.tile([P, P], U8, name="nsc%d" % b, align_bytes=64) for b in range(NB)]
-        dc = [keep.tile([P, CHUNKS[c][1]], U32, name="dc%d" % c, align_bytes=64) for c in range(NCH)]
-        ds = [keep.tile([P, CHUNKS[c][1]], U8, name="ds%d" % c, align_bytes=64) for c in range(NCH)]
+        dc = keep.tile([P, KVW], U32, name="dc", align_bytes=64)
+        ds = keep.tile([P, KVW], U8, name="ds", align_bytes=64)
         sumsq = [keep.tile([P, 1], F32, name="sumsq%d" % b) for b in range(NB)]
         rstd = [keep.tile([P, 1], F32, name="rstd%d" % b) for b in range(NB)]
 
@@ -117,8 +117,8 @@ def tile_multiheadlatentattention_pa_kernel(tc, x, freq_cis, Wckv, kv_norm_w, Wd
         nb = {}
         idle = list(range(8))
 
-        def take():
-            i = idle[0]
+        def take(place=0):
+            i = idle[place]
             idle.remove(i)
             return i, psum.tile([P, 512], F32, name="bank%d" % i)
 
@@ -151,10 +151,10 @@ def tile_multiheadlatentattention_pa_kernel(tc, x, freq_cis, Wckv, kv_norm_w, Wd
             copy(eng, dst[:, lo // 4 : hi // 4], src[:, lo // 4 : hi // 4])
 
         def d_pe(c, h):
-            pe_inter(("d", c, h), halves(wide[c], h))
+            pe_inter(("d", c, h), halves(wide_of(c), h))
 
         def d_pe_out(c, h):
-            pe_out(("d", c, h), dg_tile(c)[:, 256 * h : 256 * (h + 1), :].rearrange("p w j -> p (w j)"))
+            pe_out(("d", c, h), dg_of(c)[:, 256 * h : 256 * (h + 1), :].rearrange("p w j -> p (w j)"))
 
         def w_quant(g):
             nc.vector.quantize_mx(out=wc[g][:].bitcast(FP8X4), scales=ws[g][:], in_=wg[g][:].rearrange("p w j -> p (w j)"))
@@ -261,46 +261,48 @@ def tile_multiheadlatentattention_pa_kernel(tc, x, freq_cis, Wckv, kv_norm_w, Wd
         def n_quant(b):
             nc.vector.quantize_mx(out=ncod[b][:].bitcast(FP8X4), scales=nsc[b][:], in_=ng[b][:].rearrange("p r t -> p (r t)"))
 
-        def bytes_of(c):
-            o, n = CHUNKS[c]
+        def bytes_of(c, n):
             for i, (bo, bn) in enumerate(BLOADS):
-                if bo <= o < bo + bn:
-                    return wb[i], o - bo, n
+                if bo <= 512 * c < bo + bn:
+                    return wb[i][:, :, 512 * c - bo : 512 * (c + n) - bo]
 
-        def widen(c, j, eng):
-            t, o, n = bytes_of(c)
-            if c not in wide:
-                wide[c] = work.tile([P, 4, n], BF16, name="wide", bufs=4)
-            w = wide[c][:, j, :]
-            b = t[:, j, o : o + n].bitcast(FP8)
+        def wide_of(c, n=1):
+            if c // 2 not in wide:
+                wide[c // 2] = work.tile([P, 4, 1024], BF16, name="wide", bufs=2)
+            return wide[c // 2][:, :, 512 * (c % 2) : 512 * (c % 2 + n)]
+
+        def dg_of(c, n=1):
+            if c // 2 not in dg:
+                dg[c // 2] = work.tile([P, 1024, 4], BF16, name="dg", bufs=2, align_bytes=64)
+            return dg[c // 2][:, 512 * (c % 2) : 512 * (c % 2 + n), :]
+
+        def widen(c, j, eng, n=1):
+            w = wide_of(c, n)[:, j, :]
+            b = bytes_of(c, n)[:, j, :].bitcast(FP8)
             if eng == "v":
                 nc.vector.tensor_scalar(w, b, scale[:, j : j + 1], None, ALU.mult)
             else:
                 nc.scalar.activation(w, b, ACT.Copy, scale=scale[:, j : j + 1])
 
-        def dg_tile(c):
-            if c not in dg:
-                dg[c] = work.tile([P, CHUNKS[c][1], 4], BF16, name="dg", align_bytes=64)
-            return dg[c]
-
         def d_inter(c):
-            inter("v", dg_tile(c), wide[c], 0, 512)
+            inter("v", dg_of(c), wide_of(c), 0, 512)
 
         def d_half(c, h, eng):
-            inter(eng, dg_tile(c), wide[c], 256 * h, 256 * (h + 1))
+            inter(eng, dg_of(c), wide_of(c), 256 * h, 256 * (h + 1))
 
-        def d_quant(c):
-            nc.vector.quantize_mx(out=dc[c][:].bitcast(FP8X4), scales=ds[c][:], in_=dg[c][:].rearrange("p w j -> p (w j)"))
+        def d_quant(c, n=1):
+            cols = slice(512 * c, 512 * (c + n))
+            nc.vector.quantize_mx(out=dc[:, cols].bitcast(FP8X4), scales=ds[:, cols], in_=dg_of(c, n).rearrange("p w j -> p (w j)"))
 
         def kv_mm(b, c):
-            n = CHUNKS[c][1]
-            tp[("kv", b, c)] = take()
+            cols = slice(512 * c, 512 * (c + 1))
+            tp[("kv", b, c)] = take(-3 if c in (4, 5) else 0)
             nc.tensor.matmul_mx(
-                out=tp[("kv", b, c)][1][:, 0:n],
+                out=tp[("kv", b, c)][1][:],
                 lhsT=ncod[b][:].bitcast(FP8X4),
                 lhsT_scale=nsc[b][:],
-                rhs=dc[c][:].bitcast(FP8X4),
-                rhs_scale=ds[c][:],
+                rhs=dc[:, cols].bitcast(FP8X4),
+                rhs_scale=ds[:, cols],
                 start=True,
                 stop=True,
             )
@@ -371,10 +373,13 @@ def tile_multiheadlatentattention_pa_kernel(tc, x, freq_cis, Wckv, kv_norm_w, Wd
 
         warm_up()
         gains()
-        for c in (0, 1, 3, 2):
+        for c in range(2):
             for j in range(3):
                 widen(c, j, "v")
             widen(c, 3, "s")
+        for j in range(3):
+            widen(2, j, "v", 2)
+        widen(2, 3, "s", 2)
         d_pe(0, 0)
         d_pe(0, 1)
         x_both(0)
@@ -388,9 +393,8 @@ def tile_multiheadlatentattention_pa_kernel(tc, x, freq_cis, Wckv, kv_norm_w, Wd
         x_out(0, 0, "s")
         x_out(0, 1, "s")
         d_pe(2, 1)
-        d_half(3, 0, "v")
         w_inter(0, "v", 0, LORA)
-        d_quant(0)
+        d_half(3, 0, "v")
         w_inter(1, "v", 0, WSPLIT)
         w_inter(1, "s", WSPLIT, LORA)
         d_pe_out(1, 0)
@@ -401,7 +405,7 @@ def tile_multiheadlatentattention_pa_kernel(tc, x, freq_cis, Wckv, kv_norm_w, Wd
         w_inter(2, "v", 0, WSPLIT)
         w_inter(2, "s", WSPLIT, LORA)
         x_out(1, 0, "s")
-        d_quant(1)
+        d_half(3, 1, "v")
         w_inter(3, "v", 0, WSPLIT)
         w_inter(3, "s", WSPLIT, LORA)
         x_out(1, 1, "s")
@@ -425,9 +429,7 @@ def tile_multiheadlatentattention_pa_kernel(tc, x, freq_cis, Wckv, kv_norm_w, Wd
         stats(1)
         x_out(3, 0, "s")
         root(1)
-        d_half(3, 1, "v")
-        d_quant(2)
-        d_quant(3)
+        d_quant(0, 2)
         norm(0)
         n_trans(0)
         x_trans(3, 1)
@@ -435,10 +437,7 @@ def tile_multiheadlatentattention_pa_kernel(tc, x, freq_cis, Wckv, kv_norm_w, Wd
         x_out(3, 1, "s")
         widen(4, 3, "s")
         x_quant(2)
-        widen(4, 0, "v")
-        widen(4, 1, "v")
-        widen(4, 2, "v")
-        widen(5, 0, "v")
+        d_quant(2, 2)
         n_quant(0)
         norm(1)
         lat_all(2)
@@ -451,29 +450,29 @@ def tile_multiheadlatentattention_pa_kernel(tc, x, freq_cis, Wckv, kv_norm_w, Wd
         lat_all(3)
         stats(2)
         kv_out(0, 0, "s")
-        kv_out(0, 1, "v")
         root(2)
+        kv_out(0, 1, "s")
         n_out(1, "s")
         kv_out(0, 2, "s")
         kv_out(0, 3, "s")
-        d_half(4, 0, "v")
-        n_quant(1)
+        widen(4, 0, "v", 2)
+        widen(4, 1, "v")
         norm(2)
-        kv_mm(1, 0)
-        kv_mm(1, 1)
         n_trans(2)
-        kv_mm(1, 2)
-        kv_mm(1, 3)
+        widen(4, 2, "v")
+        n_quant(1)
+        for c in range(4):
+            kv_mm(1, c)
         stats(3)
         kv_out(1, 0, "s")
         root(3)
-        d_half(4, 1, "v")
-        kv_out(1, 1, "v")
-        kv_out(1, 2, "s")
-        kv_out(1, 3, "s")
-        n_out(2, "v")
+        for c in range(1, 4):
+            kv_out(1, c, "s")
         widen(5, 1, "v")
+        n_out(2, "v")
+        widen(5, 2, "v")
         n_quant(2)
+        d_half(4, 0, "v")
         norm(3)
         kv_mm(2, 0)
         kv_mm(2, 1)
@@ -482,49 +481,45 @@ def tile_multiheadlatentattention_pa_kernel(tc, x, freq_cis, Wckv, kv_norm_w, Wd
         kv_mm(2, 3)
         for c in range(4):
             kv_out(2, c, "s")
-        d_quant(4)
-        widen(5, 2, "v")
+        d_half(4, 1, "v")
         widen(5, 3, "v")
         n_out(3, "v")
-        widen(6, 0, "v")
+        d_quant(4)
         n_quant(3)
         for c in range(4):
             kv(3, c)
         d_inter(5)
-        widen(6, 1, "v")
+        widen(6, 0, "v", 2)
         d_quant(5)
-        widen(6, 2, "v")
+        widen(6, 1, "v", 2)
+        widen(6, 2, "v", 2)
         widen(6, 3, "v")
-        widen(7, 0, "v")
+        widen(7, 3, "v")
         d_inter(6)
-        for j in range(1, 4):
-            widen(7, j, "v")
-        d_quant(6)
         d_inter(7)
-        wr_inter(0, "v")
+        d_quant(6)
         d_quant(7)
+        for b in range(NB):
+            kv(b, 4)
+            kv(b, 5)
+        wr_inter(0, "s")
         for g in range(1, NP):
             wr_inter(g, "v")
         neg_sin()
         wr_quant()
         for b in range(NB):
-            kv(b, 4)
-            kv(b, 5)
-        for b in range(NB):
             kv_mm(b, 6)
-        for b in range(2):
             kv_mm(b, 7)
-        for b in range(2):
-            kv_out(b, 6, "s")
-        kv_out(0, 7, "s")
-        kv_out(3, 6, "v")
-        for b in range(2, NB):
-            kv_mm(b, 7)
+            if b == 1:
+                kv_out(0, 6, "s")
+                kv_out(0, 7, "s")
+        kv_out(1, 6, "s")
+        kv_out(1, 7, "s")
+        kv_out(2, 6, "v")
         for b in range(NB):
             kr_passes(b)
-        kv_out(1, 7, "s")
-        kv_out(2, 6, "s")
-        kv_out(2, 7, "s")
-        rope_products()
+        kv_out(2, 7, "v")
+        kv_out(3, 6, "s")
         kv_out(3, 7, "s")
+        rope_products()
         rope_sum()

@@ -6,6 +6,7 @@ from concourse.masks import make_identity
 T, C, LORA, ROPE, KVW = 512, 2048, 512, 128, 4096
 WIDTH = LORA + ROPE
 FLOPS = 2 * T * C * WIDTH + 2 * T * LORA * KVW
+EPS = 1e-6
 
 F32 = mybir.dt.float32
 BF16 = mybir.dt.bfloat16
@@ -17,20 +18,28 @@ ALU = mybir.AluOpType
 ACT = mybir.ActivationFunctionType
 
 P = 128
+PACK = 4
+BANK = 512
+BANKS = 8
 NB = T // P
-NP = C // 512
-CHUNKS = [(512 * c, 512) for c in range(8)]
-NCH = len(CHUNKS)
-BLOADS = [(0, 1024), (1024, 1024), (2048, 2048)]
+NP = C // (P * PACK)
+PAIRS = NB * ROPE // 2
+CHUNK = BANK
+HALF = CHUNK // 2
+BYTE_LOADS = [(0, 2 * CHUNK), (2 * CHUNK, 2 * CHUNK), (4 * CHUNK, 4 * CHUNK)]
+W_SPLIT = 288
 WARM_UPS = 5
-WSPLIT = 288
+PACED_BANK = -3
+V, S = "vector", "scalar"
 
 
 def tile_multiheadlatentattention_pa_kernel(tc, x, freq_cis, Wckv, kv_norm_w, Wdkv_bytes, Wdkv_scale, out_0, out_1):
     nc = tc.nc
-    xv = x.flatten_outer_dims().rearrange("(p b) c -> p b c", b=NB)
-    kvv = out_0.flatten_outer_dims().rearrange("(p b) n -> p b n", b=NB)
-    krv = out_1.flatten_outer_dims().rearrange("(p b) f -> p (b f)", b=NB)
+    x_rows = x.flatten_outer_dims().rearrange("(p b) c -> p b c", b=NB)
+    kv_rows = out_0.flatten_outer_dims().rearrange("(p b) n -> p b n", b=NB)
+    rope_rows = out_1.flatten_outer_dims().rearrange("(p b) f -> p (b f)", b=NB)
+    w_rows = Wckv.rearrange("(g p j) n -> g p j n", p=P, j=PACK)
+    byte_rows = Wdkv_bytes.rearrange("(p j) n -> p j n", j=PACK)
 
     with ExitStack() as ctx:
         keep = ctx.enter_context(tc.tile_pool(name="keep", bufs=1))
@@ -40,51 +49,48 @@ def tile_multiheadlatentattention_pa_kernel(tc, x, freq_cis, Wckv, kv_norm_w, Wd
         ctx.enter_context(tc.manual_schedule())
 
         ident = keep.tile([P, P], F32, name="ident")
-        identb = keep.tile([P, P], BF16, name="identb")
-        gain4 = keep.tile([P, 4], BF16, name="gain4")
+        ident_bf = keep.tile([P, P], BF16, name="ident_bf")
+        gain4 = keep.tile([P, PACK], BF16, name="gain4")
         gain = keep.tile([P, LORA], BF16, name="gain")
         eps = keep.tile([P, 1], F32, name="eps")
-        dummy = keep.tile([P, 1], F32, name="dummy")
-        scale = keep.tile([P, 4], F32, name="scale")
-        fr = keep.tile([P, NB * 64, 2], BF16, name="fr")
-        nsin = keep.tile([P, NB * 64, 1], F32, name="nsin")
-        t1 = keep.tile([P, NB * 64, 2], F32, name="t1")
-        t2 = keep.tile([P, 2, NB * 64], F32, name="t2")
-        ro = keep.tile([P, NB * 64, 2], F32, name="ro")
-        xraw = [keep.tile([P, C], BF16, name="xraw%d" % b) for b in range(NB)]
-        wraw = [keep.tile([P, 4, WIDTH], BF16, name="wraw%d" % g) for g in range(NP)]
-        wb = [keep.tile([P, 4, n], U8, name="wb%d" % i) for i, (o, n) in enumerate(BLOADS)]
-        xc = [keep.tile([P, NP, P], U32, name="xc%d" % b, align_bytes=64) for b in range(NB)]
-        xs = [keep.tile([P, NP, P], U8, name="xs%d" % b, align_bytes=64) for b in range(NB)]
-        wc = [keep.tile([P, LORA], U32, name="wc%d" % g, align_bytes=64) for g in range(NP)]
-        ws = [keep.tile([P, LORA], U8, name="ws%d" % g, align_bytes=64) for g in range(NP)]
-        wrg = keep.tile([P, NP, ROPE, 4], BF16, name="wrg", align_bytes=64)
-        wrc = keep.tile([P, NP, ROPE], U32, name="wrc", align_bytes=64)
-        wrs = keep.tile([P, NP, ROPE], U8, name="wrs", align_bytes=64)
-        ncod = [keep.tile([P, P], U32, name="ncod%d" % b, align_bytes=64) for b in range(NB)]
-        nsc = [keep.tile([P, P], U8, name="nsc%d" % b, align_bytes=64) for b in range(NB)]
-        dc = keep.tile([P, KVW], U32, name="dc", align_bytes=64)
-        ds = keep.tile([P, KVW], U8, name="ds", align_bytes=64)
+        unread = keep.tile([P, 1], F32, name="unread")
+        scale = keep.tile([P, PACK], F32, name="scale")
+        cos_sin = keep.tile([P, PAIRS, 2], BF16, name="cos_sin")
+        neg_sin = keep.tile([P, PAIRS, 1], F32, name="neg_sin")
+        by_cos = keep.tile([P, PAIRS, 2], F32, name="by_cos")
+        by_sin = keep.tile([P, 2, PAIRS], F32, name="by_sin")
+        rotated = keep.tile([P, PAIRS, 2], F32, name="rotated")
+        x_raw = [keep.tile([P, C], BF16, name="x_raw%d" % b) for b in range(NB)]
+        w_raw = [keep.tile([P, PACK, WIDTH], BF16, name="w_raw%d" % g) for g in range(NP)]
+        d_bytes = [keep.tile([P, PACK, n], U8, name="d_bytes%d" % i) for i, (o, n) in enumerate(BYTE_LOADS)]
+        x_codes = [keep.tile([P, NP, P], U32, name="x_codes%d" % b, align_bytes=64) for b in range(NB)]
+        x_scales = [keep.tile([P, NP, P], U8, name="x_scales%d" % b, align_bytes=64) for b in range(NB)]
+        w_codes = [keep.tile([P, LORA], U32, name="w_codes%d" % g, align_bytes=64) for g in range(NP)]
+        w_scales = [keep.tile([P, LORA], U8, name="w_scales%d" % g, align_bytes=64) for g in range(NP)]
+        wr_grouped = keep.tile([P, NP, ROPE, PACK], BF16, name="wr_grouped", align_bytes=64)
+        wr_codes = keep.tile([P, NP, ROPE], U32, name="wr_codes", align_bytes=64)
+        wr_scales = keep.tile([P, NP, ROPE], U8, name="wr_scales", align_bytes=64)
+        n_codes = [keep.tile([P, P], U32, name="n_codes%d" % b, align_bytes=64) for b in range(NB)]
+        n_scales = [keep.tile([P, P], U8, name="n_scales%d" % b, align_bytes=64) for b in range(NB)]
+        d_codes = keep.tile([P, KVW], U32, name="d_codes", align_bytes=64)
+        d_scales = keep.tile([P, KVW], U8, name="d_scales", align_bytes=64)
         sumsq = [keep.tile([P, 1], F32, name="sumsq%d" % b) for b in range(NB)]
         rstd = [keep.tile([P, 1], F32, name="rstd%d" % b) for b in range(NB)]
 
-        wv = Wckv.rearrange("(g p j) n -> g p j n", p=P, j=4)
-        bv = Wdkv_bytes.rearrange("(p j) n -> p j n", j=4)
-
         def load_x(b):
-            nc.sync.dma_start(out=xraw[b][:], in_=xv[:, b, :])
+            nc.sync.dma_start(out=x_raw[b][:], in_=x_rows[:, b, :])
 
         def load_w(g):
-            nc.sync.dma_start(out=wraw[g][:], in_=wv[g])
+            nc.sync.dma_start(out=w_raw[g][:], in_=w_rows[g])
 
-        def load_b(c):
-            o, n = BLOADS[c]
-            nc.sync.dma_start(out=wb[c][:], in_=bv[:, :, o : o + n])
+        def load_bytes(i):
+            o, n = BYTE_LOADS[i]
+            nc.sync.dma_start(out=d_bytes[i][:], in_=byte_rows[:, :, o : o + n])
 
-        nc.scalar.dma_start(out=scale[:], in_=Wdkv_scale.rearrange("(p j) o -> p (j o)", j=4))
-        nc.scalar.dma_start(out=gain4[:], in_=kv_norm_w.rearrange("(p j) -> p j", j=4))
-        load_b(0)
-        load_b(1)
+        nc.scalar.dma_start(out=scale[:], in_=Wdkv_scale.rearrange("(p j) o -> p (j o)", j=PACK))
+        nc.scalar.dma_start(out=gain4[:], in_=kv_norm_w.rearrange("(p j) -> p j", j=PACK))
+        load_bytes(0)
+        load_bytes(1)
         load_x(0)
         load_w(0)
         load_w(1)
@@ -93,433 +99,386 @@ def tile_multiheadlatentattention_pa_kernel(tc, x, freq_cis, Wckv, kv_norm_w, Wd
         load_w(3)
         load_x(2)
         load_x(3)
-        load_b(2)
-        nc.sync.dma_start(out=fr[:].rearrange("p i e -> p (i e)"), in_=freq_cis.rearrange("(p b) i e -> p (b i e)", b=NB))
+        load_bytes(2)
+        nc.sync.dma_start(out=cos_sin[:].rearrange("p i e -> p (i e)"), in_=freq_cis.rearrange("(p b) i e -> p (b i e)", b=NB))
 
         make_identity(nc, ident[:])
-        make_identity(nc, identb[:])
-        nc.vector.memset(eps[:], 1e-6)
-        nc.scalar.activation(dummy[:], eps[:], ACT.Abs_reciprocal_sqrt)
+        make_identity(nc, ident_bf[:])
+        nc.vector.memset(eps[:], EPS)
+        nc.scalar.activation(unread[:], eps[:], ACT.Abs_reciprocal_sqrt)
 
-        def four(t):
-            return t.rearrange("p (c i) t -> p c t i", i=4)
+        free_banks = list(range(BANKS))
+        held = {}
 
-        def by_four(t):
-            return t.rearrange("p t (c i) -> p c t i", i=4)
+        def take(key, place=0):
+            i = free_banks[place]
+            free_banks.remove(i)
+            held[key] = (i, psum.tile([P, BANK], F32, name="bank%d" % i))
+            return held[key][1]
 
-        wg = {}
-        xg = {}
-        wide = {}
-        dg = {}
-        tp = {}
-        lat = {}
-        ng = {}
-        nb = {}
-        idle = list(range(8))
+        def bank(key):
+            return held[key][1]
 
-        def take(place=0):
-            i = idle[place]
-            idle.remove(i)
-            return i, psum.tile([P, 512], F32, name="bank%d" % i)
+        def give(key):
+            free_banks.append(held[key][0])
 
+        staged = {}
 
-        def wg_tile(g):
-            if g not in wg:
-                wg[g] = work.tile([P, LORA, 4], BF16, name="wg", align_bytes=64)
-            return wg[g]
-
-        def inter(eng, dst, src, lo, hi):
-            copy(eng, four(dst[:, lo:hi, :]), by_four(src[:, :, lo:hi]))
-
-        def pe_inter(key, parts):
-            tp[key] = take()
-            bank = tp[key][1][:].bitcast(BF16)
-            for h, rows in enumerate(parts):
-                nc.tensor.matmul(bank[:, 512 * h : 512 * (h + 1)].rearrange("p (n j) -> p j n", j=4), lhsT=identb[:], rhs=rows, start=True, stop=True)
-
-        def pe_out(key, dst):
-            i, t = tp[key]
-            nc.scalar.copy(dst.bitcast(F32), t[:])
-            idle.append(i)
-
-        def halves(src, h):
-            return [src[:, :, 256 * h + 128 * q : 256 * h + 128 * (q + 1)] for q in range(2)]
-
-        def w_inter(g, eng, lo, hi):
-            dst = wg_tile(g)[:].rearrange("p (u c e) t -> p c t u e", u=2, e=2)
-            src = wraw[g][:, :, 0:LORA].rearrange("p t (c u e) -> p c t u e", u=2, e=2)
-            copy(eng, dst[:, lo // 4 : hi // 4], src[:, lo // 4 : hi // 4])
-
-        def d_pe(c, h):
-            pe_inter(("d", c, h), halves(wide_of(c), h))
-
-        def d_pe_out(c, h):
-            pe_out(("d", c, h), dg_of(c)[:, 256 * h : 256 * (h + 1), :].rearrange("p w j -> p (w j)"))
-
-        def w_quant(g):
-            nc.vector.quantize_mx(out=wc[g][:].bitcast(FP8X4), scales=ws[g][:], in_=wg[g][:].rearrange("p w j -> p (w j)"))
-
-        def wr_inter(g, eng):
-            inter(eng, wrg[:, g, :, :], wraw[g][:, :, LORA:WIDTH], 0, ROPE)
-
-        def wr_quant():
-            nc.vector.quantize_mx(
-                out=wrc[:].rearrange("p g w -> p (g w)").bitcast(FP8X4),
-                scales=wrs[:].rearrange("p g w -> p (g w)"),
-                in_=wrg[:].rearrange("p g w j -> p (g w j)"),
-            )
-
-        def x_trans(b, h):
-            words = xraw[b][:].bitcast(F32)
-            tp[(b, h)] = take()
-            t = tp[(b, h)][1][:].rearrange("p (a r) -> p a r", a=4)
-            for gg in range(2):
-                for u in range(2):
-                    nc.tensor.transpose(t[:, 2 * gg + u, :], words[:, 256 * (2 * h + gg) + u : 256 * (2 * h + gg + 1) : 2], ident[:])
+        def stage(pool, key, shape, dtype, **how):
+            if key not in staged:
+                staged[key] = pool.tile(shape, dtype, name=key[0], **how)
+            return staged[key]
 
         def copy(eng, out, in_):
-            if eng == "v":
+            if eng == V:
                 nc.vector.tensor_copy(out, in_)
             else:
                 nc.scalar.copy(out, in_)
 
-        def x_out(b, h, eng):
-            if b not in xg:
-                xg[b] = work.tile([P, NP, P, 4], BF16, name="xg", align_bytes=64)
-            flat = xg[b][:].rearrange("p g r t -> p (g r t)").bitcast(F32)
-            i, t = tp[(b, h)]
-            copy(
-                eng,
-                flat[:, 512 * h : 512 * (h + 1)].rearrange("p (g r u) -> p g r u", g=2, u=2),
-                t[:].rearrange("p (g u r) -> p g r u", g=2, u=2),
+        def interleave(eng, grouped, rows):
+            copy(eng, grouped.rearrange("p (c i) t -> p c t i", i=4), rows.rearrange("p t (c i) -> p c t i", i=4))
+
+        def quantize(codes, scales, grouped):
+            nc.vector.quantize_mx(out=codes.bitcast(FP8X4), scales=scales, in_=grouped)
+
+        def product(out, lhs_codes, lhs_scales, rhs_codes, rhs_scales, start, stop):
+            nc.tensor.matmul_mx(
+                out=out,
+                lhsT=lhs_codes.bitcast(FP8X4),
+                lhsT_scale=lhs_scales,
+                rhs=rhs_codes.bitcast(FP8X4),
+                rhs_scale=rhs_scales,
+                start=start,
+                stop=stop,
             )
-            idle.append(i)
+
+        def warm_up():
+            out = take("warm")[:].rearrange("p (a n) -> p a n", a=BANK // P)
+            for n in range(WARM_UPS):
+                nc.tensor.matmul(out, lhsT=ident_bf[:], rhs=ident_bf[:].unsqueeze(1).to_broadcast([P, BANK // P, P]), start=True, stop=True)
+            give("warm")
+
+        def x_turn(b, h):
+            words = x_raw[b][:].bitcast(F32)
+            out = take(("x", b, h))[:].rearrange("p (a r) -> p a r", a=4)
+            for g in range(2):
+                first = 2 * P * (2 * h + g)
+                for u in range(2):
+                    nc.tensor.transpose(out[:, 2 * g + u, :], words[:, first + u : first + 2 * P : 2], ident[:])
+
+        def x_grouped(b):
+            return stage(work, ("x_grouped", b), [P, NP, P, PACK], BF16, align_bytes=64)[:].rearrange("p g r t -> p (g r t)")
+
+        def x_out(b, h):
+            words = x_grouped(b).bitcast(F32)[:, BANK * h : BANK * (h + 1)]
+            nc.scalar.copy(words.rearrange("p (g r u) -> p g r u", g=2, u=2), bank(("x", b, h))[:].rearrange("p (g u r) -> p g r u", g=2, u=2))
+            give(("x", b, h))
 
         def x_quant(b):
-            nc.vector.quantize_mx(
-                out=xc[b][:].rearrange("p g r -> p (g r)").bitcast(FP8X4),
-                scales=xs[b][:].rearrange("p g r -> p (g r)"),
-                in_=xg[b][:].rearrange("p g r t -> p (g r t)"),
-            )
+            quantize(x_codes[b][:].rearrange("p g r -> p (g r)"), x_scales[b][:].rearrange("p g r -> p (g r)"), x_grouped(b))
 
-        def lat_pass(b, g):
-            if g == 0:
-                lat[b] = take()
-            nc.tensor.matmul_mx(
-                out=lat[b][1][:],
-                lhsT=xc[b][:, g, :].bitcast(FP8X4),
-                lhsT_scale=xs[b][:, g, :],
-                rhs=wc[g][:].bitcast(FP8X4),
-                rhs_scale=ws[g][:],
-                start=(g == 0),
-                stop=(g == NP - 1),
-            )
+        def w_grouped(g):
+            return stage(work, ("w_grouped", g), [P, LORA, PACK], BF16, align_bytes=64)
 
-        def kr_passes(b):
-            if b == 0:
-                tp["kr"] = take()
-            kr = tp["kr"][1][:, ROPE * b : ROPE * (b + 1)]
-            for g in range(NP):
-                nc.tensor.matmul_mx(
-                    out=kr,
-                    lhsT=xc[b][:, g, :].bitcast(FP8X4),
-                    lhsT_scale=xs[b][:, g, :],
-                    rhs=wrc[:, g, :].bitcast(FP8X4),
-                    rhs_scale=wrs[:, g, :],
-                    start=(g == 0),
-                    stop=(g == NP - 1),
-                )
+        def w_inter(g, eng, lo, hi):
+            grouped = w_grouped(g)[:].rearrange("p (u c e) t -> p c t u e", u=2, e=2)
+            rows = w_raw[g][:, :, 0:LORA].rearrange("p t (c u e) -> p c t u e", u=2, e=2)
+            copy(eng, grouped[:, lo // PACK : hi // PACK], rows[:, lo // PACK : hi // PACK])
 
-        def stats(b):
-            sq = work.tile([P, LORA], BF16, name="sq")
-            nc.scalar.activation(sq[:], lat[b][1][:], ACT.Square, accum_out=sumsq[b][:])
+        def w_shared(g):
+            w_inter(g, V, 0, W_SPLIT)
+            w_inter(g, S, W_SPLIT, LORA)
+
+        def w_quant(g):
+            quantize(w_codes[g][:], w_scales[g][:], w_grouped(g)[:].rearrange("p w t -> p (w t)"))
+
+        def lat_passes(b, passes):
+            for g in passes:
+                if g == 0:
+                    take(("lat", b))
+                product(bank(("lat", b))[:], x_codes[b][:, g, :], x_scales[b][:, g, :], w_codes[g][:], w_scales[g][:], g == 0, g == NP - 1)
+
+        def gain_spread():
+            words = gain4[:].bitcast(F32)
+            out = take("gain")
+            for u in range(2):
+                nc.tensor.transpose(out[:, P * u : P * (u + 1)], words[:, u : u + 1].to_broadcast([P, P]), ident[:])
+
+        def gain_out():
+            nc.scalar.copy(gain[:].bitcast(F32), bank("gain")[:, 0 : 2 * P])
+            give("gain")
+
+        def sum_squares(b):
+            squares = work.tile([P, LORA], BF16, name="squares")
+            nc.scalar.activation(squares[:], bank(("lat", b))[:], ACT.Square, accum_out=sumsq[b][:])
 
         def root(b):
             nc.scalar.activation(rstd[b][:], sumsq[b][:], ACT.Abs_reciprocal_sqrt, bias=eps[:], scale=1.0 / LORA)
 
-        def norm(b):
-            nb[b] = work.tile([P, LORA], BF16, name="nb")
-            nc.vector.scalar_tensor_tensor(nb[b][:], lat[b][1][:], rstd[b][:], gain[:], ALU.mult, ALU.mult)
-            idle.append(lat[b][0])
+        def n_rows(b):
+            return stage(work, ("n_rows", b), [P, LORA], BF16)[:]
 
-        def n_trans(b):
-            tp[(b, 2)] = take()
-            words = nb[b][:].bitcast(F32)
+        def norm(b):
+            nc.vector.scalar_tensor_tensor(n_rows(b), bank(("lat", b))[:], rstd[b][:], gain[:], ALU.mult, ALU.mult)
+            give(("lat", b))
+
+        def n_turn(b):
+            words = n_rows(b).bitcast(F32)
+            out = take(("n", b))
             for u in range(2):
-                nc.tensor.transpose(tp[(b, 2)][1][:, P * u : P * (u + 1)], words[:, P * u : P * (u + 1)], ident[:])
+                nc.tensor.transpose(out[:, P * u : P * (u + 1)], words[:, P * u : P * (u + 1)], ident[:])
+
+        def n_grouped(b):
+            return stage(work, ("n_grouped", b), [P, P, PACK], BF16, align_bytes=64)[:].rearrange("p r t -> p (r t)")
 
         def n_out(b, eng):
-            ng[b] = work.tile([P, P, 4], BF16, name="ng", align_bytes=64)
-            i, t = tp[(b, 2)]
-            copy(
-                eng,
-                ng[b][:].rearrange("p r t -> p (r t)").bitcast(F32).rearrange("p (r u) -> p r u", u=2),
-                t[:, 0 : 2 * P].rearrange("p (u r) -> p r u", u=2),
-            )
-            idle.append(i)
+            copy(eng, n_grouped(b).bitcast(F32).rearrange("p (r u) -> p r u", u=2), bank(("n", b))[:, 0 : 2 * P].rearrange("p (u r) -> p r u", u=2))
+            give(("n", b))
 
         def n_quant(b):
-            nc.vector.quantize_mx(out=ncod[b][:].bitcast(FP8X4), scales=nsc[b][:], in_=ng[b][:].rearrange("p r t -> p (r t)"))
+            quantize(n_codes[b][:], n_scales[b][:], n_grouped(b))
 
-        def bytes_of(c, n):
-            for i, (bo, bn) in enumerate(BLOADS):
-                if bo <= 512 * c < bo + bn:
-                    return wb[i][:, :, 512 * c - bo : 512 * (c + n) - bo]
+        def d_raw(c, n):
+            for i, (o, width) in enumerate(BYTE_LOADS):
+                if o <= CHUNK * c < o + width:
+                    return d_bytes[i][:, :, CHUNK * c - o : CHUNK * (c + n) - o]
 
-        def wide_of(c, n=1):
-            if c // 2 not in wide:
-                wide[c // 2] = work.tile([P, 4, 1024], BF16, name="wide", bufs=2)
-            return wide[c // 2][:, :, 512 * (c % 2) : 512 * (c % 2 + n)]
+        def d_wide(c, n=1):
+            pair = stage(work, ("d_wide", c // 2), [P, PACK, 2 * CHUNK], BF16, bufs=2)
+            return pair[:, :, CHUNK * (c % 2) : CHUNK * (c % 2 + n)]
 
-        def dg_of(c, n=1):
-            if c // 2 not in dg:
-                dg[c // 2] = work.tile([P, 1024, 4], BF16, name="dg", bufs=2, align_bytes=64)
-            return dg[c // 2][:, 512 * (c % 2) : 512 * (c % 2 + n), :]
+        def d_grouped(c, n=1):
+            pair = stage(work, ("d_grouped", c // 2), [P, 2 * CHUNK, PACK], BF16, bufs=2, align_bytes=64)
+            return pair[:, CHUNK * (c % 2) : CHUNK * (c % 2 + n), :]
 
-        def widen(c, j, eng, n=1):
-            w = wide_of(c, n)[:, j, :]
-            b = bytes_of(c, n)[:, j, :].bitcast(FP8)
-            if eng == "v":
-                nc.vector.tensor_scalar(w, b, scale[:, j : j + 1], None, ALU.mult)
+        def widen(c, t, eng, n=1):
+            wide = d_wide(c, n)[:, t, :]
+            raw = d_raw(c, n)[:, t, :].bitcast(FP8)
+            if eng == V:
+                nc.vector.tensor_scalar(wide, raw, scale[:, t : t + 1], None, ALU.mult)
             else:
-                nc.scalar.activation(w, b, ACT.Copy, scale=scale[:, j : j + 1])
+                nc.scalar.activation(wide, raw, ACT.Copy, scale=scale[:, t : t + 1])
+
+        def widen_shared(c, n=1):
+            for t in range(PACK - 1):
+                widen(c, t, V, n)
+            widen(c, PACK - 1, S, n)
 
         def d_inter(c):
-            inter("v", dg_of(c), wide_of(c), 0, 512)
+            interleave(V, d_grouped(c), d_wide(c))
 
-        def d_half(c, h, eng):
-            inter(eng, dg_of(c), wide_of(c), 256 * h, 256 * (h + 1))
+        def d_half(c, h):
+            cols = slice(HALF * h, HALF * (h + 1))
+            interleave(V, d_grouped(c)[:, cols, :], d_wide(c)[:, :, cols])
+
+        def d_identity(c, h):
+            out = take(("d", c, h))[:].bitcast(BF16)
+            for q in range(HALF // P):
+                first = HALF * h + P * q
+                nc.tensor.matmul(
+                    out[:, BANK * q : BANK * (q + 1)].rearrange("p (n t) -> p t n", t=PACK),
+                    lhsT=ident_bf[:],
+                    rhs=d_wide(c)[:, :, first : first + P],
+                    start=True,
+                    stop=True,
+                )
+
+        def d_identity_out(c, h):
+            grouped = d_grouped(c)[:, HALF * h : HALF * (h + 1), :].rearrange("p w t -> p (w t)")
+            nc.scalar.copy(grouped.bitcast(F32), bank(("d", c, h))[:])
+            give(("d", c, h))
 
         def d_quant(c, n=1):
-            cols = slice(512 * c, 512 * (c + n))
-            nc.vector.quantize_mx(out=dc[:, cols].bitcast(FP8X4), scales=ds[:, cols], in_=dg_of(c, n).rearrange("p w j -> p (w j)"))
+            cols = slice(CHUNK * c, CHUNK * (c + n))
+            quantize(d_codes[:, cols], d_scales[:, cols], d_grouped(c, n).rearrange("p w t -> p (w t)"))
 
-        def kv_mm(b, c):
-            cols = slice(512 * c, 512 * (c + 1))
-            tp[("kv", b, c)] = take(-3 if c in (4, 5) else 0)
-            nc.tensor.matmul_mx(
-                out=tp[("kv", b, c)][1][:],
-                lhsT=ncod[b][:].bitcast(FP8X4),
-                lhsT_scale=nsc[b][:],
-                rhs=dc[:, cols].bitcast(FP8X4),
-                rhs_scale=ds[:, cols],
-                start=True,
-                stop=True,
-            )
+        def kv_product(b, c, place=0):
+            cols = slice(CHUNK * c, CHUNK * (c + 1))
+            product(take(("kv", b, c), place)[:], n_codes[b][:], n_scales[b][:], d_codes[:, cols], d_scales[:, cols], True, True)
 
-        def kv_out(b, c, eng):
-            i, t = tp[("kv", b, c)]
-            key = ("o", b, c // 2)
-            if key not in tp:
-                tp[key] = outs.tile([P, 1024], F32, name="o")
-            copy(eng, tp[key][:, 512 * (c % 2) : 512 * (c % 2 + 1)], t[:])
-            idle.append(i)
+        def kv_out(b, c, eng=S):
+            pair = stage(outs, ("kv_pair", b, c // 2), [P, 2 * CHUNK], F32)
+            copy(eng, pair[:, CHUNK * (c % 2) : CHUNK * (c % 2 + 1)], bank(("kv", b, c))[:])
+            give(("kv", b, c))
             if c % 2 == 1:
-                m = c // 2
-                nc.sync.dma_start(out=kvv[:, b, 1024 * m : 1024 * (m + 1)], in_=tp[key][:])
+                nc.sync.dma_start(out=kv_rows[:, b, CHUNK * (c - 1) : CHUNK * (c + 1)], in_=pair[:])
 
-        def rope_products():
-            i, t = tp["kr"]
-            k2 = t[:].rearrange("p (i e) -> p i e", e=2)
-            nc.vector.tensor_tensor(t1[:], k2, fr[:, :, 0:1].to_broadcast([P, NB * 64, 2]), ALU.mult)
-            nc.vector.tensor_tensor(t2[:, 0, :].unsqueeze(2), k2[:, :, 1:2], nsin[:], ALU.mult)
-            nc.vector.tensor_tensor(t2[:, 1, :].unsqueeze(2), k2[:, :, 0:1], fr[:, :, 1:2], ALU.mult)
-            idle.append(i)
+        def kv(b, c, place=0):
+            kv_product(b, c, place)
+            kv_out(b, c)
 
-        def rope_sum():
-            nc.vector.tensor_tensor(ro[:], t1[:], t2[:].rearrange("p e i -> p i e"), ALU.add)
-            nc.sync.dma_start(out=krv, in_=ro[:].rearrange("p i e -> p (i e)"))
+        def wr_inter(g, eng):
+            interleave(eng, wr_grouped[:, g, :, :], w_raw[g][:, :, LORA:WIDTH])
 
-        def warm_up():
-            i, t = take()
-            for n in range(WARM_UPS):
-                nc.tensor.matmul(t[:].rearrange("p (a n) -> p a n", a=4), lhsT=identb[:], rhs=identb[:].unsqueeze(1).to_broadcast([P, 4, P]), start=True, stop=True)
-            idle.append(i)
+        def wr_quant():
+            quantize(wr_codes[:].rearrange("p g w -> p (g w)"), wr_scales[:].rearrange("p g w -> p (g w)"), wr_grouped[:].rearrange("p g w t -> p (g w t)"))
 
-        def gains():
-            tp["gain"] = take()
-            words = gain4[:].bitcast(F32)
-            for u in range(2):
-                nc.tensor.transpose(tp["gain"][1][:, P * u : P * (u + 1)], words[:, u : u + 1].to_broadcast([P, P]), ident[:])
+        def kr_products():
+            out = take("kr")
+            for b in range(NB):
+                for g in range(NP):
+                    product(out[:, ROPE * b : ROPE * (b + 1)], x_codes[b][:, g, :], x_scales[b][:, g, :], wr_codes[:, g, :], wr_scales[:, g, :], g == 0, g == NP - 1)
 
-        def gain_out():
-            i, t = tp["gain"]
-            nc.scalar.copy(gain[:].bitcast(F32), t[:, 0 : 2 * P])
-            idle.append(i)
+        def negate_sin():
+            nc.vector.tensor_scalar(neg_sin[:], cos_sin[:, :, 1:2], -1.0, None, ALU.mult)
 
-        def neg_sin():
-            nc.vector.tensor_scalar(nsin[:], fr[:, :, 1:2], -1.0, None, ALU.mult)
+        def rotate():
+            kr = bank("kr")[:].rearrange("p (i e) -> p i e", e=2)
+            nc.vector.tensor_tensor(by_cos[:], kr, cos_sin[:, :, 0:1].to_broadcast([P, PAIRS, 2]), ALU.mult)
+            nc.vector.tensor_tensor(by_sin[:, 0, :].unsqueeze(2), kr[:, :, 1:2], neg_sin[:], ALU.mult)
+            nc.vector.tensor_tensor(by_sin[:, 1, :].unsqueeze(2), kr[:, :, 0:1], cos_sin[:, :, 1:2], ALU.mult)
+            nc.vector.tensor_tensor(rotated[:], by_cos[:], by_sin[:].rearrange("p e i -> p i e"), ALU.add)
+            nc.sync.dma_start(out=rope_rows, in_=rotated[:].rearrange("p i e -> p (i e)"))
 
-        def x_turn(b):
-            for h in range(2):
-                x_trans(b, h)
-                x_out(b, h, "s")
-
-        def x_both(b):
-            for h in range(2):
-                x_trans(b, h)
-
-        def lat_all(b):
-            for g in range(NP):
-                lat_pass(b, g)
-
-        def widen_all(c):
-            for j in range(4):
-                widen(c, j, "v")
-
-        def kv(b, c, eng="s"):
-            kv_mm(b, c)
-            kv_out(b, c, eng)
 
         warm_up()
-        gains()
-        for c in range(2):
-            for j in range(3):
-                widen(c, j, "v")
-            widen(c, 3, "s")
-        for j in range(3):
-            widen(2, j, "v", 2)
-        widen(2, 3, "s", 2)
-        d_pe(0, 0)
-        d_pe(0, 1)
-        x_both(0)
-        d_pe(1, 0)
-        d_pe(1, 1)
-        d_pe_out(0, 0)
+        gain_spread()
+        widen_shared(0)
+        widen_shared(1)
+        widen_shared(2, 2)
+        d_identity(0, 0)
+        d_identity(0, 1)
+        x_turn(0, 0)
+        x_turn(0, 1)
+        d_identity(1, 0)
+        d_identity(1, 1)
+        d_identity_out(0, 0)
         gain_out()
-        d_pe_out(0, 1)
-        x_both(1)
-        d_pe(2, 0)
-        x_out(0, 0, "s")
-        x_out(0, 1, "s")
-        d_pe(2, 1)
-        w_inter(0, "v", 0, LORA)
-        d_half(3, 0, "v")
-        w_inter(1, "v", 0, WSPLIT)
-        w_inter(1, "s", WSPLIT, LORA)
-        d_pe_out(1, 0)
-        d_pe_out(1, 1)
+        d_identity_out(0, 1)
+        x_turn(1, 0)
+        x_turn(1, 1)
+        d_identity(2, 0)
+        x_out(0, 0)
+        x_out(0, 1)
+        d_identity(2, 1)
+
+        d_half(3, 0)
+        w_inter(0, V, 0, LORA)
+        w_shared(1)
+        d_identity_out(1, 0)
+        d_identity_out(1, 1)
         w_quant(0)
         x_quant(0)
         w_quant(1)
-        w_inter(2, "v", 0, WSPLIT)
-        w_inter(2, "s", WSPLIT, LORA)
-        x_out(1, 0, "s")
-        d_half(3, 1, "v")
-        w_inter(3, "v", 0, WSPLIT)
-        w_inter(3, "s", WSPLIT, LORA)
-        x_out(1, 1, "s")
-        d_pe_out(2, 0)
-        d_pe_out(2, 1)
+        w_shared(2)
+        x_out(1, 0)
+        d_half(3, 1)
+        w_shared(3)
+        x_out(1, 1)
+        d_identity_out(2, 0)
+        d_identity_out(2, 1)
         w_quant(2)
         w_quant(3)
         x_quant(1)
-        lat_pass(0, 0)
-        lat_pass(0, 1)
-        x_trans(2, 0)
-        lat_pass(0, 2)
-        lat_pass(0, 3)
-        x_trans(2, 1)
-        lat_all(1)
-        x_trans(3, 0)
-        x_out(2, 0, "s")
-        stats(0)
+
+        lat_passes(0, (0, 1))
+        x_turn(2, 0)
+        lat_passes(0, (2, 3))
+        x_turn(2, 1)
+        lat_passes(1, range(NP))
+        x_turn(3, 0)
+        x_out(2, 0)
+        sum_squares(0)
         root(0)
-        x_out(2, 1, "s")
-        stats(1)
-        x_out(3, 0, "s")
+        x_out(2, 1)
+        sum_squares(1)
+        x_out(3, 0)
         root(1)
         d_quant(0, 2)
+        d_quant(2)
         norm(0)
-        n_trans(0)
-        x_trans(3, 1)
-        n_out(0, "s")
-        x_out(3, 1, "s")
-        widen(4, 3, "s")
+        n_turn(0)
+        x_turn(3, 1)
+        n_out(0, S)
+        x_out(3, 1)
+        widen(4, 3, S)
         x_quant(2)
-        d_quant(2, 2)
+        d_quant(3)
+        widen(4, 0, V, 2)
         n_quant(0)
         norm(1)
-        lat_all(2)
-        kv_mm(0, 0)
-        kv_mm(0, 1)
-        n_trans(1)
-        kv_mm(0, 2)
-        kv_mm(0, 3)
+
+        lat_passes(2, range(NP))
+        kv_product(0, 0)
+        kv_product(0, 1)
+        n_turn(1)
+        kv_product(0, 2)
+        kv_product(0, 3)
         x_quant(3)
-        lat_all(3)
-        stats(2)
-        kv_out(0, 0, "s")
+        lat_passes(3, range(NP))
+        sum_squares(2)
+        kv_out(0, 0)
         root(2)
-        kv_out(0, 1, "s")
-        n_out(1, "s")
-        kv_out(0, 2, "s")
-        kv_out(0, 3, "s")
-        widen(4, 0, "v", 2)
-        widen(4, 1, "v")
+        kv_out(0, 1, V)
+        n_out(1, S)
+        kv_out(0, 2)
+        kv_out(0, 3)
+        widen(4, 1, V)
         norm(2)
-        n_trans(2)
-        widen(4, 2, "v")
+        n_turn(2)
+        widen(4, 2, V)
         n_quant(1)
         for c in range(4):
-            kv_mm(1, c)
-        stats(3)
-        kv_out(1, 0, "s")
+            kv_product(1, c)
+        sum_squares(3)
+        kv_out(1, 0)
         root(3)
         for c in range(1, 4):
-            kv_out(1, c, "s")
-        widen(5, 1, "v")
-        n_out(2, "v")
-        widen(5, 2, "v")
+            kv_out(1, c)
+        widen(5, 1, V)
+        n_out(2, V)
+        widen(5, 2, V)
         n_quant(2)
-        d_half(4, 0, "v")
+        d_half(4, 0)
         norm(3)
-        kv_mm(2, 0)
-        kv_mm(2, 1)
-        n_trans(3)
-        kv_mm(2, 2)
-        kv_mm(2, 3)
+        kv_product(2, 0)
+        kv_product(2, 1)
+        n_turn(3)
+        kv_product(2, 2)
+        kv_product(2, 3)
         for c in range(4):
-            kv_out(2, c, "s")
-        d_half(4, 1, "v")
-        widen(5, 3, "v")
-        n_out(3, "v")
+            kv_out(2, c)
+        d_half(4, 1)
+        widen(5, 3, V)
+        n_out(3, V)
         d_quant(4)
         n_quant(3)
         for c in range(4):
             kv(3, c)
+
         d_inter(5)
-        widen(6, 0, "v", 2)
+        widen(6, 0, V, 2)
         d_quant(5)
-        widen(6, 1, "v", 2)
-        widen(6, 2, "v", 2)
-        widen(6, 3, "v")
-        widen(7, 3, "v")
+        widen(6, 1, V, 2)
+        widen(6, 2, V, 2)
+        widen(6, 3, V)
+        widen(7, 3, V)
         d_inter(6)
         d_inter(7)
         d_quant(6)
         d_quant(7)
         for b in range(NB):
-            kv(b, 4)
-            kv(b, 5)
-        wr_inter(0, "s")
+            kv(b, 4, PACED_BANK)
+            kv(b, 5, PACED_BANK)
+
+        wr_inter(0, S)
         for g in range(1, NP):
-            wr_inter(g, "v")
-        neg_sin()
+            wr_inter(g, V)
+        negate_sin()
         wr_quant()
-        for b in range(NB):
-            kv_mm(b, 6)
-            kv_mm(b, 7)
-            if b == 1:
-                kv_out(0, 6, "s")
-                kv_out(0, 7, "s")
-        kv_out(1, 6, "s")
-        kv_out(1, 7, "s")
-        kv_out(2, 6, "v")
-        for b in range(NB):
-            kr_passes(b)
-        kv_out(2, 7, "v")
-        kv_out(3, 6, "s")
-        kv_out(3, 7, "s")
-        rope_products()
-        rope_sum()
+        for b in range(2):
+            kv_product(b, 6)
+            kv_product(b, 7)
+        kv_out(0, 6)
+        kv_out(0, 7)
+        for b in range(2, NB):
+            kv_product(b, 6)
+            kv_product(b, 7)
+        kv_out(1, 6)
+        kv_out(1, 7)
+        kv_out(2, 6, V)
+        kr_products()
+        kv_out(2, 7, V)
+        kv_out(3, 6)
+        kv_out(3, 7)
+        rotate()

@@ -26,7 +26,8 @@ NP = C // (P * PACK)
 PAIRS = NB * ROPE // 2
 CHUNK = BANK
 HALF = CHUNK // 2
-BYTE_LOADS = [(0, 2 * CHUNK), (2 * CHUNK, 2 * CHUNK), (4 * CHUNK, 4 * CHUNK)]
+LATE = 4
+STORES = [(0, 2), (2, 2), (4, 2), (6, 1), (7, 1)]
 W_SPLIT = 288
 WARM_UPS = 5
 PACED_BANK = -3
@@ -56,13 +57,13 @@ def tile_multiheadlatentattention_pa_kernel(tc, x, freq_cis, Wckv, kv_norm_w, Wd
         unread = keep.tile([P, 1], F32, name="unread")
         scale = keep.tile([P, PACK], F32, name="scale")
         cos_sin = keep.tile([P, PAIRS, 2], BF16, name="cos_sin")
-        neg_sin = keep.tile([P, PAIRS, 1], F32, name="neg_sin")
         by_cos = keep.tile([P, PAIRS, 2], F32, name="by_cos")
         by_sin = keep.tile([P, 2, PAIRS], F32, name="by_sin")
         rotated = keep.tile([P, PAIRS, 2], F32, name="rotated")
         x_raw = [keep.tile([P, C], BF16, name="x_raw%d" % b) for b in range(NB)]
         w_raw = [keep.tile([P, PACK, WIDTH], BF16, name="w_raw%d" % g) for g in range(NP)]
-        d_bytes = [keep.tile([P, PACK, n], U8, name="d_bytes%d" % i) for i, (o, n) in enumerate(BYTE_LOADS)]
+        d_early = [[keep.tile([P, 2 * CHUNK], U8, name="d_early%d_%d" % (j, t)) for t in range(PACK)] for j in range(LATE // 2)]
+        d_late = keep.tile([P, PACK, KVW - LATE * CHUNK], U8, name="d_late")
         x_codes = [keep.tile([P, NP, P], U32, name="x_codes%d" % b, align_bytes=64) for b in range(NB)]
         x_scales = [keep.tile([P, NP, P], U8, name="x_scales%d" % b, align_bytes=64) for b in range(NB)]
         w_codes = [keep.tile([P, LORA], U32, name="w_codes%d" % g, align_bytes=64) for g in range(NP)]
@@ -83,23 +84,21 @@ def tile_multiheadlatentattention_pa_kernel(tc, x, freq_cis, Wckv, kv_norm_w, Wd
         def load_w(g):
             nc.sync.dma_start(out=w_raw[g][:], in_=w_rows[g])
 
-        def load_bytes(i):
-            o, n = BYTE_LOADS[i]
-            nc.sync.dma_start(out=d_bytes[i][:], in_=byte_rows[:, :, o : o + n])
+        def load_early(j):
+            for t in range(PACK):
+                nc.sync.dma_start(out=d_early[j][t][:], in_=byte_rows[:, t, 2 * CHUNK * j : 2 * CHUNK * (j + 1)])
 
         nc.scalar.dma_start(out=scale[:], in_=Wdkv_scale.rearrange("(p j) o -> p (j o)", j=PACK))
         nc.scalar.dma_start(out=gain4[:], in_=kv_norm_w.rearrange("(p j) -> p j", j=PACK))
-        load_bytes(0)
-        load_bytes(1)
+        load_early(0)
         load_x(0)
-        load_w(0)
-        load_w(1)
+        load_early(1)
+        for g in range(NP):
+            load_w(g)
         load_x(1)
-        load_w(2)
-        load_w(3)
         load_x(2)
         load_x(3)
-        load_bytes(2)
+        nc.sync.dma_start(out=d_late[:], in_=byte_rows[:, :, LATE * CHUNK : KVW])
         nc.sync.dma_start(out=cos_sin[:].rearrange("p i e -> p (i e)"), in_=freq_cis.rearrange("(p b) i e -> p (b i e)", b=NB))
 
         make_identity(nc, ident[:])
@@ -185,9 +184,23 @@ def tile_multiheadlatentattention_pa_kernel(tc, x, freq_cis, Wckv, kv_norm_w, Wd
             rows = w_raw[g][:, :, 0:LORA].rearrange("p t (c u e) -> p c t u e", u=2, e=2)
             copy(eng, grouped[:, lo // PACK : hi // PACK], rows[:, lo // PACK : hi // PACK])
 
-        def w_shared(g):
-            w_inter(g, V, 0, W_SPLIT)
-            w_inter(g, S, W_SPLIT, LORA)
+        def w_shared(g, split=W_SPLIT):
+            w_inter(g, V, 0, split)
+            w_inter(g, S, split, LORA)
+
+        def by_identity(out, rows):
+            nc.tensor.matmul(out.rearrange("p (n t) -> p t n", t=PACK), lhsT=ident_bf[:], rhs=rows, start=True, stop=True)
+
+        def w_identity(g, lo, hi):
+            out = take(("w", g, lo))[:].bitcast(BF16)
+            for q in range((hi - lo) // P):
+                by_identity(out[:, BANK * q : BANK * (q + 1)], w_raw[g][:, :, lo + P * q : lo + P * (q + 1)])
+
+        def w_identity_out(g, lo, hi):
+            words = w_grouped(g)[:].rearrange("p w t -> p (w t)").bitcast(F32).rearrange("p (u c x) -> p u c x", u=2, x=PACK)
+            made = bank(("w", g, lo))[:, 0 : 2 * (hi - lo)].rearrange("p (c u x) -> p u c x", u=2, x=PACK)
+            nc.scalar.copy(words[:, :, lo // PACK : hi // PACK, :], made)
+            give(("w", g, lo))
 
         def w_quant(g):
             quantize(w_codes[g][:], w_scales[g][:], w_grouped(g)[:].rearrange("p w t -> p (w t)"))
@@ -238,10 +251,10 @@ def tile_multiheadlatentattention_pa_kernel(tc, x, freq_cis, Wckv, kv_norm_w, Wd
         def n_quant(b):
             quantize(n_codes[b][:], n_scales[b][:], n_grouped(b))
 
-        def d_raw(c, n):
-            for i, (o, width) in enumerate(BYTE_LOADS):
-                if o <= CHUNK * c < o + width:
-                    return d_bytes[i][:, :, CHUNK * c - o : CHUNK * (c + n) - o]
+        def d_raw(c, t, n):
+            if c < LATE:
+                return d_early[c // 2][t][:, CHUNK * (c % 2) : CHUNK * (c % 2 + n)]
+            return d_late[:, t, CHUNK * (c - LATE) : CHUNK * (c - LATE + n)]
 
         def d_wide(c, n=1):
             pair = stage(work, ("d_wide", c // 2), [P, PACK, 2 * CHUNK], BF16, bufs=2)
@@ -253,7 +266,7 @@ def tile_multiheadlatentattention_pa_kernel(tc, x, freq_cis, Wckv, kv_norm_w, Wd
 
         def widen(c, t, eng, n=1):
             wide = d_wide(c, n)[:, t, :]
-            raw = d_raw(c, n)[:, t, :].bitcast(FP8)
+            raw = d_raw(c, t, n).bitcast(FP8)
             if eng == V:
                 nc.vector.tensor_scalar(wide, raw, scale[:, t : t + 1], None, ALU.mult)
             else:
@@ -267,21 +280,17 @@ def tile_multiheadlatentattention_pa_kernel(tc, x, freq_cis, Wckv, kv_norm_w, Wd
         def d_inter(c):
             interleave(V, d_grouped(c), d_wide(c))
 
-        def d_half(c, h):
+        def d_half(c, h, eng=V):
             cols = slice(HALF * h, HALF * (h + 1))
-            interleave(V, d_grouped(c)[:, cols, :], d_wide(c)[:, :, cols])
+            interleave(eng, d_grouped(c)[:, cols, :], d_wide(c)[:, :, cols])
 
-        def d_identity(c, h):
-            out = take(("d", c, h))[:].bitcast(BF16)
-            for q in range(HALF // P):
+        def d_identity(c, h, quarters=(0, 1)):
+            if 0 in quarters:
+                take(("d", c, h))
+            out = bank(("d", c, h))[:].bitcast(BF16)
+            for q in quarters:
                 first = HALF * h + P * q
-                nc.tensor.matmul(
-                    out[:, BANK * q : BANK * (q + 1)].rearrange("p (n t) -> p t n", t=PACK),
-                    lhsT=ident_bf[:],
-                    rhs=d_wide(c)[:, :, first : first + P],
-                    start=True,
-                    stop=True,
-                )
+                by_identity(out[:, BANK * q : BANK * (q + 1)], d_wide(c)[:, :, first : first + P])
 
         def d_identity_out(c, h):
             grouped = d_grouped(c)[:, HALF * h : HALF * (h + 1), :].rearrange("p w t -> p (w t)")
@@ -297,11 +306,12 @@ def tile_multiheadlatentattention_pa_kernel(tc, x, freq_cis, Wckv, kv_norm_w, Wd
             product(take(("kv", b, c), place)[:], n_codes[b][:], n_scales[b][:], d_codes[:, cols], d_scales[:, cols], True, True)
 
         def kv_out(b, c, eng=S):
-            pair = stage(outs, ("kv_pair", b, c // 2), [P, 2 * CHUNK], F32)
-            copy(eng, pair[:, CHUNK * (c % 2) : CHUNK * (c % 2 + 1)], bank(("kv", b, c))[:])
+            first, count = [s for s in STORES if s[0] <= c < s[0] + s[1]][0]
+            rows = stage(outs, ("kv_rows", b, first), [P, count * CHUNK], F32)
+            copy(eng, rows[:, CHUNK * (c - first) : CHUNK * (c - first + 1)], bank(("kv", b, c))[:])
             give(("kv", b, c))
-            if c % 2 == 1:
-                nc.sync.dma_start(out=kv_rows[:, b, CHUNK * (c - 1) : CHUNK * (c + 1)], in_=pair[:])
+            if c == first + count - 1:
+                nc.sync.dma_start(out=kv_rows[:, b, CHUNK * first : CHUNK * (c + 1)], in_=rows[:])
 
         def kv(b, c, place=0):
             kv_product(b, c, place)
@@ -310,126 +320,144 @@ def tile_multiheadlatentattention_pa_kernel(tc, x, freq_cis, Wckv, kv_norm_w, Wd
         def wr_inter(g, eng):
             interleave(eng, wr_grouped[:, g, :, :], w_raw[g][:, :, LORA:WIDTH])
 
+        def wr_identity(g):
+            if g % 2 == 0:
+                take(("wr", g // 2))
+            out = bank(("wr", g // 2))[:].bitcast(BF16)
+            by_identity(out[:, BANK * (g % 2) : BANK * (g % 2 + 1)], w_raw[g][:, :, LORA:WIDTH])
+
+        def wr_identity_out(h):
+            nc.scalar.copy(wr_grouped[:, 2 * h : 2 * h + 2, :, :].rearrange("p g w t -> p (g w t)").bitcast(F32), bank(("wr", h))[:])
+            give(("wr", h))
+
         def wr_quant():
             quantize(wr_codes[:].rearrange("p g w -> p (g w)"), wr_scales[:].rearrange("p g w -> p (g w)"), wr_grouped[:].rearrange("p g w t -> p (g w t)"))
 
-        def kr_products():
-            out = take("kr")
-            for b in range(NB):
-                for g in range(NP):
-                    product(out[:, ROPE * b : ROPE * (b + 1)], x_codes[b][:, g, :], x_scales[b][:, g, :], wr_codes[:, g, :], wr_scales[:, g, :], g == 0, g == NP - 1)
+        def kr_products(b):
+            if b == 0:
+                take("kr")
+            out = bank("kr")
+            for g in range(NP):
+                product(out[:, ROPE * b : ROPE * (b + 1)], x_codes[b][:, g, :], x_scales[b][:, g, :], wr_codes[:, g, :], wr_scales[:, g, :], g == 0, g == NP - 1)
 
-        def negate_sin():
-            nc.vector.tensor_scalar(neg_sin[:], cos_sin[:, :, 1:2], -1.0, None, ALU.mult)
-
-        def rotate():
+        def times_cos():
             kr = bank("kr")[:].rearrange("p (i e) -> p i e", e=2)
             nc.vector.tensor_tensor(by_cos[:], kr, cos_sin[:, :, 0:1].to_broadcast([P, PAIRS, 2]), ALU.mult)
-            nc.vector.tensor_tensor(by_sin[:, 0, :].unsqueeze(2), kr[:, :, 1:2], neg_sin[:], ALU.mult)
+
+        def times_sin():
+            kr = bank("kr")[:].rearrange("p (i e) -> p i e", e=2)
+            nc.vector.scalar_tensor_tensor(by_sin[:, 0, :].unsqueeze(2), kr[:, :, 1:2], -1.0, cos_sin[:, :, 1:2], ALU.mult, ALU.mult)
             nc.vector.tensor_tensor(by_sin[:, 1, :].unsqueeze(2), kr[:, :, 0:1], cos_sin[:, :, 1:2], ALU.mult)
+            give("kr")
+
+        def rotate_sum():
             nc.vector.tensor_tensor(rotated[:], by_cos[:], by_sin[:].rearrange("p e i -> p i e"), ALU.add)
             nc.sync.dma_start(out=rope_rows, in_=rotated[:].rearrange("p i e -> p (i e)"))
 
 
         warm_up()
         gain_spread()
-        widen_shared(0)
-        widen_shared(1)
-        widen_shared(2, 2)
-        d_identity(0, 0)
-        d_identity(0, 1)
-        x_turn(0, 0)
-        x_turn(0, 1)
-        d_identity(1, 0)
-        d_identity(1, 1)
-        d_identity_out(0, 0)
+        widen(0, 0, V, 2)
+        widen(0, 1, S, 2)
+        widen(0, 2, V, 2)
+        widen(0, 3, V, 2)
         gain_out()
-        d_identity_out(0, 1)
-        x_turn(1, 0)
-        x_turn(1, 1)
-        d_identity(2, 0)
+        d_half(1, 0)
+        d_half(1, 1, S)
+        x_turn(0, 0)
+        d_identity(0, 0)
+        x_turn(0, 1)
+        d_identity(0, 1)
         x_out(0, 0)
+        widen(2, 0, V, 2)
+        widen(2, 1, V, 2)
+        widen(2, 2, V, 2)
+        widen(2, 3, V, 2)
+        d_identity_out(0, 0)
         x_out(0, 1)
+        d_identity(2, 0)
         d_identity(2, 1)
-
-        d_half(3, 0)
-        w_inter(0, V, 0, LORA)
-        w_shared(1)
-        d_identity_out(1, 0)
-        d_identity_out(1, 1)
-        w_quant(0)
+        w_shared(0, 384)
+        d_identity_out(0, 1)
+        d_identity(3, 0)
+        d_identity(3, 1)
         x_quant(0)
-        w_quant(1)
-        w_shared(2)
-        x_out(1, 0)
-        d_half(3, 1)
-        w_shared(3)
-        x_out(1, 1)
+        w_shared(1)
         d_identity_out(2, 0)
-        d_identity_out(2, 1)
+        w_quant(0)
+        w_shared(2)
+        w_quant(1)
+        w_shared(3, 320)
         w_quant(2)
         w_quant(3)
-        x_quant(1)
-
         lat_passes(0, (0, 1))
-        x_turn(2, 0)
+        d_identity_out(2, 1)
+        d_identity_out(3, 0)
+        x_turn(1, 0)
+        x_turn(1, 1)
         lat_passes(0, (2, 3))
+        x_out(1, 0)
+        x_out(1, 1)
+        x_turn(2, 0)
         x_turn(2, 1)
-        lat_passes(1, range(NP))
-        x_turn(3, 0)
-        x_out(2, 0)
         sum_squares(0)
+        d_identity_out(3, 1)
         root(0)
+        x_out(2, 0)
         x_out(2, 1)
-        sum_squares(1)
-        x_out(3, 0)
-        root(1)
         d_quant(0, 2)
+        wr_inter(0, V)
+        x_quant(1)
+        x_turn(3, 0)
+        lat_passes(1, range(NP))
         d_quant(2)
         norm(0)
         n_turn(0)
         x_turn(3, 1)
-        n_out(0, S)
-        x_out(3, 1)
-        widen(4, 3, S)
-        x_quant(2)
         d_quant(3)
+        x_quant(2)
+        x_out(3, 0)
+        sum_squares(1)
+        n_out(0, S)
+        root(1)
+        x_out(3, 1)
         widen(4, 0, V, 2)
         n_quant(0)
-        norm(1)
-
         lat_passes(2, range(NP))
         kv_product(0, 0)
         kv_product(0, 1)
+        norm(1)
         n_turn(1)
         kv_product(0, 2)
         kv_product(0, 3)
         x_quant(3)
-        lat_passes(3, range(NP))
+        widen(4, 3, S)
+        wr_inter(1, V)
         sum_squares(2)
         kv_out(0, 0)
         root(2)
         kv_out(0, 1, V)
+        lat_passes(3, range(NP))
         n_out(1, S)
         kv_out(0, 2)
         kv_out(0, 3)
-        widen(4, 1, V)
         norm(2)
-        n_turn(2)
-        widen(4, 2, V)
         n_quant(1)
+        n_turn(2)
         for c in range(4):
             kv_product(1, c)
+        widen(4, 1, V, 2)
+        widen(4, 2, V, 2)
+        widen(5, 3, V)
         sum_squares(3)
         kv_out(1, 0)
         root(3)
-        for c in range(1, 4):
-            kv_out(1, c)
-        widen(5, 1, V)
+        kv_out(1, 1)
+        kv_out(1, 2)
+        kv_out(1, 3)
         n_out(2, V)
-        widen(5, 2, V)
+        wr_inter(2, V)
         n_quant(2)
-        d_half(4, 0)
         norm(3)
         kv_product(2, 0)
         kv_product(2, 1)
@@ -438,47 +466,40 @@ def tile_multiheadlatentattention_pa_kernel(tc, x, freq_cis, Wckv, kv_norm_w, Wd
         kv_product(2, 3)
         for c in range(4):
             kv_out(2, c)
-        d_half(4, 1)
-        widen(5, 3, V)
+        d_half(4, 0)
+        wr_inter(3, V)
         n_out(3, V)
-        d_quant(4)
+        widen(6, 0, V)
         n_quant(3)
         for c in range(4):
             kv(3, c)
-
+        d_half(4, 1)
         d_inter(5)
-        widen(6, 0, V, 2)
+        d_quant(4)
         d_quant(5)
-        widen(6, 1, V, 2)
-        widen(6, 2, V, 2)
-        widen(6, 3, V)
-        widen(7, 3, V)
+
+        for t in range(1, PACK):
+            widen(6, t, V)
+        wr_quant()
         d_inter(6)
-        d_inter(7)
+        widen(7, 0, V)
         d_quant(6)
-        d_quant(7)
+        for t in range(1, PACK):
+            widen(7, t, V)
         for b in range(NB):
             kv(b, 4, PACED_BANK)
             kv(b, 5, PACED_BANK)
-
-        wr_inter(0, S)
-        for g in range(1, NP):
-            wr_inter(g, V)
-        negate_sin()
-        wr_quant()
-        for b in range(2):
-            kv_product(b, 6)
-            kv_product(b, 7)
-        kv_out(0, 6)
-        kv_out(0, 7)
-        for b in range(2, NB):
-            kv_product(b, 6)
-            kv_product(b, 7)
-        kv_out(1, 6)
-        kv_out(1, 7)
-        kv_out(2, 6, V)
-        kr_products()
-        kv_out(2, 7, V)
-        kv_out(3, 6)
-        kv_out(3, 7)
-        rotate()
+        for b in range(NB):
+            kr_products(b)
+            kv(b, 6)
+        d_inter(7)
+        times_cos()
+        d_quant(7)
+        times_sin()
+        kv(0, 7)
+        kv(1, 7)
+        rotate_sum()
+        kv_product(2, 7)
+        kv_product(3, 7)
+        kv_out(2, 7)
+        kv_out(3, 7, V)

@@ -27,10 +27,11 @@ PAIRS = NB * ROPE // 2
 CHUNK = BANK
 HALF = CHUNK // 2
 LATE = 4
-STORES = [(0, 2), (2, 2), (4, 2), (6, 1), (7, 1)]
+STORES = [(b, 1, c, 2) for b in range(NB) for c in (0, 2, 4)] + [(0, 1, 6, 2), (1, 1, 6, 2), (2, 2, 6, 2)]
 W_SPLIT = 288
 WARM_UPS = 5
 PACED_BANK = -3
+LARGE_BUFS, SMALL_BUFS = 1, 10
 V, S = "vector", "scalar"
 
 
@@ -45,7 +46,7 @@ def tile_multiheadlatentattention_pa_kernel(tc, x, freq_cis, Wckv, kv_norm_w, Wd
     with ExitStack() as ctx:
         keep = ctx.enter_context(tc.tile_pool(name="keep", bufs=1))
         work = ctx.enter_context(tc.tile_pool(name="work", bufs=4))
-        outs = ctx.enter_context(tc.tile_pool(name="outs", bufs=10))
+        outs = ctx.enter_context(tc.tile_pool(name="outs", bufs=1))
         psum = ctx.enter_context(tc.psum_pool(name="psum", bufs=1))
         ctx.enter_context(tc.manual_schedule())
 
@@ -62,7 +63,8 @@ def tile_multiheadlatentattention_pa_kernel(tc, x, freq_cis, Wckv, kv_norm_w, Wd
         rotated = keep.tile([P, PAIRS, 2], F32, name="rotated")
         x_raw = [keep.tile([P, C], BF16, name="x_raw%d" % b) for b in range(NB)]
         w_raw = [keep.tile([P, PACK, WIDTH], BF16, name="w_raw%d" % g) for g in range(NP)]
-        d_early = [[keep.tile([P, 2 * CHUNK], U8, name="d_early%d_%d" % (j, t)) for t in range(PACK)] for j in range(LATE // 2)]
+        d_first = [keep.tile([P, 2, 2 * CHUNK], U8, name="d_first%d" % j) for j in range(2)]
+        d_next = keep.tile([P, PACK, 2 * CHUNK], U8, name="d_next")
         d_late = keep.tile([P, PACK, KVW - LATE * CHUNK], U8, name="d_late")
         x_codes = [keep.tile([P, NP, P], U32, name="x_codes%d" % b, align_bytes=64) for b in range(NB)]
         x_scales = [keep.tile([P, NP, P], U8, name="x_scales%d" % b, align_bytes=64) for b in range(NB)]
@@ -84,15 +86,13 @@ def tile_multiheadlatentattention_pa_kernel(tc, x, freq_cis, Wckv, kv_norm_w, Wd
         def load_w(g):
             nc.sync.dma_start(out=w_raw[g][:], in_=w_rows[g])
 
-        def load_early(j):
-            for t in range(PACK):
-                nc.sync.dma_start(out=d_early[j][t][:], in_=byte_rows[:, t, 2 * CHUNK * j : 2 * CHUNK * (j + 1)])
 
         nc.scalar.dma_start(out=scale[:], in_=Wdkv_scale.rearrange("(p j) o -> p (j o)", j=PACK))
         nc.scalar.dma_start(out=gain4[:], in_=kv_norm_w.rearrange("(p j) -> p j", j=PACK))
-        load_early(0)
+        for j in range(2):
+            nc.sync.dma_start(out=d_first[j][:], in_=byte_rows[:, 2 * j : 2 * j + 2, 0 : 2 * CHUNK])
+        nc.sync.dma_start(out=d_next[:], in_=byte_rows[:, :, 2 * CHUNK : LATE * CHUNK])
         load_x(0)
-        load_early(1)
         for g in range(NP):
             load_w(g)
         load_x(1)
@@ -122,6 +122,7 @@ def tile_multiheadlatentattention_pa_kernel(tc, x, freq_cis, Wckv, kv_norm_w, Wd
             free_banks.append(held[key][0])
 
         staged = {}
+        emptied = []
 
         def stage(pool, key, shape, dtype, **how):
             if key not in staged:
@@ -222,7 +223,7 @@ def tile_multiheadlatentattention_pa_kernel(tc, x, freq_cis, Wckv, kv_norm_w, Wd
             give("gain")
 
         def sum_squares(b):
-            squares = work.tile([P, LORA], BF16, name="squares")
+            squares = work.tile([P, LORA], BF16, name="squares", bufs=1)
             nc.scalar.activation(squares[:], bank(("lat", b))[:], ACT.Square, accum_out=sumsq[b][:])
 
         def root(b):
@@ -252,8 +253,10 @@ def tile_multiheadlatentattention_pa_kernel(tc, x, freq_cis, Wckv, kv_norm_w, Wd
             quantize(n_codes[b][:], n_scales[b][:], n_grouped(b))
 
         def d_raw(c, t, n):
+            if c < 2:
+                return d_first[t // 2][:, t % 2, CHUNK * c : CHUNK * (c + n)]
             if c < LATE:
-                return d_early[c // 2][t][:, CHUNK * (c % 2) : CHUNK * (c % 2 + n)]
+                return d_next[:, t, CHUNK * (c - 2) : CHUNK * (c - 2 + n)]
             return d_late[:, t, CHUNK * (c - LATE) : CHUNK * (c - LATE + n)]
 
         def d_wide(c, n=1):
@@ -306,12 +309,14 @@ def tile_multiheadlatentattention_pa_kernel(tc, x, freq_cis, Wckv, kv_norm_w, Wd
             product(take(("kv", b, c), place)[:], n_codes[b][:], n_scales[b][:], d_codes[:, cols], d_scales[:, cols], True, True)
 
         def kv_out(b, c, eng=S):
-            first, count = [s for s in STORES if s[0] <= c < s[0] + s[1]][0]
-            rows = stage(outs, ("kv_rows", b, first), [P, count * CHUNK], F32)
-            copy(eng, rows[:, CHUNK * (c - first) : CHUNK * (c - first + 1)], bank(("kv", b, c))[:])
+            b0, nb, c0, n = [s for s in STORES if s[0] <= b < s[0] + s[1] and s[2] <= c < s[2] + s[3]][0]
+            large = nb * n > 2
+            rows = stage(outs, ("kv_large" if large else "kv_small", b0, c0), [P, nb, n * CHUNK], F32, bufs=LARGE_BUFS if large else SMALL_BUFS)
+            copy(eng, rows[:, b - b0, CHUNK * (c - c0) : CHUNK * (c - c0 + 1)], bank(("kv", b, c))[:])
             give(("kv", b, c))
-            if c == first + count - 1:
-                nc.sync.dma_start(out=kv_rows[:, b, CHUNK * first : CHUNK * (c + 1)], in_=rows[:])
+            emptied.append((b0, c0))
+            if emptied.count((b0, c0)) == nb * n:
+                nc.sync.dma_start(out=kv_rows[:, b0 : b0 + nb, CHUNK * c0 : CHUNK * (c0 + n)], in_=rows[:])
 
         def kv(b, c, place=0):
             kv_product(b, c, place)
@@ -359,31 +364,36 @@ def tile_multiheadlatentattention_pa_kernel(tc, x, freq_cis, Wckv, kv_norm_w, Wd
         gain_spread()
         widen(0, 0, V, 2)
         widen(0, 1, S, 2)
-        widen(0, 2, V, 2)
-        widen(0, 3, V, 2)
+        widen(0, 2, V)
+        widen(0, 3, V)
+        widen(1, 2, V)
+        widen(1, 3, V)
         gain_out()
-        d_half(1, 0)
-        d_half(1, 1, S)
-        x_turn(0, 0)
-        d_identity(0, 0)
-        x_turn(0, 1)
-        d_identity(0, 1)
-        x_out(0, 0)
         widen(2, 0, V, 2)
-        widen(2, 1, V, 2)
-        widen(2, 2, V, 2)
-        widen(2, 3, V, 2)
+        widen(2, 1, S, 2)
+        widen(3, 2, V)
+        widen(2, 2, S)
+        widen(3, 3, V)
+        widen(2, 3, V)
+        d_identity(0, 0)
+        d_identity(0, 1, (0,))
+        x_turn(0, 0)
+        d_identity(0, 1, (1,))
+        x_turn(0, 1)
+        d_identity(1, 0)
+        d_identity(1, 1)
         d_identity_out(0, 0)
+        x_out(0, 0)
+        w_inter(0, S, 416, LORA)
         x_out(0, 1)
+        d_identity_out(0, 1)
         d_identity(2, 0)
         d_identity(2, 1)
-        w_shared(0, 384)
-        d_identity_out(0, 1)
-        d_identity(3, 0)
-        d_identity(3, 1)
-        x_quant(0)
+        d_inter(3)
+        w_inter(0, V, 0, 416)
         w_shared(1)
-        d_identity_out(2, 0)
+        d_identity_out(1, 0)
+        x_quant(0)
         w_quant(0)
         w_shared(2)
         w_quant(1)
@@ -391,8 +401,8 @@ def tile_multiheadlatentattention_pa_kernel(tc, x, freq_cis, Wckv, kv_norm_w, Wd
         w_quant(2)
         w_quant(3)
         lat_passes(0, (0, 1))
-        d_identity_out(2, 1)
-        d_identity_out(3, 0)
+        d_identity_out(1, 1)
+        d_identity_out(2, 0)
         x_turn(1, 0)
         x_turn(1, 1)
         lat_passes(0, (2, 3))
@@ -401,20 +411,19 @@ def tile_multiheadlatentattention_pa_kernel(tc, x, freq_cis, Wckv, kv_norm_w, Wd
         x_turn(2, 0)
         x_turn(2, 1)
         sum_squares(0)
-        d_identity_out(3, 1)
+        d_identity_out(2, 1)
         root(0)
         x_out(2, 0)
         x_out(2, 1)
         d_quant(0, 2)
-        wr_inter(0, V)
         x_quant(1)
         x_turn(3, 0)
         lat_passes(1, range(NP))
-        d_quant(2)
+        d_quant(3)
         norm(0)
         n_turn(0)
         x_turn(3, 1)
-        d_quant(3)
+        d_quant(2)
         x_quant(2)
         x_out(3, 0)
         sum_squares(1)
@@ -432,7 +441,7 @@ def tile_multiheadlatentattention_pa_kernel(tc, x, freq_cis, Wckv, kv_norm_w, Wd
         kv_product(0, 3)
         x_quant(3)
         widen(4, 3, S)
-        wr_inter(1, V)
+        widen(4, 1, V, 2)
         sum_squares(2)
         kv_out(0, 0)
         root(2)
@@ -441,14 +450,16 @@ def tile_multiheadlatentattention_pa_kernel(tc, x, freq_cis, Wckv, kv_norm_w, Wd
         n_out(1, S)
         kv_out(0, 2)
         kv_out(0, 3)
-        norm(2)
+        widen(4, 2, V)
         n_quant(1)
+        norm(2)
+        kv_product(1, 0)
+        kv_product(1, 1)
         n_turn(2)
-        for c in range(4):
-            kv_product(1, c)
-        widen(4, 1, V, 2)
-        widen(4, 2, V, 2)
-        widen(5, 3, V)
+        kv_product(1, 2)
+        kv_product(1, 3)
+        d_half(4, 0)
+        widen(5, 2, V)
         sum_squares(3)
         kv_out(1, 0)
         root(3)
@@ -456,7 +467,7 @@ def tile_multiheadlatentattention_pa_kernel(tc, x, freq_cis, Wckv, kv_norm_w, Wd
         kv_out(1, 2)
         kv_out(1, 3)
         n_out(2, V)
-        wr_inter(2, V)
+        widen(5, 3, V)
         n_quant(2)
         norm(3)
         kv_product(2, 0)
@@ -466,40 +477,47 @@ def tile_multiheadlatentattention_pa_kernel(tc, x, freq_cis, Wckv, kv_norm_w, Wd
         kv_product(2, 3)
         for c in range(4):
             kv_out(2, c)
-        d_half(4, 0)
-        wr_inter(3, V)
+        d_half(4, 1)
+        widen(7, 0, V)
         n_out(3, V)
         widen(6, 0, V)
         n_quant(3)
         for c in range(4):
             kv(3, c)
-        d_half(4, 1)
         d_inter(5)
         d_quant(4)
         d_quant(5)
-
-        for t in range(1, PACK):
-            widen(6, t, V)
-        wr_quant()
+        widen(6, 1, V, 2)
+        widen(6, 2, V, 2)
+        widen(6, 3, V)
+        widen(7, 3, V)
         d_inter(6)
-        widen(7, 0, V)
+        d_inter(7)
         d_quant(6)
-        for t in range(1, PACK):
-            widen(7, t, V)
+        d_quant(7)
         for b in range(NB):
             kv(b, 4, PACED_BANK)
             kv(b, 5, PACED_BANK)
+        wr_inter(0, S)
+        for g in range(1, NP):
+            wr_inter(g, V)
+        wr_quant()
+        for b in range(2):
+            kv_product(b, 6)
+            kv_product(b, 7)
+        kv_out(0, 6)
+        kv_out(0, 7)
+        for b in range(2, NB):
+            kv_product(b, 6)
+            kv_product(b, 7)
+        kv_out(1, 6)
+        kv_out(1, 7)
+        kv_out(2, 6, V)
         for b in range(NB):
             kr_products(b)
-            kv(b, 6)
-        d_inter(7)
+        kv_out(2, 7, V)
+        kv_out(3, 6)
+        kv_out(3, 7)
         times_cos()
-        d_quant(7)
         times_sin()
-        kv(0, 7)
-        kv(1, 7)
         rotate_sum()
-        kv_product(2, 7)
-        kv_product(3, 7)
-        kv_out(2, 7)
-        kv_out(3, 7, V)

@@ -32,6 +32,7 @@ W_SPLIT = 288
 WARM_UPS = 5
 PACED_BANK = -3
 LARGE_BUFS, SMALL_BUFS = 1, 10
+DMA_ALIGN = 256
 V, S = "vector", "scalar"
 
 
@@ -57,15 +58,15 @@ def tile_multiheadlatentattention_pa_kernel(tc, x, freq_cis, Wckv, kv_norm_w, Wd
         eps = keep.tile([P, 1], F32, name="eps")
         unread = keep.tile([P, 1], F32, name="unread")
         scale = keep.tile([P, PACK], F32, name="scale")
-        cos_sin = keep.tile([P, PAIRS, 2], BF16, name="cos_sin")
+        cos_sin = keep.tile([P, PAIRS, 2], BF16, name="cos_sin", align_bytes=DMA_ALIGN)
         by_cos = keep.tile([P, PAIRS, 2], F32, name="by_cos")
         by_sin = keep.tile([P, 2, PAIRS], F32, name="by_sin")
-        rotated = keep.tile([P, PAIRS, 2], F32, name="rotated")
-        x_raw = [keep.tile([P, C], BF16, name="x_raw%d" % b) for b in range(NB)]
-        w_raw = [keep.tile([P, PACK, WIDTH], BF16, name="w_raw%d" % g) for g in range(NP)]
-        d_first = [keep.tile([P, 2, 2 * CHUNK], U8, name="d_first%d" % j) for j in range(2)]
-        d_next = keep.tile([P, PACK, 2 * CHUNK], U8, name="d_next")
-        d_late = keep.tile([P, PACK, KVW - LATE * CHUNK], U8, name="d_late")
+        rotated = keep.tile([P, PAIRS, 2], F32, name="rotated", align_bytes=DMA_ALIGN)
+        x_raw = [keep.tile([P, C], BF16, name="x_raw%d" % b, align_bytes=DMA_ALIGN) for b in range(NB)]
+        w_raw = [keep.tile([P, PACK, WIDTH], BF16, name="w_raw%d" % g, align_bytes=DMA_ALIGN) for g in range(NP)]
+        d_first = [keep.tile([P, 2, 2 * CHUNK], U8, name="d_first%d" % j, align_bytes=DMA_ALIGN) for j in range(2)]
+        d_next = keep.tile([P, PACK, 2 * CHUNK], U8, name="d_next", align_bytes=DMA_ALIGN)
+        d_late = keep.tile([P, PACK, KVW - LATE * CHUNK], U8, name="d_late", align_bytes=DMA_ALIGN)
         x_codes = [keep.tile([P, NP, P], U32, name="x_codes%d" % b, align_bytes=64) for b in range(NB)]
         x_scales = [keep.tile([P, NP, P], U8, name="x_scales%d" % b, align_bytes=64) for b in range(NB)]
         w_codes = [keep.tile([P, LORA], U32, name="w_codes%d" % g, align_bytes=64) for g in range(NP)]
@@ -311,7 +312,7 @@ def tile_multiheadlatentattention_pa_kernel(tc, x, freq_cis, Wckv, kv_norm_w, Wd
         def kv_out(b, c, eng=S):
             b0, nb, c0, n = [s for s in STORES if s[0] <= b < s[0] + s[1] and s[2] <= c < s[2] + s[3]][0]
             large = nb * n > 2
-            rows = stage(outs, ("kv_large" if large else "kv_small", b0, c0), [P, nb, n * CHUNK], F32, bufs=LARGE_BUFS if large else SMALL_BUFS)
+            rows = stage(outs, ("kv_large" if large else "kv_small", b0, c0), [P, nb, n * CHUNK], F32, bufs=LARGE_BUFS if large else SMALL_BUFS, align_bytes=DMA_ALIGN)
             copy(eng, rows[:, b - b0, CHUNK * (c - c0) : CHUNK * (c - c0 + 1)], bank(("kv", b, c))[:])
             give(("kv", b, c))
             emptied.append((b0, c0))

@@ -26,9 +26,10 @@ NP = C // (P * PACK)
 PAIRS = NB * ROPE // 2
 CHUNK = BANK
 HALF = CHUNK // 2
-LATE = 4
+FIRST, LATE = 2, 4
 STORES = [(b, 1, c, 2) for b in range(NB) for c in (0, 2, 4)] + [(0, 1, 6, 2), (1, 1, 6, 2), (2, 2, 6, 2)]
-W_SPLIT = 288
+W_SPLIT = (416, 288, 288, 320)
+RUN = 2
 WARM_UPS = 5
 PACED_BANK = -3
 LARGE_BUFS, SMALL_BUFS = 1, 10
@@ -64,8 +65,8 @@ def tile_multiheadlatentattention_pa_kernel(tc, x, freq_cis, Wckv, kv_norm_w, Wd
         rotated = keep.tile([P, PAIRS, 2], F32, name="rotated", align_bytes=DMA_ALIGN)
         x_raw = [keep.tile([P, C], BF16, name="x_raw%d" % b, align_bytes=DMA_ALIGN) for b in range(NB)]
         w_raw = [keep.tile([P, PACK, WIDTH], BF16, name="w_raw%d" % g, align_bytes=DMA_ALIGN) for g in range(NP)]
-        d_first = [keep.tile([P, 2, 2 * CHUNK], U8, name="d_first%d" % j, align_bytes=DMA_ALIGN) for j in range(2)]
-        d_next = keep.tile([P, PACK, 2 * CHUNK], U8, name="d_next", align_bytes=DMA_ALIGN)
+        d_first = [keep.tile([P, 2, FIRST * CHUNK], U8, name="d_first%d" % j, align_bytes=DMA_ALIGN) for j in range(2)]
+        d_next = keep.tile([P, PACK, (LATE - FIRST) * CHUNK], U8, name="d_next", align_bytes=DMA_ALIGN)
         d_late = keep.tile([P, PACK, KVW - LATE * CHUNK], U8, name="d_late", align_bytes=DMA_ALIGN)
         x_codes = [keep.tile([P, NP, P], U32, name="x_codes%d" % b, align_bytes=64) for b in range(NB)]
         x_scales = [keep.tile([P, NP, P], U8, name="x_scales%d" % b, align_bytes=64) for b in range(NB)]
@@ -87,18 +88,16 @@ def tile_multiheadlatentattention_pa_kernel(tc, x, freq_cis, Wckv, kv_norm_w, Wd
         def load_w(g):
             nc.sync.dma_start(out=w_raw[g][:], in_=w_rows[g])
 
-
         nc.scalar.dma_start(out=scale[:], in_=Wdkv_scale.rearrange("(p j) o -> p (j o)", j=PACK))
         nc.scalar.dma_start(out=gain4[:], in_=kv_norm_w.rearrange("(p j) -> p j", j=PACK))
         for j in range(2):
-            nc.sync.dma_start(out=d_first[j][:], in_=byte_rows[:, 2 * j : 2 * j + 2, 0 : 2 * CHUNK])
-        nc.sync.dma_start(out=d_next[:], in_=byte_rows[:, :, 2 * CHUNK : LATE * CHUNK])
+            nc.sync.dma_start(out=d_first[j][:], in_=byte_rows[:, 2 * j : 2 * j + 2, 0 : FIRST * CHUNK])
+        nc.sync.dma_start(out=d_next[:], in_=byte_rows[:, :, FIRST * CHUNK : LATE * CHUNK])
         load_x(0)
         for g in range(NP):
             load_w(g)
-        load_x(1)
-        load_x(2)
-        load_x(3)
+        for b in range(1, NB):
+            load_x(b)
         nc.sync.dma_start(out=d_late[:], in_=byte_rows[:, :, LATE * CHUNK : KVW])
         nc.sync.dma_start(out=cos_sin[:].rearrange("p i e -> p (i e)"), in_=freq_cis.rearrange("(p b) i e -> p (b i e)", b=NB))
 
@@ -137,7 +136,7 @@ def tile_multiheadlatentattention_pa_kernel(tc, x, freq_cis, Wckv, kv_norm_w, Wd
                 nc.scalar.copy(out, in_)
 
         def interleave(eng, grouped, rows):
-            copy(eng, grouped.rearrange("p (c i) t -> p c t i", i=4), rows.rearrange("p t (c i) -> p c t i", i=4))
+            copy(eng, grouped.rearrange("p (c i) t -> p c t i", i=RUN), rows.rearrange("p t (c i) -> p c t i", i=RUN))
 
         def quantize(codes, scales, grouped):
             nc.vector.quantize_mx(out=codes.bitcast(FP8X4), scales=scales, in_=grouped)
@@ -155,7 +154,7 @@ def tile_multiheadlatentattention_pa_kernel(tc, x, freq_cis, Wckv, kv_norm_w, Wd
 
         def warm_up():
             out = take("warm")[:].rearrange("p (a n) -> p a n", a=BANK // P)
-            for n in range(WARM_UPS):
+            for repeat in range(WARM_UPS):
                 nc.tensor.matmul(out, lhsT=ident_bf[:], rhs=ident_bf[:].unsqueeze(1).to_broadcast([P, BANK // P, P]), start=True, stop=True)
             give("warm")
 
@@ -186,23 +185,9 @@ def tile_multiheadlatentattention_pa_kernel(tc, x, freq_cis, Wckv, kv_norm_w, Wd
             rows = w_raw[g][:, :, 0:LORA].rearrange("p t (c u e) -> p c t u e", u=2, e=2)
             copy(eng, grouped[:, lo // PACK : hi // PACK], rows[:, lo // PACK : hi // PACK])
 
-        def w_shared(g, split=W_SPLIT):
-            w_inter(g, V, 0, split)
-            w_inter(g, S, split, LORA)
-
-        def by_identity(out, rows):
-            nc.tensor.matmul(out.rearrange("p (n t) -> p t n", t=PACK), lhsT=ident_bf[:], rhs=rows, start=True, stop=True)
-
-        def w_identity(g, lo, hi):
-            out = take(("w", g, lo))[:].bitcast(BF16)
-            for q in range((hi - lo) // P):
-                by_identity(out[:, BANK * q : BANK * (q + 1)], w_raw[g][:, :, lo + P * q : lo + P * (q + 1)])
-
-        def w_identity_out(g, lo, hi):
-            words = w_grouped(g)[:].rearrange("p w t -> p (w t)").bitcast(F32).rearrange("p (u c x) -> p u c x", u=2, x=PACK)
-            made = bank(("w", g, lo))[:, 0 : 2 * (hi - lo)].rearrange("p (c u x) -> p u c x", u=2, x=PACK)
-            nc.scalar.copy(words[:, :, lo // PACK : hi // PACK, :], made)
-            give(("w", g, lo))
+        def w_shared(g):
+            w_inter(g, V, 0, W_SPLIT[g])
+            w_inter(g, S, W_SPLIT[g], LORA)
 
         def w_quant(g):
             quantize(w_codes[g][:], w_scales[g][:], w_grouped(g)[:].rearrange("p w t -> p (w t)"))
@@ -254,10 +239,10 @@ def tile_multiheadlatentattention_pa_kernel(tc, x, freq_cis, Wckv, kv_norm_w, Wd
             quantize(n_codes[b][:], n_scales[b][:], n_grouped(b))
 
         def d_raw(c, t, n):
-            if c < 2:
+            if c < FIRST:
                 return d_first[t // 2][:, t % 2, CHUNK * c : CHUNK * (c + n)]
             if c < LATE:
-                return d_next[:, t, CHUNK * (c - 2) : CHUNK * (c - 2 + n)]
+                return d_next[:, t, CHUNK * (c - FIRST) : CHUNK * (c - FIRST + n)]
             return d_late[:, t, CHUNK * (c - LATE) : CHUNK * (c - LATE + n)]
 
         def d_wide(c, n=1):
@@ -276,17 +261,15 @@ def tile_multiheadlatentattention_pa_kernel(tc, x, freq_cis, Wckv, kv_norm_w, Wd
             else:
                 nc.scalar.activation(wide, raw, ACT.Copy, scale=scale[:, t : t + 1])
 
-        def widen_shared(c, n=1):
-            for t in range(PACK - 1):
-                widen(c, t, V, n)
-            widen(c, PACK - 1, S, n)
-
         def d_inter(c):
             interleave(V, d_grouped(c), d_wide(c))
 
-        def d_half(c, h, eng=V):
+        def d_half(c, h):
             cols = slice(HALF * h, HALF * (h + 1))
-            interleave(eng, d_grouped(c)[:, cols, :], d_wide(c)[:, :, cols])
+            interleave(V, d_grouped(c)[:, cols, :], d_wide(c)[:, :, cols])
+
+        def by_identity(out, rows):
+            nc.tensor.matmul(out.rearrange("p (n t) -> p t n", t=PACK), lhsT=ident_bf[:], rhs=rows, start=True, stop=True)
 
         def d_identity(c, h, quarters=(0, 1)):
             if 0 in quarters:
@@ -325,16 +308,6 @@ def tile_multiheadlatentattention_pa_kernel(tc, x, freq_cis, Wckv, kv_norm_w, Wd
 
         def wr_inter(g, eng):
             interleave(eng, wr_grouped[:, g, :, :], w_raw[g][:, :, LORA:WIDTH])
-
-        def wr_identity(g):
-            if g % 2 == 0:
-                take(("wr", g // 2))
-            out = bank(("wr", g // 2))[:].bitcast(BF16)
-            by_identity(out[:, BANK * (g % 2) : BANK * (g % 2 + 1)], w_raw[g][:, :, LORA:WIDTH])
-
-        def wr_identity_out(h):
-            nc.scalar.copy(wr_grouped[:, 2 * h : 2 * h + 2, :, :].rearrange("p g w t -> p (g w t)").bitcast(F32), bank(("wr", h))[:])
-            give(("wr", h))
 
         def wr_quant():
             quantize(wr_codes[:].rearrange("p g w -> p (g w)"), wr_scales[:].rearrange("p g w -> p (g w)"), wr_grouped[:].rearrange("p g w t -> p (g w t)"))
@@ -376,6 +349,7 @@ def tile_multiheadlatentattention_pa_kernel(tc, x, freq_cis, Wckv, kv_norm_w, Wd
         widen(2, 2, S)
         widen(3, 3, V)
         widen(2, 3, V)
+
         d_identity(0, 0)
         d_identity(0, 1, (0,))
         x_turn(0, 0)
@@ -385,22 +359,23 @@ def tile_multiheadlatentattention_pa_kernel(tc, x, freq_cis, Wckv, kv_norm_w, Wd
         d_identity(1, 1)
         d_identity_out(0, 0)
         x_out(0, 0)
-        w_inter(0, S, 416, LORA)
+        w_inter(0, S, W_SPLIT[0], LORA)
         x_out(0, 1)
         d_identity_out(0, 1)
         d_identity(2, 0)
         d_identity(2, 1)
         d_inter(3)
-        w_inter(0, V, 0, 416)
+        w_inter(0, V, 0, W_SPLIT[0])
         w_shared(1)
         d_identity_out(1, 0)
         x_quant(0)
         w_quant(0)
         w_shared(2)
         w_quant(1)
-        w_shared(3, 320)
+        w_shared(3)
         w_quant(2)
         w_quant(3)
+
         lat_passes(0, (0, 1))
         d_identity_out(1, 1)
         d_identity_out(2, 0)
@@ -433,6 +408,7 @@ def tile_multiheadlatentattention_pa_kernel(tc, x, freq_cis, Wckv, kv_norm_w, Wd
         x_out(3, 1)
         widen(4, 0, V, 2)
         n_quant(0)
+
         lat_passes(2, range(NP))
         kv_product(0, 0)
         kv_product(0, 1)
@@ -476,15 +452,16 @@ def tile_multiheadlatentattention_pa_kernel(tc, x, freq_cis, Wckv, kv_norm_w, Wd
         n_turn(3)
         kv_product(2, 2)
         kv_product(2, 3)
-        for c in range(4):
+        for c in range(LATE):
             kv_out(2, c)
         d_half(4, 1)
         widen(7, 0, V)
         n_out(3, V)
         widen(6, 0, V)
         n_quant(3)
-        for c in range(4):
+        for c in range(LATE):
             kv(3, c)
+
         d_inter(5)
         d_quant(4)
         d_quant(5)
@@ -499,6 +476,7 @@ def tile_multiheadlatentattention_pa_kernel(tc, x, freq_cis, Wckv, kv_norm_w, Wd
         for b in range(NB):
             kv(b, 4, PACED_BANK)
             kv(b, 5, PACED_BANK)
+
         wr_inter(0, S)
         for g in range(1, NP):
             wr_inter(g, V)

@@ -27,12 +27,12 @@ PAIRS = NB * ROPE // 2
 CHUNK = BANK
 HALF = CHUNK // 2
 FIRST, LATE = 2, 4
-STORES = [(b, 1, c, 2) for b in range(NB) for c in (0, 2, 4)] + [(0, 1, 6, 2), (1, 1, 6, 2), (2, 2, 6, 2)]
+GROUPS = ((0, 4), (4, 4), (8, 4), (12, 4))
 W_SPLIT = (416, 288, 288, 320)
 RUN = 2
 WARM_UPS = 5
 PACED_BANK = -3
-LARGE_BUFS, SMALL_BUFS = 1, 10
+STORE_BUFS = 9
 DMA_ALIGN = 256
 V, S = "vector", "scalar"
 
@@ -101,8 +101,8 @@ def tile_multiheadlatentattention_pa_kernel(tc, x, freq_cis, Wckv, kv_norm_w, Wd
         nc.sync.dma_start(out=d_late[:], in_=byte_rows[:, :, LATE * CHUNK : KVW])
         nc.sync.dma_start(out=cos_sin[:].rearrange("p i e -> p (i e)"), in_=freq_cis.rearrange("(p b) i e -> p (b i e)", b=NB))
 
-        make_identity(nc, ident[:])
         make_identity(nc, ident_bf[:])
+        make_identity(nc, ident[:])
         nc.vector.memset(eps[:], EPS)
         nc.scalar.activation(unread[:], eps[:], ACT.Abs_reciprocal_sqrt)
 
@@ -238,86 +238,89 @@ def tile_multiheadlatentattention_pa_kernel(tc, x, freq_cis, Wckv, kv_norm_w, Wd
         def n_quant(b):
             quantize(n_codes[b][:], n_scales[b][:], n_grouped(b))
 
-        def d_raw(c, t, n):
-            if c < FIRST:
-                return d_first[t // 2][:, t % 2, CHUNK * c : CHUNK * (c + n)]
-            if c < LATE:
-                return d_next[:, t, CHUNK * (c - FIRST) : CHUNK * (c - FIRST + n)]
-            return d_late[:, t, CHUNK * (c - LATE) : CHUNK * (c - LATE + n)]
+        def group(h):
+            return [g for g in GROUPS if g[0] <= h < g[0] + g[1]][0]
 
-        def d_wide(c, n=1):
-            pair = stage(work, ("d_wide", c // 2), [P, PACK, 2 * CHUNK], BF16, bufs=2)
-            return pair[:, :, CHUNK * (c % 2) : CHUNK * (c % 2 + n)]
+        def d_raw(h, n, t):
+            if h < 2 * FIRST:
+                return d_first[t // 2][:, t % 2, HALF * h : HALF * (h + n)]
+            if h < 2 * LATE:
+                return d_next[:, t, HALF * (h - 2 * FIRST) : HALF * (h - 2 * FIRST + n)]
+            return d_late[:, t, HALF * (h - 2 * LATE) : HALF * (h - 2 * LATE + n)]
 
-        def d_grouped(c, n=1):
-            pair = stage(work, ("d_grouped", c // 2), [P, 2 * CHUNK, PACK], BF16, bufs=2, align_bytes=64)
-            return pair[:, CHUNK * (c % 2) : CHUNK * (c % 2 + n), :]
+        def d_wide(h, n):
+            first, count = group(h)
+            rows = stage(work, ("d_wide", first), [P, PACK, HALF * count], BF16, bufs=2)
+            return rows[:, :, HALF * (h - first) : HALF * (h - first + n)]
 
-        def widen(c, t, eng, n=1):
-            wide = d_wide(c, n)[:, t, :]
-            raw = d_raw(c, t, n).bitcast(FP8)
+        def d_grouped(h, n):
+            first, count = group(h)
+            grouped = stage(work, ("d_grouped", first), [P, HALF * count, PACK], BF16, bufs=2, align_bytes=64)
+            return grouped[:, HALF * (h - first) : HALF * (h - first + n), :]
+
+        def widen(h, n, t, eng=V):
+            wide = d_wide(h, n)[:, t, :]
+            raw = d_raw(h, n, t).bitcast(FP8)
             if eng == V:
                 nc.vector.tensor_scalar(wide, raw, scale[:, t : t + 1], None, ALU.mult)
             else:
                 nc.scalar.activation(wide, raw, ACT.Copy, scale=scale[:, t : t + 1])
 
-        def d_inter(c):
-            interleave(V, d_grouped(c), d_wide(c))
-
-        def d_half(c, h):
-            cols = slice(HALF * h, HALF * (h + 1))
-            interleave(V, d_grouped(c)[:, cols, :], d_wide(c)[:, :, cols])
+        def d_inter(h, n):
+            interleave(V, d_grouped(h, n), d_wide(h, n))
 
         def by_identity(out, rows):
             nc.tensor.matmul(out.rearrange("p (n t) -> p t n", t=PACK), lhsT=ident_bf[:], rhs=rows, start=True, stop=True)
 
-        def d_identity(c, h, quarters=(0, 1)):
+        def d_identity(h, quarters=(0, 1)):
             if 0 in quarters:
-                take(("d", c, h))
-            out = bank(("d", c, h))[:].bitcast(BF16)
+                take(("d", h))
+            out = bank(("d", h))[:].bitcast(BF16)
             for q in quarters:
-                first = HALF * h + P * q
-                by_identity(out[:, BANK * q : BANK * (q + 1)], d_wide(c)[:, :, first : first + P])
+                by_identity(out[:, BANK * q : BANK * (q + 1)], d_wide(h, 1)[:, :, P * q : P * (q + 1)])
 
-        def d_identity_out(c, h):
-            grouped = d_grouped(c)[:, HALF * h : HALF * (h + 1), :].rearrange("p w t -> p (w t)")
-            nc.scalar.copy(grouped.bitcast(F32), bank(("d", c, h))[:])
-            give(("d", c, h))
+        def d_identity_out(h):
+            nc.scalar.copy(d_grouped(h, 1).rearrange("p w t -> p (w t)").bitcast(F32), bank(("d", h))[:])
+            give(("d", h))
 
-        def d_quant(c, n=1):
-            cols = slice(CHUNK * c, CHUNK * (c + n))
-            quantize(d_codes[:, cols], d_scales[:, cols], d_grouped(c, n).rearrange("p w t -> p (w t)"))
+        def d_quant(h, n):
+            cols = slice(HALF * h, HALF * (h + n))
+            quantize(d_codes[:, cols], d_scales[:, cols], d_grouped(h, n).rearrange("p w t -> p (w t)"))
 
-        def kv_product(b, c, place=0):
-            cols = slice(CHUNK * c, CHUNK * (c + 1))
-            product(take(("kv", b, c), place)[:], n_codes[b][:], n_scales[b][:], d_codes[:, cols], d_scales[:, cols], True, True)
+        def width(h):
+            first, count = group(h)
+            return HALF * min(2, first + count - h)
 
-        def kv_out(b, c, eng=S):
-            b0, nb, c0, n = [s for s in STORES if s[0] <= b < s[0] + s[1] and s[2] <= c < s[2] + s[3]][0]
-            large = nb * n > 2
-            rows = stage(outs, ("kv_large" if large else "kv_small", b0, c0), [P, nb, n * CHUNK], F32, bufs=LARGE_BUFS if large else SMALL_BUFS, align_bytes=DMA_ALIGN)
-            copy(eng, rows[:, b - b0, CHUNK * (c - c0) : CHUNK * (c - c0 + 1)], bank(("kv", b, c))[:])
-            give(("kv", b, c))
-            emptied.append((b0, c0))
-            if emptied.count((b0, c0)) == nb * n:
-                nc.sync.dma_start(out=kv_rows[:, b0 : b0 + nb, CHUNK * c0 : CHUNK * (c0 + n)], in_=rows[:])
+        def kv_product(b, h, place=0):
+            cols = slice(HALF * h, HALF * h + width(h))
+            product(take(("kv", b, h), place)[:, 0 : width(h)], n_codes[b][:], n_scales[b][:], d_codes[:, cols], d_scales[:, cols], True, True)
 
-        def kv(b, c, place=0):
-            kv_product(b, c, place)
-            kv_out(b, c)
+        def kv_out(b, h, eng=S):
+            first, count = group(h)
+            rows = stage(outs, ("kv_rows", b, first), [P, HALF * count], F32, bufs=STORE_BUFS, align_bytes=DMA_ALIGN)
+            copy(eng, rows[:, HALF * (h - first) : HALF * (h - first) + width(h)], bank(("kv", b, h))[:, 0 : width(h)])
+            give(("kv", b, h))
+            emptied.append((b, first))
+            if emptied.count((b, first)) == (count + 1) // 2:
+                nc.sync.dma_start(out=kv_rows[:, b, HALF * first : HALF * (first + count)], in_=rows[:])
+
+        def kv(b, h, place=0):
+            kv_product(b, h, place)
+            kv_out(b, h)
 
         def wr_inter(g, eng):
             interleave(eng, wr_grouped[:, g, :, :], w_raw[g][:, :, LORA:WIDTH])
 
-        def wr_quant():
-            quantize(wr_codes[:].rearrange("p g w -> p (g w)"), wr_scales[:].rearrange("p g w -> p (g w)"), wr_grouped[:].rearrange("p g w t -> p (g w t)"))
+        def wr_quant(g):
+            two = slice(g, g + 2)
+            quantize(wr_codes[:, two, :].rearrange("p g w -> p (g w)"), wr_scales[:, two, :].rearrange("p g w -> p (g w)"), wr_grouped[:, two, :, :].rearrange("p g w t -> p (g w t)"))
 
-        def kr_products(b):
-            if b == 0:
+        def kr_products(g):
+            if g == 0:
                 take("kr")
             out = bank("kr")
-            for g in range(NP):
-                product(out[:, ROPE * b : ROPE * (b + 1)], x_codes[b][:, g, :], x_scales[b][:, g, :], wr_codes[:, g, :], wr_scales[:, g, :], g == 0, g == NP - 1)
+            for b in range(NB):
+                product(out[:, ROPE * b : ROPE * (b + 1)], x_codes[b][:, g, :], x_scales[b][:, g, :], wr_codes[:, g, :], wr_scales[:, g, :], g == 0 and b == 0, g == NP - 1 and b == NB - 1)
 
         def times_cos():
             kr = bank("kr")[:].rearrange("p (i e) -> p i e", e=2)
@@ -336,38 +339,37 @@ def tile_multiheadlatentattention_pa_kernel(tc, x, freq_cis, Wckv, kv_norm_w, Wd
 
         warm_up()
         gain_spread()
-        widen(0, 0, V, 2)
-        widen(0, 1, S, 2)
-        widen(0, 2, V)
-        widen(0, 3, V)
-        widen(1, 2, V)
-        widen(1, 3, V)
+        widen(0, 4, 0)
+        widen(0, 4, 1, S)
+        widen(0, 2, 2)
+        widen(0, 2, 3)
+        widen(2, 2, 2)
+        widen(2, 2, 3)
         gain_out()
-        widen(2, 0, V, 2)
-        widen(2, 1, S, 2)
-        widen(3, 2, V)
-        widen(2, 2, S)
-        widen(3, 3, V)
-        widen(2, 3, V)
+        widen(4, 4, 0)
+        widen(4, 4, 1, S)
+        widen(6, 2, 2)
+        widen(4, 2, 2, S)
+        widen(6, 2, 3)
+        widen(4, 2, 3)
 
-        d_identity(0, 0)
-        d_identity(0, 1, (0,))
+        d_identity(0)
+        d_identity(1)
         x_turn(0, 0)
-        d_identity(0, 1, (1,))
         x_turn(0, 1)
-        d_identity(1, 0)
-        d_identity(1, 1)
-        d_identity_out(0, 0)
+        d_identity(2)
+        d_identity(3)
+        d_identity_out(0)
+        d_identity_out(1)
         x_out(0, 0)
-        w_inter(0, S, W_SPLIT[0], LORA)
         x_out(0, 1)
-        d_identity_out(0, 1)
-        d_identity(2, 0)
-        d_identity(2, 1)
-        d_inter(3)
+        w_inter(0, S, W_SPLIT[0], LORA)
+        d_identity(4)
+        d_identity(5)
+        d_inter(6, 2)
         w_inter(0, V, 0, W_SPLIT[0])
         w_shared(1)
-        d_identity_out(1, 0)
+        d_identity_out(2)
         x_quant(0)
         w_quant(0)
         w_shared(2)
@@ -377,8 +379,8 @@ def tile_multiheadlatentattention_pa_kernel(tc, x, freq_cis, Wckv, kv_norm_w, Wd
         w_quant(3)
 
         lat_passes(0, (0, 1))
-        d_identity_out(1, 1)
-        d_identity_out(2, 0)
+        d_identity_out(3)
+        d_identity_out(4)
         x_turn(1, 0)
         x_turn(1, 1)
         lat_passes(0, (2, 3))
@@ -387,116 +389,114 @@ def tile_multiheadlatentattention_pa_kernel(tc, x, freq_cis, Wckv, kv_norm_w, Wd
         x_turn(2, 0)
         x_turn(2, 1)
         sum_squares(0)
-        d_identity_out(2, 1)
+        d_identity_out(5)
         root(0)
         x_out(2, 0)
         x_out(2, 1)
-        d_quant(0, 2)
+        d_quant(0, 4)
         x_quant(1)
         x_turn(3, 0)
         lat_passes(1, range(NP))
-        d_quant(3)
+        d_quant(6, 2)
         norm(0)
         n_turn(0)
         x_turn(3, 1)
-        d_quant(2)
+        d_quant(4, 2)
         x_quant(2)
         x_out(3, 0)
         sum_squares(1)
         n_out(0, S)
         root(1)
         x_out(3, 1)
-        widen(4, 0, V, 2)
+        widen(8, 4, 0)
         n_quant(0)
 
         lat_passes(2, range(NP))
         kv_product(0, 0)
-        kv_product(0, 1)
+        kv_product(0, 2)
         norm(1)
         n_turn(1)
-        kv_product(0, 2)
-        kv_product(0, 3)
+        kv_product(0, 4)
+        kv_product(0, 6)
         x_quant(3)
-        widen(4, 3, S)
-        widen(4, 1, V, 2)
+        widen(8, 2, 3, S)
+        widen(8, 4, 1)
         sum_squares(2)
         kv_out(0, 0)
         root(2)
-        kv_out(0, 1, V)
+        kv_out(0, 2, V)
         lat_passes(3, range(NP))
         n_out(1, S)
-        kv_out(0, 2)
-        kv_out(0, 3)
-        widen(4, 2, V)
+        kv_out(0, 4)
+        kv_out(0, 6)
+        widen(8, 2, 2)
         n_quant(1)
         norm(2)
         kv_product(1, 0)
-        kv_product(1, 1)
-        n_turn(2)
         kv_product(1, 2)
-        kv_product(1, 3)
-        d_half(4, 0)
-        widen(5, 2, V)
+        n_turn(2)
+        kv_product(1, 4)
+        kv_product(1, 6)
+        d_inter(8, 1)
+        widen(10, 2, 2)
         sum_squares(3)
         kv_out(1, 0)
         root(3)
-        kv_out(1, 1)
         kv_out(1, 2)
-        kv_out(1, 3)
+        kv_out(1, 4)
+        kv_out(1, 6)
         n_out(2, V)
-        widen(5, 3, V)
+        widen(10, 2, 3)
         n_quant(2)
         norm(3)
         kv_product(2, 0)
-        kv_product(2, 1)
-        n_turn(3)
         kv_product(2, 2)
-        kv_product(2, 3)
-        for c in range(LATE):
-            kv_out(2, c)
-        d_half(4, 1)
-        widen(7, 0, V)
+        n_turn(3)
+        kv_product(2, 4)
+        kv_product(2, 6)
+        for h in range(0, 2 * LATE, 2):
+            kv_out(2, h)
+        d_inter(9, 1)
+        widen(14, 2, 0)
         n_out(3, V)
-        widen(6, 0, V)
+        widen(12, 2, 0)
         n_quant(3)
-        for c in range(LATE):
-            kv(3, c)
+        for h in range(0, 2 * LATE, 2):
+            kv(3, h)
 
-        d_inter(5)
-        d_quant(4)
-        d_quant(5)
-        widen(6, 1, V, 2)
-        widen(6, 2, V, 2)
-        widen(6, 3, V)
-        widen(7, 3, V)
-        d_inter(6)
-        d_inter(7)
-        d_quant(6)
-        d_quant(7)
+        d_inter(10, 2)
+        d_quant(8, 2)
+        d_quant(10, 2)
+        widen(12, 4, 1)
+        widen(12, 4, 2)
+        widen(12, 2, 3)
+        widen(14, 2, 3)
+        d_inter(12, 2)
+        d_inter(14, 1)
+        d_quant(12, 2)
+        d_inter(15, 1)
+        d_quant(14, 1)
+        d_quant(15, 1)
         for b in range(NB):
-            kv(b, 4, PACED_BANK)
-            kv(b, 5, PACED_BANK)
+            kv(b, 8, PACED_BANK)
+            kv(b, 10, PACED_BANK)
 
+        for b in range(NB):
+            kv_product(b, 12)
         wr_inter(0, S)
+        kv_out(0, 12)
         for g in range(1, NP):
             wr_inter(g, V)
-        wr_quant()
-        for b in range(2):
-            kv_product(b, 6)
-            kv_product(b, 7)
-        kv_out(0, 6)
-        kv_out(0, 7)
-        for b in range(2, NB):
-            kv_product(b, 6)
-            kv_product(b, 7)
-        kv_out(1, 6)
-        kv_out(1, 7)
-        kv_out(2, 6, V)
+        wr_quant(0)
+        wr_quant(2)
         for b in range(NB):
-            kr_products(b)
-        kv_out(2, 7, V)
-        kv_out(3, 6)
-        kv_out(3, 7)
+            kv_product(b, 14)
+        kv_out(0, 14)
+        for g in range(NP):
+            kr_products(g)
+        for b in range(1, NB):
+            kv_out(b, 12)
+            kv_out(b, 14)
         times_cos()
         times_sin()
         rotate_sum()

@@ -26,8 +26,8 @@ NP = C // (P * PACK)
 PAIRS = NB * ROPE // 2
 CHUNK = BANK
 HALF = CHUNK // 2
-FIRST, LATE = 2, 4
-GROUPS = ((0, 4), (4, 4), (8, 4), (12, 4))
+FIRST, LATE = 8, 16
+GROUPS = ((0, 8), (8, 8), (16, 8), (24, 8))
 W_SPLIT = (416, 288, 288, 320)
 RUN = 2
 WARM_UPS = 5
@@ -65,9 +65,9 @@ def tile_multiheadlatentattention_pa_kernel(tc, x, freq_cis, Wckv, kv_norm_w, Wd
         rotated = keep.tile([P, PAIRS, 2], F32, name="rotated", align_bytes=DMA_ALIGN)
         x_raw = [keep.tile([P, C], BF16, name="x_raw%d" % b, align_bytes=DMA_ALIGN) for b in range(NB)]
         w_raw = [keep.tile([P, PACK, WIDTH], BF16, name="w_raw%d" % g, align_bytes=DMA_ALIGN) for g in range(NP)]
-        d_first = [keep.tile([P, 2, FIRST * CHUNK], U8, name="d_first%d" % j, align_bytes=DMA_ALIGN) for j in range(2)]
-        d_next = keep.tile([P, PACK, (LATE - FIRST) * CHUNK], U8, name="d_next", align_bytes=DMA_ALIGN)
-        d_late = keep.tile([P, PACK, KVW - LATE * CHUNK], U8, name="d_late", align_bytes=DMA_ALIGN)
+        d_first = [keep.tile([P, 2, FIRST * P], U8, name="d_first%d" % j, align_bytes=DMA_ALIGN) for j in range(2)]
+        d_next = keep.tile([P, PACK, (LATE - FIRST) * P], U8, name="d_next", align_bytes=DMA_ALIGN)
+        d_late = keep.tile([P, PACK, KVW - LATE * P], U8, name="d_late", align_bytes=DMA_ALIGN)
         x_codes = [keep.tile([P, NP, P], U32, name="x_codes%d" % b, align_bytes=64) for b in range(NB)]
         x_scales = [keep.tile([P, NP, P], U8, name="x_scales%d" % b, align_bytes=64) for b in range(NB)]
         w_codes = [keep.tile([P, LORA], U32, name="w_codes%d" % g, align_bytes=64) for g in range(NP)]
@@ -91,14 +91,14 @@ def tile_multiheadlatentattention_pa_kernel(tc, x, freq_cis, Wckv, kv_norm_w, Wd
         nc.scalar.dma_start(out=scale[:], in_=Wdkv_scale.rearrange("(p j) o -> p (j o)", j=PACK))
         nc.scalar.dma_start(out=gain4[:], in_=kv_norm_w.rearrange("(p j) -> p j", j=PACK))
         for j in range(2):
-            nc.sync.dma_start(out=d_first[j][:], in_=byte_rows[:, 2 * j : 2 * j + 2, 0 : FIRST * CHUNK])
-        nc.sync.dma_start(out=d_next[:], in_=byte_rows[:, :, FIRST * CHUNK : LATE * CHUNK])
+            nc.sync.dma_start(out=d_first[j][:], in_=byte_rows[:, 2 * j : 2 * j + 2, 0 : FIRST * P])
+        nc.sync.dma_start(out=d_next[:], in_=byte_rows[:, :, FIRST * P : LATE * P])
         load_x(0)
         for g in range(NP):
             load_w(g)
         for b in range(1, NB):
             load_x(b)
-        nc.sync.dma_start(out=d_late[:], in_=byte_rows[:, :, LATE * CHUNK : KVW])
+        nc.sync.dma_start(out=d_late[:], in_=byte_rows[:, :, LATE * P : KVW])
         nc.sync.dma_start(out=cos_sin[:].rearrange("p i e -> p (i e)"), in_=freq_cis.rearrange("(p b) i e -> p (b i e)", b=NB))
 
         make_identity(nc, ident_bf[:])
@@ -238,75 +238,83 @@ def tile_multiheadlatentattention_pa_kernel(tc, x, freq_cis, Wckv, kv_norm_w, Wd
         def n_quant(b):
             quantize(n_codes[b][:], n_scales[b][:], n_grouped(b))
 
-        def group(h):
-            return [g for g in GROUPS if g[0] <= h < g[0] + g[1]][0]
+        def group(s):
+            return [g for g in GROUPS if g[0] <= s < g[0] + g[1]][0]
 
-        def d_raw(h, n, t):
-            if h < 2 * FIRST:
-                return d_first[t // 2][:, t % 2, HALF * h : HALF * (h + n)]
-            if h < 2 * LATE:
-                return d_next[:, t, HALF * (h - 2 * FIRST) : HALF * (h - 2 * FIRST + n)]
-            return d_late[:, t, HALF * (h - 2 * LATE) : HALF * (h - 2 * LATE + n)]
+        def d_raw(s, n, t):
+            if s < FIRST:
+                return d_first[t // 2][:, t % 2, P * s : P * (s + n)]
+            if s < LATE:
+                return d_next[:, t, P * (s - FIRST) : P * (s - FIRST + n)]
+            return d_late[:, t, P * (s - LATE) : P * (s - LATE + n)]
 
-        def d_wide(h, n):
-            first, count = group(h)
-            rows = stage(work, ("d_wide", first), [P, PACK, HALF * count], BF16, bufs=2)
-            return rows[:, :, HALF * (h - first) : HALF * (h - first + n)]
+        def d_wide(s, n):
+            first, count = group(s)
+            rows = stage(work, ("d_wide", first), [P, PACK, P * count], BF16, bufs=2)
+            return rows[:, :, P * (s - first) : P * (s - first + n)]
 
-        def d_grouped(h, n):
-            first, count = group(h)
-            grouped = stage(work, ("d_grouped", first), [P, HALF * count, PACK], BF16, bufs=2, align_bytes=64)
-            return grouped[:, HALF * (h - first) : HALF * (h - first + n), :]
+        def d_grouped(s, n):
+            first, count = group(s)
+            grouped = stage(work, ("d_grouped", first), [P, P * count, PACK], BF16, bufs=2, align_bytes=64)
+            return grouped[:, P * (s - first) : P * (s - first + n), :]
 
-        def widen(h, n, t, eng=V):
-            wide = d_wide(h, n)[:, t, :]
-            raw = d_raw(h, n, t).bitcast(FP8)
+        def widen(s, n, t, eng=V):
+            wide = d_wide(s, n)[:, t, :]
+            raw = d_raw(s, n, t).bitcast(FP8)
             if eng == V:
                 nc.vector.tensor_scalar(wide, raw, scale[:, t : t + 1], None, ALU.mult)
             else:
                 nc.scalar.activation(wide, raw, ACT.Copy, scale=scale[:, t : t + 1])
 
-        def d_inter(h, n):
-            interleave(V, d_grouped(h, n), d_wide(h, n))
+        def d_inter(s, n):
+            interleave(V, d_grouped(s, n), d_wide(s, n))
 
         def by_identity(out, rows):
             nc.tensor.matmul(out.rearrange("p (n t) -> p t n", t=PACK), lhsT=ident_bf[:], rhs=rows, start=True, stop=True)
 
-        def d_identity(h, quarters=(0, 1)):
-            if 0 in quarters:
-                take(("d", h))
-            out = bank(("d", h))[:].bitcast(BF16)
-            for q in quarters:
-                by_identity(out[:, BANK * q : BANK * (q + 1)], d_wide(h, 1)[:, :, P * q : P * (q + 1)])
+        def d_identity(s):
+            out = take(("d", s))[:].bitcast(BF16)
+            for q in range(2):
+                by_identity(out[:, BANK * q : BANK * (q + 1)], d_wide(s + q, 1))
 
-        def d_identity_out(h):
-            nc.scalar.copy(d_grouped(h, 1).rearrange("p w t -> p (w t)").bitcast(F32), bank(("d", h))[:])
-            give(("d", h))
+        def d_identity_out(s):
+            nc.scalar.copy(d_grouped(s, 2).rearrange("p w t -> p (w t)").bitcast(F32), bank(("d", s))[:])
+            give(("d", s))
 
-        def d_quant(h, n):
-            cols = slice(HALF * h, HALF * (h + n))
-            quantize(d_codes[:, cols], d_scales[:, cols], d_grouped(h, n).rearrange("p w t -> p (w t)"))
+        def d_quant(s, n):
+            cols = slice(P * s, P * (s + n))
+            quantize(d_codes[:, cols], d_scales[:, cols], d_grouped(s, n).rearrange("p w t -> p (w t)"))
 
-        def width(h):
-            first, count = group(h)
-            return HALF * min(2, first + count - h)
+        def strips(s):
+            first, count = group(s)
+            return min(BANK // P, first + count - s)
 
-        def kv_product(b, h, place=0):
-            cols = slice(HALF * h, HALF * h + width(h))
-            product(take(("kv", b, h), place)[:, 0 : width(h)], n_codes[b][:], n_scales[b][:], d_codes[:, cols], d_scales[:, cols], True, True)
+        def kv_product(b, s, place=0):
+            out = take(("kv", b, s), place)
+            done = 0
+            for n in (4, 2, 1):
+                if strips(s) - done >= n:
+                    cols = slice(P * (s + done), P * (s + done + n))
+                    product(out[:, P * done : P * (done + n)], n_codes[b][:], n_scales[b][:], d_codes[:, cols], d_scales[:, cols], True, True)
+                    done = done + n
 
-        def kv_out(b, h, eng=S):
-            first, count = group(h)
-            rows = stage(outs, ("kv_rows", b, first), [P, HALF * count], F32, bufs=STORE_BUFS, align_bytes=DMA_ALIGN)
-            copy(eng, rows[:, HALF * (h - first) : HALF * (h - first) + width(h)], bank(("kv", b, h))[:, 0 : width(h)])
-            give(("kv", b, h))
-            emptied.append((b, first))
-            if emptied.count((b, first)) == (count + 1) // 2:
-                nc.sync.dma_start(out=kv_rows[:, b, HALF * first : HALF * (first + count)], in_=rows[:])
+        def kv_out(b, s, eng=S):
+            first, count = group(s)
+            if (first, count) == GROUPS[-1] and b >= 2:
+                b0, nb = 2, 2
+                rows = stage(outs, ("kv_last",), [P, nb, P * count], F32, bufs=1, align_bytes=DMA_ALIGN)
+            else:
+                b0, nb = b, 1
+                rows = stage(outs, ("kv_rows", b, first), [P, nb, P * count], F32, bufs=STORE_BUFS, align_bytes=DMA_ALIGN)
+            copy(eng, rows[:, b - b0, P * (s - first) : P * (s - first + strips(s))], bank(("kv", b, s))[:, 0 : P * strips(s)])
+            give(("kv", b, s))
+            emptied.append((b0, first))
+            if emptied.count((b0, first)) == nb * ((count + 3) // 4):
+                nc.sync.dma_start(out=kv_rows[:, b0 : b0 + nb, P * first : P * (first + count)], in_=rows[:])
 
-        def kv(b, h, place=0):
-            kv_product(b, h, place)
-            kv_out(b, h)
+        def kv(b, s, place=0):
+            kv_product(b, s, place)
+            kv_out(b, s)
 
         def wr_inter(g, eng):
             interleave(eng, wr_grouped[:, g, :, :], w_raw[g][:, :, LORA:WIDTH])
@@ -339,37 +347,37 @@ def tile_multiheadlatentattention_pa_kernel(tc, x, freq_cis, Wckv, kv_norm_w, Wd
 
         warm_up()
         gain_spread()
-        widen(0, 4, 0)
-        widen(0, 4, 1, S)
-        widen(0, 2, 2)
-        widen(0, 2, 3)
-        widen(2, 2, 2)
-        widen(2, 2, 3)
+        widen(0, 8, 0)
+        widen(0, 8, 1, S)
+        widen(0, 4, 2)
+        widen(0, 4, 3)
+        widen(4, 4, 2)
+        widen(4, 4, 3)
         gain_out()
-        widen(4, 4, 0)
-        widen(4, 4, 1, S)
-        widen(6, 2, 2)
-        widen(4, 2, 2, S)
-        widen(6, 2, 3)
-        widen(4, 2, 3)
+        widen(8, 8, 0)
+        widen(8, 8, 1, S)
+        widen(12, 4, 2)
+        widen(8, 4, 2, S)
+        widen(12, 4, 3)
+        widen(8, 4, 3)
 
         d_identity(0)
-        d_identity(1)
+        d_identity(2)
         x_turn(0, 0)
         x_turn(0, 1)
-        d_identity(2)
-        d_identity(3)
+        d_identity(4)
+        d_identity(6)
         d_identity_out(0)
-        d_identity_out(1)
+        d_identity_out(2)
         x_out(0, 0)
         x_out(0, 1)
         w_inter(0, S, W_SPLIT[0], LORA)
-        d_identity(4)
-        d_identity(5)
-        d_inter(6, 2)
+        d_identity(8)
+        d_identity(10)
+        d_inter(12, 4)
         w_inter(0, V, 0, W_SPLIT[0])
         w_shared(1)
-        d_identity_out(2)
+        d_identity_out(4)
         x_quant(0)
         w_quant(0)
         w_shared(2)
@@ -379,8 +387,8 @@ def tile_multiheadlatentattention_pa_kernel(tc, x, freq_cis, Wckv, kv_norm_w, Wd
         w_quant(3)
 
         lat_passes(0, (0, 1))
-        d_identity_out(3)
-        d_identity_out(4)
+        d_identity_out(6)
+        d_identity_out(8)
         x_turn(1, 0)
         x_turn(1, 1)
         lat_passes(0, (2, 3))
@@ -389,114 +397,113 @@ def tile_multiheadlatentattention_pa_kernel(tc, x, freq_cis, Wckv, kv_norm_w, Wd
         x_turn(2, 0)
         x_turn(2, 1)
         sum_squares(0)
-        d_identity_out(5)
+        d_identity_out(10)
         root(0)
         x_out(2, 0)
         x_out(2, 1)
-        d_quant(0, 4)
+        d_quant(0, 8)
         x_quant(1)
         x_turn(3, 0)
         lat_passes(1, range(NP))
-        d_quant(6, 2)
+        d_quant(12, 4)
         norm(0)
         n_turn(0)
         x_turn(3, 1)
-        d_quant(4, 2)
+        d_quant(8, 4)
         x_quant(2)
         x_out(3, 0)
         sum_squares(1)
         n_out(0, S)
         root(1)
         x_out(3, 1)
-        widen(8, 4, 0)
+        widen(16, 8, 0)
         n_quant(0)
 
         lat_passes(2, range(NP))
         kv_product(0, 0)
-        kv_product(0, 2)
+        kv_product(0, 4)
         norm(1)
         n_turn(1)
-        kv_product(0, 4)
-        kv_product(0, 6)
+        kv_product(0, 8)
+        kv_product(0, 12)
         x_quant(3)
-        widen(8, 2, 3, S)
-        widen(8, 4, 1)
+        widen(16, 4, 3, S)
+        widen(16, 8, 1)
         sum_squares(2)
         kv_out(0, 0)
         root(2)
-        kv_out(0, 2, V)
+        kv_out(0, 4, V)
         lat_passes(3, range(NP))
         n_out(1, S)
-        kv_out(0, 4)
-        kv_out(0, 6)
-        widen(8, 2, 2)
+        kv_out(0, 8)
+        kv_out(0, 12)
+        widen(16, 4, 2)
         n_quant(1)
         norm(2)
         kv_product(1, 0)
-        kv_product(1, 2)
-        n_turn(2)
         kv_product(1, 4)
-        kv_product(1, 6)
-        d_inter(8, 1)
-        widen(10, 2, 2)
+        n_turn(2)
+        kv_product(1, 8)
+        kv_product(1, 12)
+        d_inter(16, 2)
+        widen(20, 4, 2)
         sum_squares(3)
         kv_out(1, 0)
         root(3)
-        kv_out(1, 2)
         kv_out(1, 4)
-        kv_out(1, 6)
+        kv_out(1, 8)
+        kv_out(1, 12)
         n_out(2, V)
-        widen(10, 2, 3)
+        widen(20, 4, 3)
         n_quant(2)
         norm(3)
         kv_product(2, 0)
-        kv_product(2, 2)
-        n_turn(3)
         kv_product(2, 4)
-        kv_product(2, 6)
-        for h in range(0, 2 * LATE, 2):
-            kv_out(2, h)
-        d_inter(9, 1)
-        widen(14, 2, 0)
+        n_turn(3)
+        kv_product(2, 8)
+        kv_product(2, 12)
+        for s in range(0, LATE, 4):
+            kv_out(2, s)
+        d_inter(18, 2)
+        widen(28, 4, 0)
         n_out(3, V)
-        widen(12, 2, 0)
+        widen(24, 4, 0)
         n_quant(3)
-        for h in range(0, 2 * LATE, 2):
-            kv(3, h)
+        for s in range(0, LATE, 4):
+            kv(3, s)
 
-        d_inter(10, 2)
-        d_quant(8, 2)
-        d_quant(10, 2)
-        widen(12, 4, 1)
-        widen(12, 4, 2)
-        widen(12, 2, 3)
-        widen(14, 2, 3)
-        d_inter(12, 2)
-        d_inter(14, 1)
-        d_quant(12, 2)
-        d_inter(15, 1)
-        d_quant(14, 1)
-        d_quant(15, 1)
+        d_inter(20, 4)
+        d_quant(16, 4)
+        d_quant(20, 4)
+        widen(24, 8, 1)
+        widen(24, 8, 2)
+        widen(24, 4, 3)
+        widen(28, 4, 3)
+        d_inter(24, 4)
+        d_inter(28, 2)
+        d_quant(24, 4)
+        d_inter(30, 2)
+        d_quant(28, 2)
+        d_quant(30, 2)
         for b in range(NB):
-            kv(b, 8, PACED_BANK)
-            kv(b, 10, PACED_BANK)
+            kv(b, 16, PACED_BANK)
+            kv(b, 20, PACED_BANK)
 
         for b in range(NB):
-            kv_product(b, 12)
-        wr_inter(0, S)
-        kv_out(0, 12)
-        for g in range(1, NP):
+            kv_product(b, 24)
+        kv_out(0, 24)
+        for g in range(NP):
             wr_inter(g, V)
         wr_quant(0)
         wr_quant(2)
         for b in range(NB):
-            kv_product(b, 14)
-        kv_out(0, 14)
+            kv_product(b, 28)
+        kv_out(0, 28)
         for g in range(NP):
             kr_products(g)
         for b in range(1, NB):
-            kv_out(b, 12)
-            kv_out(b, 14)
+            kv_out(b, 24, V if b == 2 else S)
+            kv_out(b, 28, V if b == 2 else S)
         times_cos()
         times_sin()
         rotate_sum()

from contextlib import ExitStack

import concourse.mybir as mybir
from concourse.masks import make_identity

T, C, LORA, ROPE, KVW = 512, 2048, 512, 128, 4096
WIDTH = LORA + ROPE
FLOPS = 2 * T * C * WIDTH + 2 * T * LORA * KVW
EPS = 1e-6

F32 = mybir.dt.float32
BF16 = mybir.dt.bfloat16
U32 = mybir.dt.uint32
U8 = mybir.dt.uint8
FP8 = mybir.dt.float8_e4m3fn
FP8X4 = mybir.dt.float8_e4m3fn_x4
ALU = mybir.AluOpType
ACT = mybir.ActivationFunctionType

P = 128
PACK = 4
BANK = 512
BANKS = 8
NB = T // P
NP = C // (P * PACK)
PAIRS = NB * ROPE // 2
CHUNK = BANK
HALF = CHUNK // 2
FIRST, LATE = 8, 16
GROUPS = ((0, 8), (8, 8), (16, 8), (24, 8))
W_SPLIT = (416, 288, 288, 320)
RUN = 2
WARM_UPS = 5
PACED_BANK = -3
STORE_BUFS = 9
DMA_ALIGN = 256
V, S = "vector", "scalar"


def tile_multiheadlatentattention_pa_kernel(tc, x, freq_cis, Wckv, kv_norm_w, Wdkv_bytes, Wdkv_scale, out_0, out_1):
    nc = tc.nc
    x_rows = x.flatten_outer_dims().rearrange("(p b) c -> p b c", b=NB)
    kv_rows = out_0.flatten_outer_dims().rearrange("(p b) n -> p b n", b=NB)
    rope_rows = out_1.flatten_outer_dims().rearrange("(p b) f -> p (b f)", b=NB)
    w_rows = Wckv.rearrange("(g p j) n -> g p j n", p=P, j=PACK)
    byte_rows = Wdkv_bytes.rearrange("(p j) n -> p j n", j=PACK)

    with ExitStack() as ctx:
        keep = ctx.enter_context(tc.tile_pool(name="keep", bufs=1))
        work = ctx.enter_context(tc.tile_pool(name="work", bufs=4))
        outs = ctx.enter_context(tc.tile_pool(name="outs", bufs=1))
        psum = ctx.enter_context(tc.psum_pool(name="psum", bufs=1))
        ctx.enter_context(tc.manual_schedule())

        ident = keep.tile([P, P], F32, name="ident")
        ident_bf = keep.tile([P, P], BF16, name="ident_bf")
        gain4 = keep.tile([P, PACK], BF16, name="gain4")
        gain = keep.tile([P, LORA], BF16, name="gain")
        eps = keep.tile([P, 1], F32, name="eps")
        unread = keep.tile([P, 1], F32, name="unread")
        scale = keep.tile([P, PACK], F32, name="scale")
        cos_sin = keep.tile([P, PAIRS, 2], BF16, name="cos_sin", align_bytes=DMA_ALIGN)
        by_cos = keep.tile([P, PAIRS, 2], F32, name="by_cos")
        by_sin = keep.tile([P, 2, PAIRS], F32, name="by_sin")
        rotated = keep.tile([P, PAIRS, 2], F32, name="rotated", align_bytes=DMA_ALIGN)
        x_raw = [keep.tile([P, C], BF16, name="x_raw%d" % b, align_bytes=DMA_ALIGN) for b in range(NB)]
        w_raw = [keep.tile([P, PACK, WIDTH], BF16, name="w_raw%d" % g, align_bytes=DMA_ALIGN) for g in range(NP)]
        d_first = [keep.tile([P, 2, FIRST * P], U8, name="d_first%d" % j, align_bytes=DMA_ALIGN) for j in range(2)]
        d_next = keep.tile([P, PACK, (LATE - FIRST) * P], U8, name="d_next", align_bytes=DMA_ALIGN)
        d_late = keep.tile([P, PACK, KVW - LATE * P], U8, name="d_late", align_bytes=DMA_ALIGN)
        x_codes = [keep.tile([P, NP, P], U32, name="x_codes%d" % b, align_bytes=64) for b in range(NB)]
        x_scales = [keep.tile([P, NP, P], U8, name="x_scales%d" % b, align_bytes=64) for b in range(NB)]
        w_codes = [keep.tile([P, LORA], U32, name="w_codes%d" % g, align_bytes=64) for g in range(NP)]
        w_scales = [keep.tile([P, LORA], U8, name="w_scales%d" % g, align_bytes=64) for g in range(NP)]
        wr_grouped = keep.tile([P, NP, ROPE, PACK], BF16, name="wr_grouped", align_bytes=64)
        wr_codes = keep.tile([P, NP, ROPE], U32, name="wr_codes", align_bytes=64)
        wr_scales = keep.tile([P, NP, ROPE], U8, name="wr_scales", align_bytes=64)
        n_codes = [keep.tile([P, P], U32, name="n_codes%d" % b, align_bytes=64) for b in range(NB)]
        n_scales = [keep.tile([P, P], U8, name="n_scales%d" % b, align_bytes=64) for b in range(NB)]
        d_codes = keep.tile([P, KVW], U32, name="d_codes", align_bytes=64)
        d_scales = keep.tile([P, KVW], U8, name="d_scales", align_bytes=64)
        sumsq = [keep.tile([P, 1], F32, name="sumsq%d" % b) for b in range(NB)]
        rstd = [keep.tile([P, 1], F32, name="rstd%d" % b) for b in range(NB)]

        def load_x(b):
            nc.sync.dma_start(out=x_raw[b][:], in_=x_rows[:, b, :])

        def load_w(g):
            nc.sync.dma_start(out=w_raw[g][:], in_=w_rows[g])

        nc.scalar.dma_start(out=scale[:], in_=Wdkv_scale.rearrange("(p j) o -> p (j o)", j=PACK))
        nc.scalar.dma_start(out=gain4[:], in_=kv_norm_w.rearrange("(p j) -> p j", j=PACK))
        for j in range(2):
            nc.sync.dma_start(out=d_first[j][:], in_=byte_rows[:, 2 * j : 2 * j + 2, 0 : FIRST * P])
        nc.sync.dma_start(out=d_next[:], in_=byte_rows[:, :, FIRST * P : LATE * P])
        load_x(0)
        for g in range(NP):
            load_w(g)
        for b in range(1, NB):
            load_x(b)
        nc.sync.dma_start(out=d_late[:], in_=byte_rows[:, :, LATE * P : KVW])
        nc.sync.dma_start(out=cos_sin[:].rearrange("p i e -> p (i e)"), in_=freq_cis.rearrange("(p b) i e -> p (b i e)", b=NB))

        make_identity(nc, ident_bf[:])
        make_identity(nc, ident[:])
        nc.vector.memset(eps[:], EPS)
        nc.scalar.activation(unread[:], eps[:], ACT.Abs_reciprocal_sqrt)

        free_banks = list(range(BANKS))
        held = {}

        def take(key, place=0):
            i = free_banks[place]
            free_banks.remove(i)
            held[key] = (i, psum.tile([P, BANK], F32, name="bank%d" % i))
            return held[key][1]

        def bank(key):
            return held[key][1]

        def give(key):
            free_banks.append(held[key][0])

        staged = {}
        emptied = []

        def stage(pool, key, shape, dtype, **how):
            if key not in staged:
                staged[key] = pool.tile(shape, dtype, name=key[0], **how)
            return staged[key]

        def copy(eng, out, in_):
            if eng == V:
                nc.vector.tensor_copy(out, in_)
            else:
                nc.scalar.copy(out, in_)

        def interleave(eng, grouped, rows):
            copy(eng, grouped.rearrange("p (c i) t -> p c t i", i=RUN), rows.rearrange("p t (c i) -> p c t i", i=RUN))

        def quantize(codes, scales, grouped):
            nc.vector.quantize_mx(out=codes.bitcast(FP8X4), scales=scales, in_=grouped)

        def product(out, lhs_codes, lhs_scales, rhs_codes, rhs_scales, start, stop):
            nc.tensor.matmul_mx(
                out=out,
                lhsT=lhs_codes.bitcast(FP8X4),
                lhsT_scale=lhs_scales,
                rhs=rhs_codes.bitcast(FP8X4),
                rhs_scale=rhs_scales,
                start=start,
                stop=stop,
            )

        def warm_up():
            out = take("warm")[:].rearrange("p (a n) -> p a n", a=BANK // P)
            for repeat in range(WARM_UPS):
                nc.tensor.matmul(out, lhsT=ident_bf[:], rhs=ident_bf[:].unsqueeze(1).to_broadcast([P, BANK // P, P]), start=True, stop=True)
            give("warm")

        def x_turn(b, h):
            words = x_raw[b][:].bitcast(F32)
            out = take(("x", b, h))[:].rearrange("p (a r) -> p a r", a=4)
            for g in range(2):
                first = 2 * P * (2 * h + g)
                for u in range(2):
                    nc.tensor.transpose(out[:, 2 * g + u, :], words[:, first + u : first + 2 * P : 2], ident[:])

        def x_grouped(b):
            return stage(work, ("x_grouped", b), [P, NP, P, PACK], BF16, align_bytes=64)[:].rearrange("p g r t -> p (g r t)")

        def x_out(b, h):
            words = x_grouped(b).bitcast(F32)[:, BANK * h : BANK * (h + 1)]
            nc.scalar.copy(words.rearrange("p (g r u) -> p g r u", g=2, u=2), bank(("x", b, h))[:].rearrange("p (g u r) -> p g r u", g=2, u=2))
            give(("x", b, h))

        def x_quant(b):
            quantize(x_codes[b][:].rearrange("p g r -> p (g r)"), x_scales[b][:].rearrange("p g r -> p (g r)"), x_grouped(b))

        def w_grouped(g):
            return stage(work, ("w_grouped", g), [P, LORA, PACK], BF16, align_bytes=64)

        def w_inter(g, eng, lo, hi):
            grouped = w_grouped(g)[:].rearrange("p (u c e) t -> p c t u e", u=2, e=2)
            rows = w_raw[g][:, :, 0:LORA].rearrange("p t (c u e) -> p c t u e", u=2, e=2)
            copy(eng, grouped[:, lo // PACK : hi // PACK], rows[:, lo // PACK : hi // PACK])

        def w_shared(g):
            w_inter(g, V, 0, W_SPLIT[g])
            w_inter(g, S, W_SPLIT[g], LORA)

        def w_quant(g):
            quantize(w_codes[g][:], w_scales[g][:], w_grouped(g)[:].rearrange("p w t -> p (w t)"))

        def lat_passes(b, passes):
            for g in passes:
                if g == 0:
                    take(("lat", b))
                product(bank(("lat", b))[:], x_codes[b][:, g, :], x_scales[b][:, g, :], w_codes[g][:], w_scales[g][:], g == 0, g == NP - 1)

        def gain_spread():
            words = gain4[:].bitcast(F32)
            out = take("gain")
            for u in range(2):
                nc.tensor.transpose(out[:, P * u : P * (u + 1)], words[:, u : u + 1].to_broadcast([P, P]), ident[:])

        def gain_out():
            nc.scalar.copy(gain[:].bitcast(F32), bank("gain")[:, 0 : 2 * P])
            give("gain")

        def sum_squares(b):
            squares = work.tile([P, LORA], BF16, name="squares", bufs=1)
            nc.scalar.activation(squares[:], bank(("lat", b))[:], ACT.Square, accum_out=sumsq[b][:])

        def root(b):
            nc.scalar.activation(rstd[b][:], sumsq[b][:], ACT.Abs_reciprocal_sqrt, bias=eps[:], scale=1.0 / LORA)

        def n_rows(b):
            return stage(work, ("n_rows", b), [P, LORA], BF16)[:]

        def norm(b):
            nc.vector.scalar_tensor_tensor(n_rows(b), bank(("lat", b))[:], rstd[b][:], gain[:], ALU.mult, ALU.mult)
            give(("lat", b))

        def n_turn(b):
            words = n_rows(b).bitcast(F32)
            out = take(("n", b))
            for u in range(2):
                nc.tensor.transpose(out[:, P * u : P * (u + 1)], words[:, P * u : P * (u + 1)], ident[:])

        def n_grouped(b):
            return stage(work, ("n_grouped", b), [P, P, PACK], BF16, align_bytes=64)[:].rearrange("p r t -> p (r t)")

        def n_out(b, eng):
            copy(eng, n_grouped(b).bitcast(F32).rearrange("p (r u) -> p r u", u=2), bank(("n", b))[:, 0 : 2 * P].rearrange("p (u r) -> p r u", u=2))
            give(("n", b))

        def n_quant(b):
            quantize(n_codes[b][:], n_scales[b][:], n_grouped(b))

        def group(s):
            return [g for g in GROUPS if g[0] <= s < g[0] + g[1]][0]

        def d_raw(s, n, t):
            if s < FIRST:
                return d_first[t // 2][:, t % 2, P * s : P * (s + n)]
            if s < LATE:
                return d_next[:, t, P * (s - FIRST) : P * (s - FIRST + n)]
            return d_late[:, t, P * (s - LATE) : P * (s - LATE + n)]

        def d_wide(s, n):
            first, count = group(s)
            rows = stage(work, ("d_wide", first), [P, PACK, P * count], BF16, bufs=2)
            return rows[:, :, P * (s - first) : P * (s - first + n)]

        def d_grouped(s, n):
            first, count = group(s)
            grouped = stage(work, ("d_grouped", first), [P, P * count, PACK], BF16, bufs=2, align_bytes=64)
            return grouped[:, P * (s - first) : P * (s - first + n), :]

        def widen(s, n, t, eng=V):
            wide = d_wide(s, n)[:, t, :]
            raw = d_raw(s, n, t).bitcast(FP8)
            if eng == V:
                nc.vector.tensor_scalar(wide, raw, scale[:, t : t + 1], None, ALU.mult)
            else:
                nc.scalar.activation(wide, raw, ACT.Copy, scale=scale[:, t : t + 1])

        def d_inter(s, n):
            interleave(V, d_grouped(s, n), d_wide(s, n))

        def by_identity(out, rows):
            nc.tensor.matmul(out.rearrange("p (n t) -> p t n", t=PACK), lhsT=ident_bf[:], rhs=rows, start=True, stop=True)

        def d_identity(s):
            out = take(("d", s))[:].bitcast(BF16)
            for q in range(2):
                by_identity(out[:, BANK * q : BANK * (q + 1)], d_wide(s + q, 1))

        def d_identity_out(s):
            nc.scalar.copy(d_grouped(s, 2).rearrange("p w t -> p (w t)").bitcast(F32), bank(("d", s))[:])
            give(("d", s))

        def d_quant(s, n):
            cols = slice(P * s, P * (s + n))
            quantize(d_codes[:, cols], d_scales[:, cols], d_grouped(s, n).rearrange("p w t -> p (w t)"))

        def strips(s):
            first, count = group(s)
            return min(BANK // P, first + count - s)

        def kv_product(b, s, place=0):
            out = take(("kv", b, s), place)
            done = 0
            for n in (4, 2, 1):
                if strips(s) - done >= n:
                    cols = slice(P * (s + done), P * (s + done + n))
                    product(out[:, P * done : P * (done + n)], n_codes[b][:], n_scales[b][:], d_codes[:, cols], d_scales[:, cols], True, True)
                    done = done + n

        def kv_out(b, s, eng=S):
            first, count = group(s)
            if (first, count) == GROUPS[-1] and b >= 2:
                b0, nb = 2, 2
                rows = stage(outs, ("kv_last",), [P, nb, P * count], F32, bufs=1, align_bytes=DMA_ALIGN)
            else:
                b0, nb = b, 1
                rows = stage(outs, ("kv_rows", b, first), [P, nb, P * count], F32, bufs=STORE_BUFS, align_bytes=DMA_ALIGN)
            copy(eng, rows[:, b - b0, P * (s - first) : P * (s - first + strips(s))], bank(("kv", b, s))[:, 0 : P * strips(s)])
            give(("kv", b, s))
            emptied.append((b0, first))
            if emptied.count((b0, first)) == nb * ((count + 3) // 4):
                nc.sync.dma_start(out=kv_rows[:, b0 : b0 + nb, P * first : P * (first + count)], in_=rows[:])

        def kv(b, s, place=0):
            kv_product(b, s, place)
            kv_out(b, s)

        def wr_inter(g, eng):
            interleave(eng, wr_grouped[:, g, :, :], w_raw[g][:, :, LORA:WIDTH])

        def wr_quant(g):
            two = slice(g, g + 2)
            quantize(wr_codes[:, two, :].rearrange("p g w -> p (g w)"), wr_scales[:, two, :].rearrange("p g w -> p (g w)"), wr_grouped[:, two, :, :].rearrange("p g w t -> p (g w t)"))

        def kr_products(g):
            if g == 0:
                take("kr")
            out = bank("kr")
            for b in range(NB):
                product(out[:, ROPE * b : ROPE * (b + 1)], x_codes[b][:, g, :], x_scales[b][:, g, :], wr_codes[:, g, :], wr_scales[:, g, :], g == 0 and b == 0, g == NP - 1 and b == NB - 1)

        def times_cos():
            kr = bank("kr")[:].rearrange("p (i e) -> p i e", e=2)
            nc.vector.tensor_tensor(by_cos[:], kr, cos_sin[:, :, 0:1].to_broadcast([P, PAIRS, 2]), ALU.mult)

        def times_sin():
            kr = bank("kr")[:].rearrange("p (i e) -> p i e", e=2)
            nc.vector.scalar_tensor_tensor(by_sin[:, 0, :].unsqueeze(2), kr[:, :, 1:2], -1.0, cos_sin[:, :, 1:2], ALU.mult, ALU.mult)
            nc.vector.tensor_tensor(by_sin[:, 1, :].unsqueeze(2), kr[:, :, 0:1], cos_sin[:, :, 1:2], ALU.mult)
            give("kr")

        def rotate_sum():
            nc.vector.tensor_tensor(rotated[:], by_cos[:], by_sin[:].rearrange("p e i -> p i e"), ALU.add)
            nc.sync.dma_start(out=rope_rows, in_=rotated[:].rearrange("p i e -> p (i e)"))


        warm_up()
        gain_spread()
        widen(0, 8, 0)
        widen(0, 8, 1, S)
        widen(0, 4, 2)
        widen(0, 4, 3)
        widen(4, 4, 2)
        widen(4, 4, 3)
        gain_out()
        widen(8, 8, 0)
        widen(8, 8, 1, S)
        widen(12, 4, 2)
        widen(8, 4, 2, S)
        widen(12, 4, 3)
        widen(8, 4, 3)

        d_identity(0)
        d_identity(2)
        x_turn(0, 0)
        x_turn(0, 1)
        d_identity(4)
        d_identity(6)
        d_identity_out(0)
        d_identity_out(2)
        x_out(0, 0)
        x_out(0, 1)
        w_inter(0, S, W_SPLIT[0], LORA)
        d_identity(8)
        d_identity(10)
        d_inter(12, 4)
        w_inter(0, V, 0, W_SPLIT[0])
        w_shared(1)
        d_identity_out(4)
        x_quant(0)
        w_quant(0)
        w_shared(2)
        w_quant(1)
        w_shared(3)
        w_quant(2)
        w_quant(3)

        lat_passes(0, (0, 1))
        d_identity_out(6)
        d_identity_out(8)
        x_turn(1, 0)
        x_turn(1, 1)
        lat_passes(0, (2, 3))
        x_out(1, 0)
        x_out(1, 1)
        x_turn(2, 0)
        x_turn(2, 1)
        sum_squares(0)
        d_identity_out(10)
        root(0)
        x_out(2, 0)
        x_out(2, 1)
        d_quant(0, 8)
        x_quant(1)
        x_turn(3, 0)
        lat_passes(1, range(NP))
        d_quant(12, 4)
        norm(0)
        n_turn(0)
        x_turn(3, 1)
        d_quant(8, 4)
        x_quant(2)
        x_out(3, 0)
        sum_squares(1)
        n_out(0, S)
        root(1)
        x_out(3, 1)
        widen(16, 8, 0)
        n_quant(0)

        lat_passes(2, range(NP))
        kv_product(0, 0)
        kv_product(0, 4)
        norm(1)
        n_turn(1)
        kv_product(0, 8)
        kv_product(0, 12)
        x_quant(3)
        widen(16, 4, 3, S)
        widen(16, 8, 1)
        sum_squares(2)
        kv_out(0, 0)
        root(2)
        kv_out(0, 4, V)
        lat_passes(3, range(NP))
        n_out(1, S)
        kv_out(0, 8)
        kv_out(0, 12)
        widen(16, 4, 2)
        n_quant(1)
        norm(2)
        kv_product(1, 0)
        kv_product(1, 4)
        n_turn(2)
        kv_product(1, 8)
        kv_product(1, 12)
        d_inter(16, 2)
        widen(20, 4, 2)
        sum_squares(3)
        kv_out(1, 0)
        root(3)
        kv_out(1, 4)
        kv_out(1, 8)
        kv_out(1, 12)
        n_out(2, V)
        widen(20, 4, 3)
        n_quant(2)
        norm(3)
        kv_product(2, 0)
        kv_product(2, 4)
        n_turn(3)
        kv_product(2, 8)
        kv_product(2, 12)
        for s in range(0, LATE, 4):
            kv_out(2, s)
        d_inter(18, 2)
        widen(28, 4, 0)
        n_out(3, V)
        widen(24, 4, 0)
        n_quant(3)
        for s in range(0, LATE, 4):
            kv(3, s)

        d_inter(20, 4)
        d_quant(16, 4)
        d_quant(20, 4)
        widen(24, 8, 1)
        widen(24, 8, 2)
        widen(24, 4, 3)
        widen(28, 4, 3)
        d_inter(24, 4)
        d_inter(28, 2)
        d_quant(24, 4)
        d_inter(30, 2)
        d_quant(28, 2)
        d_quant(30, 2)
        for b in range(NB):
            kv(b, 16, PACED_BANK)
            kv(b, 20, PACED_BANK)

        for b in range(NB):
            kv_product(b, 24)
        kv_out(0, 24)
        for g in range(NP):
            wr_inter(g, V)
        wr_quant(0)
        wr_quant(2)
        for b in range(NB):
            kv_product(b, 28)
        kv_out(0, 28)
        for g in range(NP):
            kr_products(g)
        for b in range(1, NB):
            kv_out(b, 24, V if b == 2 else S)
            kv_out(b, 28, V if b == 2 else S)
        times_cos()
        times_sin()
        rotate_sum()
